import numpy as np
import ml_dtypes


def mxq(x, axis, fmt="e4m3"):
    dtype, down = {"e4m3": (ml_dtypes.float8_e4m3fn, 7), "e5m2": (ml_dtypes.float8_e5m2, 14)}[fmt]
    v = np.moveaxis(np.asarray(x, np.float32).astype(ml_dtypes.bfloat16).astype(np.float64), axis, -1)
    blocks = v.reshape(v.shape[:-1] + (-1, 32))
    amax = np.abs(blocks).max(-1, keepdims=True)
    byte = np.maximum(np.where(amax > 0, np.frexp(amax)[1] - 1 + 127, 0) - down, 1)
    scale = np.exp2(byte - 127.0)
    codes = (blocks / scale).astype(np.float32).astype(dtype).astype(np.float64)
    return np.moveaxis((codes * scale).reshape(v.shape), -1, axis)


WIDE = False


def mx_kscale(k):
    if not WIDE:
        return np.ones(k)
    levels = np.array([10, -10, 5, -5, 0])
    a = np.random.permutation(np.resize(levels, k // 512 * 4)).reshape(k // 512, 4)
    idx = np.arange(k)
    return np.exp2(a[idx // 512, idx % 128 // 32])


BF16 = ml_dtypes.bfloat16


def bf(x):
    return np.asarray(x, np.float32).astype(BF16)


def f64(x):
    return np.asarray(x).astype(np.float64)


B, C, M, O, H, W = 4, 1024, 512, 128, 64, 64
H2, W2 = H // 2, W // 2
KS = 3
PAD = KS // 2
BN_EPS = 1e-5


def haar_ll(x):
    a = x[:, :, 0::2, 0::2]
    b = x[:, :, 0::2, 1::2]
    c = x[:, :, 1::2, 0::2]
    d = x[:, :, 1::2, 1::2]
    return (a + b + c + d) * 0.5


def windows(u):
    up = np.pad(u, ((0, 0), (0, 0), (PAD, PAD), (PAD, PAD)))
    return np.stack([up[:, :, i:i + H2, j:j + W2] for i in range(KS) for j in range(KS)], axis=-1)


def setup_inputs():
    s, t = mx_kscale(C), mx_kscale(M)
    return {
        "x": bf(np.random.standard_normal((B, C, H, W)) * s[None, :, None, None]),
        "w_c1": bf(np.random.standard_normal((M, C)) / np.sqrt(C) * t[:, None] / s[None, :]),
        "b_c1": bf(np.random.standard_normal(M) * 0.3 * t),
        "w_q": bf(np.random.standard_normal((O, M)) / np.sqrt(M) / t[None, :]),
        "w_k": bf(np.random.standard_normal((O, M)) / np.sqrt(M) / t[None, :]),
        "w_v": bf(np.random.standard_normal((O, M)) / np.sqrt(M) / t[None, :]),
        "bn_gamma": bf(1.0 + 0.1 * np.random.standard_normal(O)),
        "bn_beta": bf(0.3 * np.random.standard_normal(O)),
        "prelu_a": bf(np.random.uniform(0.15, 0.35, (1,))),
    }


def reference(x, w_c1, b_c1, w_q, w_k, w_v, bn_gamma, bn_beta, prelu_a):
    ll = haar_ll(f64(x)).reshape(B, C, H2 * W2)
    y = (mxq(f64(w_c1), 1, "e4m3") @ mxq(ll, 1, "e4m3")) + f64(b_c1)[None, :, None]
    yq = mxq(y, 1, "e4m3")
    q = (mxq(f64(w_q), 1, "e4m3") @ yq).reshape(B, O, H2, W2)
    k = (mxq(f64(w_k), 1, "e4m3") @ yq).reshape(B, O, H2, W2)
    v = (mxq(f64(w_v), 1, "e4m3") @ yq).reshape(B, O, H2, W2)
    kw = windows(k)
    vw = windows(v)
    z = q[..., None] * kw
    e = np.exp(z - z.max(-1, keepdims=True))
    attn = e / e.sum(-1, keepdims=True)
    att = (attn * vw).sum(-1)
    m = att.mean(axis=(0, 2, 3), keepdims=True)
    var = att.var(axis=(0, 2, 3), keepdims=True)
    n = f64(bn_gamma)[None, :, None, None] * (att - m) / np.sqrt(var + BN_EPS) + f64(bn_beta)[None, :, None, None]
    return np.where(n >= 0, n, f64(prelu_a) * n)

@@ -1,0 +1,396 @@
+from contextlib import ExitStack
+
+import concourse.mybir as mybir
+from concourse.masks import make_identity
+
+F32 = mybir.dt.float32
+BF16 = mybir.dt.bfloat16
+U32 = mybir.dt.uint32
+U8 = mybir.dt.uint8
+FP8X4 = mybir.dt.float8_e4m3fn_x4
+ALU = mybir.AluOpType
+ACT = mybir.ActivationFunctionType
+
+B, C, M, O, H, W = 4, 1024, 512, 128, 64, 64
+H2, W2 = H // 2, W // 2
+BN_EPS = 1e-5
+
+P = 128
+PACK = 4
+K_PASS = P * PACK
+C_PASSES = C // K_PASS
+M_TILES = M // P
+HALF = 512
+HALF_ROWS = HALF // W2
+N_HALVES = B * H2 * W2 // HALF
+PIECE_ROWS = 8
+PIECE = PIECE_ROWS * W2
+BLOCKS = HALF // P
+BLOCK_ROWS = P // W2
+OFFSETS = [(di, dj) for di in range(3) for dj in range(3)]
+N_OFF = len(OFFSETS)
+
+FLOPS = 2 * B * H2 * W2 * (M * C + 3 * O * M)
+
+
+def add_transposed(nc, out, in_, identity, start, stop):
+    nc.tensor.matmul(out=out, lhsT=in_, rhs=identity, is_transpose=True, start=start, stop=stop)
+
+
+def tile_merge_pa_t_kernel(
+    tc, x, w_c1, b_c1, w_q, w_k, w_v, bn_gamma, bn_beta, prelu_a, out
+):
+    nc = tc.nc
+    with ExitStack() as whole:
+        keep = whole.enter_context(tc.tile_pool(name="keep", bufs=1))
+
+        ident_f32 = keep.tile([P, P], F32)
+        make_identity(nc, ident_f32[:])
+        ident_bf16 = keep.tile([P, P], BF16)
+        make_identity(nc, ident_bf16[:])
+
+        w1_codes = keep.tile([P, C_PASSES, M], U32, align_bytes=64)
+        w1_scales = keep.tile([P, C_PASSES, M], U8, align_bytes=64)
+        wqkv_codes = keep.tile([P, 3, O], U32, align_bytes=64)
+        wqkv_scales = keep.tile([P, 3, O], U8, align_bytes=64)
+        bias = keep.tile([P, M_TILES], F32)
+
+        q_all = keep.tile([P, B, H2 * W2], F32)
+        k_ring = keep.tile([P, B, H2 + 2, W2 + 2], F32)
+        v_moved = keep.tile([P, B, 3, H2 + 2, W2], F32)
+        nc.gpsimd.memset(k_ring[:], 0.0)
+        nc.gpsimd.memset(v_moved[:, :, :, 0, :], 0.0)
+        nc.gpsimd.memset(v_moved[:, :, :, H2 + 1, :], 0.0)
+        nc.gpsimd.memset(v_moved[:, :, 0, :, 0:8], 0.0)
+        nc.gpsimd.memset(v_moved[:, :, 2, :, W2 - 8 : W2], 0.0)
+
+        bias_bf16 = keep.tile([P, M_TILES], BF16)
+        nc.scalar.dma_start(out=bias_bf16[:], in_=b_c1.rearrange("(n t) -> n t", t=M_TILES))
+        gamma_bf16 = keep.tile([P, 1], BF16)
+        nc.scalar.dma_start(out=gamma_bf16[:], in_=bn_gamma.rearrange("(o one) -> o one", one=1))
+        beta_bf16 = keep.tile([P, 1], BF16)
+        nc.scalar.dma_start(out=beta_bf16[:], in_=bn_beta.rearrange("(o one) -> o one", one=1))
+        slope_bf16 = keep.tile([P, 1], BF16)
+        nc.scalar.dma_start(out=slope_bf16[:], in_=prelu_a.partition_broadcast(P))
+        gamma = keep.tile([P, 1], F32)
+        beta = keep.tile([P, 1], F32)
+        slope = keep.tile([P, 1], F32)
+        one_minus_slope = keep.tile([P, 1], F32)
+
+        with ExitStack() as front:
+            stage = front.enter_context(tc.tile_pool(name="stage", bufs=1))
+            x_pool = front.enter_context(tc.tile_pool(name="x_pool", bufs=4))
+            work = front.enter_context(tc.tile_pool(name="work", bufs=2))
+            turned_psum = front.enter_context(tc.psum_pool(name="turned_psum", bufs=2))
+            mx_psum = front.enter_context(tc.psum_pool(name="mx_psum", bufs=3))
+
+            def load_piece(half, g, s):
+                b, h = divmod(half, 2)
+                row = 2 * (h * HALF_ROWS + s * PIECE_ROWS)
+                x_piece = x_pool.tile([P, PACK, 2 * PIECE_ROWS * W], BF16)
+                nc.sync.dma_start(
+                    out=x_piece[:],
+                    in_=x[
+                        b, g * K_PASS : (g + 1) * K_PASS, row : row + 2 * PIECE_ROWS, :
+                    ].rearrange("(p j) r w -> p j (r w)", j=PACK),
+                )
+                return x_piece
+
+            w1_rows = stage.tile([P, M_TILES, C], BF16)
+            nc.scalar.dma_start(out=w1_rows[:], in_=w_c1.rearrange("(n t) c -> n t c", t=M_TILES))
+            wqkv_rows = stage.tile([P, 3, M], BF16)
+            for s, w_s in enumerate((w_q, w_k, w_v)):
+                nc.scalar.dma_start(out=wqkv_rows[:, s, :], in_=w_s)
+
+            nc.vector.tensor_copy(out=bias[:], in_=bias_bf16[:])
+            nc.vector.tensor_copy(out=gamma[:], in_=gamma_bf16[:])
+            nc.vector.tensor_copy(out=beta[:], in_=beta_bf16[:])
+            nc.vector.tensor_copy(out=slope[:], in_=slope_bf16[:])
+            nc.vector.tensor_scalar(
+                out=one_minus_slope[:], in0=slope[:], scalar1=-1.0, scalar2=1.0,
+                op0=ALU.mult, op1=ALU.add,
+            )
+
+            w1_sorted = stage.tile([P, M_TILES, C_PASSES, PACK, P], BF16)
+            w1_grouped = stage.tile([P, C_PASSES, M_TILES, P, PACK], BF16, align_bytes=64)
+            for t in range(M_TILES):
+                nc.scalar.copy(
+                    out=w1_sorted[:, t],
+                    in_=w1_rows[:, t, :].rearrange("n (g p j) -> n g j p", g=C_PASSES, j=PACK),
+                )
+                for g in range(C_PASSES):
+                    turned = turned_psum.tile([P, PACK, P], BF16)
+                    for j in range(PACK):
+                        nc.tensor.transpose(turned[:, j, :], w1_sorted[:, t, g, j, :], ident_bf16[:])
+                    nc.scalar.copy(
+                        out=w1_grouped[:, g, t], in_=turned[:].rearrange("p j n -> p n j")
+                    )
+            wqkv_sorted = stage.tile([P, 3, PACK, P], BF16)
+            wqkv_grouped = stage.tile([P, 3, O, PACK], BF16, align_bytes=64)
+            nc.scalar.copy(
+                out=wqkv_sorted[:], in_=wqkv_rows[:].rearrange("o s (p j) -> o s j p", j=PACK)
+            )
+            for s in range(3):
+                turned = turned_psum.tile([P, PACK, P], BF16)
+                for j in range(PACK):
+                    nc.tensor.transpose(turned[:, j, :], wqkv_sorted[:, s, j, :], ident_bf16[:])
+                nc.scalar.copy(out=wqkv_grouped[:, s], in_=turned[:].rearrange("p j o -> p o j"))
+
+            def quantise_weights():
+                for g in range(C_PASSES):
+                    nc.vector.quantize_mx(
+                        out=w1_codes[:, g, :].bitcast(FP8X4),
+                        scales=w1_scales[:, g, :],
+                        in_=w1_grouped[:, g].rearrange("p t n j -> p (t n j)"),
+                    )
+                for s in range(3):
+                    nc.vector.quantize_mx(
+                        out=wqkv_codes[:, s, :].bitcast(FP8X4),
+                        scales=wqkv_scales[:, s, :],
+                        in_=wqkv_grouped[:, s].rearrange("p o j -> p (o j)"),
+                    )
+
+            def haar(half):
+                ll_grouped = work.tile([P, C_PASSES, HALF, PACK], BF16, align_bytes=64)
+                for g in range(C_PASSES):
+                    for s in range(HALF_ROWS // PIECE_ROWS):
+                        x_piece = load_piece(half, g, s)
+                        rows = x_piece[:].rearrange("p j (r two w) -> p (j r) two w", two=2, w=W)
+                        row_sum = work.tile([P, PACK * PIECE_ROWS, W], F32)
+                        nc.vector.tensor_tensor(
+                            out=row_sum[:], in0=rows[:, :, 0, :], in1=rows[:, :, 1, :], op=ALU.add
+                        )
+                        pairs = row_sum[:].rearrange(
+                            "p (j r) (w two) -> p j (r w) two", j=PACK, two=2
+                        )
+                        nc.vector.tensor_tensor(
+                            out=ll_grouped[:, g, s * PIECE : (s + 1) * PIECE, :],
+                            in0=pairs[:, :, :, 0].rearrange("p j x -> p x j"),
+                            in1=pairs[:, :, :, 1].rearrange("p j x -> p x j"),
+                            op=ALU.add,
+                        )
+                return ll_grouped
+
+            def first_convolution(ll_grouped):
+                ll_codes = work.tile([P, C_PASSES, HALF], U32, align_bytes=64)
+                ll_scales = work.tile([P, C_PASSES, HALF], U8, align_bytes=64)
+                nc.vector.quantize_mx(
+                    out=ll_codes[:].rearrange("p g x -> p (g x)").bitcast(FP8X4),
+                    scales=ll_scales[:].rearrange("p g x -> p (g x)"),
+                    in_=ll_grouped[:].rearrange("p g x j -> p (g x j)"),
+                )
+                y_grouped = work.tile([P, HALF, PACK], BF16, align_bytes=64)
+                for t in range(M_TILES):
+                    cols = slice(t * P, (t + 1) * P)
+                    y_acc = mx_psum.tile([P, HALF], F32)
+                    for g in range(C_PASSES):
+                        nc.tensor.matmul_mx(
+                            out=y_acc[:],
+                            lhsT=w1_codes[:, g, cols].bitcast(FP8X4),
+                            lhsT_scale=w1_scales[:, g, cols],
+                            rhs=ll_codes[:, g, :].bitcast(FP8X4),
+                            rhs_scale=ll_scales[:, g, :],
+                            start=(g == 0),
+                            stop=(g == C_PASSES - 1),
+                        )
+                    nc.scalar.activation(
+                        out=y_grouped[:, :, t], in_=y_acc[:], func=ACT.Identity,
+                        bias=bias[:, t : t + 1], scale=0.5,
+                    )
+                return y_grouped
+
+            def project(half, y_grouped):
+                b, h = divmod(half, 2)
+                top = 1 + h * HALF_ROWS
+                y_codes = work.tile([P, HALF], U32, align_bytes=64)
+                y_scales = work.tile([P, HALF], U8, align_bytes=64)
+                nc.vector.quantize_mx(
+                    out=y_codes[:].bitcast(FP8X4),
+                    scales=y_scales[:],
+                    in_=y_grouped[:].rearrange("p x t -> p (x t)"),
+                )
+                qkv = []
+                for s in range(3):
+                    proj = mx_psum.tile([P, HALF_ROWS, W2], F32)
+                    nc.tensor.matmul_mx(
+                        out=proj[:].rearrange("p r w -> p (r w)"),
+                        lhsT=wqkv_codes[:, s, :].bitcast(FP8X4),
+                        lhsT_scale=wqkv_scales[:, s, :],
+                        rhs=y_codes[:].bitcast(FP8X4),
+                        rhs_scale=y_scales[:],
+                        start=True,
+                        stop=True,
+                    )
+                    qkv.append(proj)
+                q_acc, k_acc, v_acc = qkv
+                rows = slice(top, top + HALF_ROWS)
+                nc.scalar.copy(
+                    out=q_all[:, b, h * HALF : (h + 1) * HALF],
+                    in_=q_acc[:].rearrange("p r w -> p (r w)"),
+                )
+                nc.scalar.copy(out=k_ring[:, b, rows, 1 : W2 + 1], in_=k_acc[:])
+                nc.scalar.copy(out=v_moved[:, b, 0, rows, 1:W2], in_=v_acc[:, :, 0 : W2 - 1])
+                nc.scalar.copy(out=v_moved[:, b, 1, rows, :], in_=v_acc[:])
+                nc.scalar.copy(out=v_moved[:, b, 2, rows, 0 : W2 - 1], in_=v_acc[:, :, 1:W2])
+
+            y_waiting = None
+            for half in range(N_HALVES + 1):
+                if half < N_HALVES:
+                    ll_grouped = haar(half)
+                if half == 0:
+                    quantise_weights()
+                if half >= 1:
+                    project(half - 1, y_waiting)
+                if half < N_HALVES:
+                    y_waiting = first_convolution(ll_grouped)
+
+        with ExitStack() as back:
+            z_pool = back.enter_context(tc.tile_pool(name="z_pool", bufs=2, reuse_waits="tile"))
+            tree = back.enter_context(tc.tile_pool(name="tree", bufs=1, reuse_waits="tile"))
+            e_pool = back.enter_context(tc.tile_pool(name="e_pool", bufs=N_OFF + 1, reuse_waits="tile"))
+            prod_pool = back.enter_context(tc.tile_pool(name="prod_pool", bufs=3, reuse_waits="tile"))
+            pair = back.enter_context(tc.tile_pool(name="pair", bufs=2, reuse_waits="tile"))
+            result = back.enter_context(tc.tile_pool(name="result", bufs=1, reuse_waits="tile"))
+            back_psum = back.enter_context(tc.psum_pool(name="back_psum", bufs=2, reuse_waits="tile"))
+
+            att = result.tile([P, N_HALVES, HALF], F32)
+            stats = result.tile([P, N_HALVES, 6], F32)
+
+            def scores(half):
+                b, h = divmod(half, 2)
+                top = h * HALF_ROWS
+                q_half = q_all[:, b, h * HALF : (h + 1) * HALF].rearrange("p (r w) -> p r w", w=W2)
+                z = z_pool.tile([P, N_OFF, HALF], F32)
+                for d, (di, dj) in enumerate(OFFSETS):
+                    nc.vector.tensor_tensor(
+                        out=z[:, d, :].rearrange("p (r w) -> p r w", w=W2),
+                        in0=q_half,
+                        in1=k_ring[:, b, top + di : top + di + HALF_ROWS, dj : dj + W2],
+                        op=ALU.mult,
+                    )
+                max4 = tree.tile([P, 4, HALF], F32)
+                nc.vector.tensor_tensor(out=max4[:], in0=z[:, 0:4, :], in1=z[:, 4:8, :], op=ALU.max)
+                max2 = tree.tile([P, 2, HALF], F32)
+                nc.vector.tensor_tensor(
+                    out=max2[:], in0=max4[:, 0:2, :], in1=max4[:, 2:4, :], op=ALU.max
+                )
+                max1 = tree.tile([P, HALF], F32)
+                nc.vector.tensor_tensor(
+                    out=max1[:], in0=max2[:, 0, :], in1=max2[:, 1, :], op=ALU.max
+                )
+                z_max = tree.tile([P, HALF], F32)
+                nc.vector.tensor_tensor(out=z_max[:], in0=max1[:], in1=z[:, 8, :], op=ALU.max)
+                neg_max = pair.tile([P, HALF], F32)
+                nc.scalar.mul(out=neg_max[:], in_=z_max[:], mul=-1.0)
+                return z, neg_max
+
+            def weights(z, neg_max):
+                e_tiles = []
+                e_sum = back_psum.tile([P, HALF], F32)
+                for d in range(N_OFF + 1):
+                    if d < N_OFF:
+                        shifted = back_psum.tile([P, BLOCKS, P], F32)
+                        for blk in range(BLOCKS):
+                            cols = slice(blk * P, (blk + 1) * P)
+                            add_transposed(
+                                nc, shifted[:, blk, :], z[:, d, cols], ident_f32[:], True, False
+                            )
+                            add_transposed(
+                                nc, shifted[:, blk, :], neg_max[:, cols], ident_f32[:], False, True
+                            )
+                        e_t = e_pool.tile([P, BLOCKS, P], F32)
+                        nc.scalar.activation(out=e_t[:], in_=shifted[:], func=ACT.Exp)
+                        e_tiles.append(e_t)
+                    if d >= 1:
+                        for blk in range(BLOCKS):
+                            add_transposed(
+                                nc, e_sum[:, blk * P : (blk + 1) * P], e_tiles[d - 1][:, blk, :],
+                                ident_f32[:],
+                                d - 1 == 0 and blk == 0,
+                                d - 1 == N_OFF - 1 and blk == BLOCKS - 1,
+                            )
+                log_sum = pair.tile([P, HALF], F32)
+                nc.scalar.activation(out=log_sum[:], in_=e_sum[:], func=ACT.Ln)
+                inv_sum = pair.tile([P, HALF], F32)
+                nc.scalar.activation(out=inv_sum[:], in_=log_sum[:], func=ACT.Exp, scale=-1.0)
+                return e_tiles, inv_sum
+
+            def mix(half, e_tiles, inv_sum):
+                b, h = divmod(half, 2)
+                top = h * HALF_ROWS
+                ev_sum = back_psum.tile([P, HALF], F32)
+                prods = []
+                for d in range(N_OFF + 1):
+                    if d < N_OFF:
+                        di, dj = OFFSETS[d]
+                        v_t = back_psum.tile([P, BLOCKS, P], F32)
+                        for blk in range(BLOCKS):
+                            row = top + blk * BLOCK_ROWS + di
+                            nc.tensor.transpose(
+                                v_t[:, blk, :],
+                                v_moved[:, b, dj, row : row + BLOCK_ROWS, :].rearrange(
+                                    "p r w -> p (r w)"
+                                ),
+                                ident_f32[:],
+                            )
+                        prod = prod_pool.tile([P, BLOCKS, P], F32)
+                        nc.vector.tensor_tensor(
+                            out=prod[:], in0=e_tiles[d][:], in1=v_t[:], op=ALU.mult
+                        )
+                        prods.append(prod)
+                    if d >= 1:
+                        for blk in range(BLOCKS):
+                            add_transposed(
+                                nc, ev_sum[:, blk * P : (blk + 1) * P], prods[d - 1][:, blk, :],
+                                ident_f32[:],
+                                d - 1 == 0 and blk == 0,
+                                d - 1 == N_OFF - 1 and blk == BLOCKS - 1,
+                            )
+                nc.vector.tensor_tensor(
+                    out=att[:, half, :], in0=ev_sum[:], in1=inv_sum[:], op=ALU.mult
+                )
+                nc.vector.bn_stats(out=stats[:, half, :], in_=att[:, half, :])
+
+            ready = weights(*scores(0))
+            for half in range(N_HALVES):
+                if half + 1 < N_HALVES:
+                    scored = scores(half + 1)
+                mix(half, *ready)
+                if half + 1 < N_HALVES:
+                    ready = weights(*scored)
+
+            mean_var = result.tile([P, 2], F32)
+            nc.vector.bn_aggr(out=mean_var[:], in_=stats[:].rearrange("p t s -> p (t s)"))
+            var_eps = result.tile([P, 1], F32)
+            nc.vector.tensor_scalar_add(out=var_eps[:], in0=mean_var[:, 1:2], scalar1=BN_EPS)
+            std = result.tile([P, 1], F32)
+            nc.scalar.sqrt(out=std[:], in_=var_eps[:])
+            inv_std = result.tile([P, 1], F32)
+            nc.vector.reciprocal(out=inv_std[:], in_=std[:])
+            gain = result.tile([P, 1], F32)
+            nc.vector.tensor_mul(out=gain[:], in0=gamma[:], in1=inv_std[:])
+            mean_gain = result.tile([P, 1], F32)
+            nc.vector.tensor_mul(out=mean_gain[:], in0=mean_var[:, 0:1], in1=gain[:])
+            shift = result.tile([P, 1], F32)
+            nc.vector.tensor_sub(out=shift[:], in0=beta[:], in1=mean_gain[:])
+            slope_gain = result.tile([P, 1], F32)
+            nc.vector.tensor_mul(out=slope_gain[:], in0=slope[:], in1=gain[:])
+            slope_shift = result.tile([P, 1], F32)
+            nc.vector.tensor_mul(out=slope_shift[:], in0=slope[:], in1=shift[:])
+
+            for b in range(B):
+                att_b = att[:, 2 * b : 2 * b + 2, :].rearrange("p t x -> p (t x)")
+                positive = pair.tile([P, H2 * W2], F32)
+                nc.scalar.activation(
+                    out=positive[:], in_=att_b, func=ACT.Relu, bias=shift[:], scale=gain[:]
+                )
+                final = pair.tile([P, H2 * W2], F32)
+                nc.vector.tensor_scalar(
+                    out=final[:], in0=att_b, scalar1=slope_gain[:], scalar2=slope_shift[:],
+                    op0=ALU.mult, op1=ALU.add,
+                )
+                nc.vector.scalar_tensor_tensor(
+                    out=final[:], in0=positive[:], scalar=one_minus_slope[:], in1=final[:],
+                    op0=ALU.mult, op1=ALU.add,
+                )
+                nc.sync.dma_start(out=out[b].rearrange("o i j -> o (i j)"), in_=final[:])

@@ -29,6 +29,9 @@ BLOCKS = HALF // P
 BLOCK_ROWS = P // W2
 OFFSETS = [(di, dj) for di in range(3) for dj in range(3)]
 N_OFF = len(OFFSETS)
+SETS = 2
+LEAD = 3
+VECTOR_SHIFTS = 4
 
 FLOPS = 2 * B * H2 * W2 * (M * C + 3 * O * M)
 
@@ -55,14 +58,17 @@ def tile_merge_pa_t_kernel(
         wqkv_scales = keep.tile([P, 3, O], U8, align_bytes=64)
         bias = keep.tile([P, M_TILES], F32)
 
-        q_all = keep.tile([P, B, H2 * W2], F32)
-        k_ring = keep.tile([P, B, H2 + 2, W2 + 2], F32)
-        v_moved = keep.tile([P, B, 3, H2 + 2, W2], F32)
+        q_sets = keep.tile([P, SETS, H2 * W2], F32)
+        k_ring = keep.tile([P, SETS, H2 + 2, W2 + 2], F32)
+        v_moved = keep.tile([P, SETS, 3, H2 + 2, W2], F32)
         nc.gpsimd.memset(k_ring[:], 0.0)
         nc.gpsimd.memset(v_moved[:, :, :, 0, :], 0.0)
         nc.gpsimd.memset(v_moved[:, :, :, H2 + 1, :], 0.0)
         nc.gpsimd.memset(v_moved[:, :, 0, :, 0:8], 0.0)
         nc.gpsimd.memset(v_moved[:, :, 2, :, W2 - 8 : W2], 0.0)
+
+        att = keep.tile([P, N_HALVES, HALF], F32)
+        stats = keep.tile([P, N_HALVES, 6], F32)
 
         bias_bf16 = keep.tile([P, M_TILES], BF16)
         nc.scalar.dma_start(out=bias_bf16[:], in_=b_c1.rearrange("(n t) -> n t", t=M_TILES))
@@ -76,85 +82,34 @@ def tile_merge_pa_t_kernel(
         beta = keep.tile([P, 1], F32)
         slope = keep.tile([P, 1], F32)
         one_minus_slope = keep.tile([P, 1], F32)
+        nc.vector.tensor_copy(out=bias[:], in_=bias_bf16[:])
+        nc.vector.tensor_copy(out=gamma[:], in_=gamma_bf16[:])
+        nc.vector.tensor_copy(out=beta[:], in_=beta_bf16[:])
+        nc.vector.tensor_copy(out=slope[:], in_=slope_bf16[:])
+        nc.vector.tensor_scalar(
+            out=one_minus_slope[:], in0=slope[:], scalar1=-1.0, scalar2=1.0,
+            op0=ALU.mult, op1=ALU.add,
+        )
 
-        with ExitStack() as front:
-            stage = front.enter_context(tc.tile_pool(name="stage", bufs=1))
-            x_pool = front.enter_context(tc.tile_pool(name="x_pool", bufs=4))
-            work = front.enter_context(tc.tile_pool(name="work", bufs=2))
-            turned_psum = front.enter_context(tc.psum_pool(name="turned_psum", bufs=2))
-            mx_psum = front.enter_context(tc.psum_pool(name="mx_psum", bufs=3))
-
-            def load_piece(half, g, s):
-                b, h = divmod(half, 2)
-                row = 2 * (h * HALF_ROWS + s * PIECE_ROWS)
-                x_piece = x_pool.tile([P, PACK, 2 * PIECE_ROWS * W], BF16)
-                nc.sync.dma_start(
-                    out=x_piece[:],
-                    in_=x[
-                        b, g * K_PASS : (g + 1) * K_PASS, row : row + 2 * PIECE_ROWS, :
-                    ].rearrange("(p j) r w -> p j (r w)", j=PACK),
-                )
-                return x_piece
-
-            w1_rows = stage.tile([P, M_TILES, C], BF16)
-            nc.scalar.dma_start(out=w1_rows[:], in_=w_c1.rearrange("(n t) c -> n t c", t=M_TILES))
-            wqkv_rows = stage.tile([P, 3, M], BF16)
-            for s, w_s in enumerate((w_q, w_k, w_v)):
-                nc.scalar.dma_start(out=wqkv_rows[:, s, :], in_=w_s)
-
-            nc.vector.tensor_copy(out=bias[:], in_=bias_bf16[:])
-            nc.vector.tensor_copy(out=gamma[:], in_=gamma_bf16[:])
-            nc.vector.tensor_copy(out=beta[:], in_=beta_bf16[:])
-            nc.vector.tensor_copy(out=slope[:], in_=slope_bf16[:])
-            nc.vector.tensor_scalar(
-                out=one_minus_slope[:], in0=slope[:], scalar1=-1.0, scalar2=1.0,
-                op0=ALU.mult, op1=ALU.add,
-            )
-
-            w1_sorted = stage.tile([P, M_TILES, C_PASSES, PACK, P], BF16)
-            w1_grouped = stage.tile([P, C_PASSES, M_TILES, P, PACK], BF16, align_bytes=64)
-            for t in range(M_TILES):
-                nc.scalar.copy(
-                    out=w1_sorted[:, t],
-                    in_=w1_rows[:, t, :].rearrange("n (g p j) -> n g j p", g=C_PASSES, j=PACK),
-                )
-                for g in range(C_PASSES):
-                    turned = turned_psum.tile([P, PACK, P], BF16)
-                    for j in range(PACK):
-                        nc.tensor.transpose(turned[:, j, :], w1_sorted[:, t, g, j, :], ident_bf16[:])
-                    nc.scalar.copy(
-                        out=w1_grouped[:, g, t], in_=turned[:].rearrange("p j n -> p n j")
-                    )
-            wqkv_sorted = stage.tile([P, 3, PACK, P], BF16)
-            wqkv_grouped = stage.tile([P, 3, O, PACK], BF16, align_bytes=64)
-            nc.scalar.copy(
-                out=wqkv_sorted[:], in_=wqkv_rows[:].rearrange("o s (p j) -> o s j p", j=PACK)
-            )
-            for s in range(3):
-                turned = turned_psum.tile([P, PACK, P], BF16)
-                for j in range(PACK):
-                    nc.tensor.transpose(turned[:, j, :], wqkv_sorted[:, s, j, :], ident_bf16[:])
-                nc.scalar.copy(out=wqkv_grouped[:, s], in_=turned[:].rearrange("p j o -> p o j"))
-
-            def quantise_weights():
-                for g in range(C_PASSES):
-                    nc.vector.quantize_mx(
-                        out=w1_codes[:, g, :].bitcast(FP8X4),
-                        scales=w1_scales[:, g, :],
-                        in_=w1_grouped[:, g].rearrange("p t n j -> p (t n j)"),
-                    )
-                for s in range(3):
-                    nc.vector.quantize_mx(
-                        out=wqkv_codes[:, s, :].bitcast(FP8X4),
-                        scales=wqkv_scales[:, s, :],
-                        in_=wqkv_grouped[:, s].rearrange("p o j -> p (o j)"),
-                    )
+        with ExitStack() as stream:
+            x_pool = stream.enter_context(tc.tile_pool(name="x_pool", bufs=3))
+            work = stream.enter_context(tc.tile_pool(name="work", bufs=2))
+            single = stream.enter_context(tc.tile_pool(name="single", bufs=1))
+            mx_psum = stream.enter_context(tc.psum_pool(name="mx_psum", bufs=2))
 
             def haar(half):
+                b, h = divmod(half, 2)
                 ll_grouped = work.tile([P, C_PASSES, HALF, PACK], BF16, align_bytes=64)
                 for g in range(C_PASSES):
                     for s in range(HALF_ROWS // PIECE_ROWS):
-                        x_piece = load_piece(half, g, s)
+                        row = 2 * (h * HALF_ROWS + s * PIECE_ROWS)
+                        x_piece = x_pool.tile([P, PACK, 2 * PIECE_ROWS * W], BF16)
+                        nc.sync.dma_start(
+                            out=x_piece[:],
+                            in_=x[
+                                b, g * K_PASS : (g + 1) * K_PASS, row : row + 2 * PIECE_ROWS, :
+                            ].rearrange("(p j) r w -> p j (r w)", j=PACK),
+                        )
                         rows = x_piece[:].rearrange("p j (r two w) -> p (j r) two w", two=2, w=W)
                         row_sum = work.tile([P, PACK * PIECE_ROWS, W], F32)
                         nc.vector.tensor_tensor(
@@ -179,10 +134,10 @@ def tile_merge_pa_t_kernel(
                     scales=ll_scales[:].rearrange("p g x -> p (g x)"),
                     in_=ll_grouped[:].rearrange("p g x j -> p (g x j)"),
                 )
-                y_grouped = work.tile([P, HALF, PACK], BF16, align_bytes=64)
+                y_rows = single.tile([P, M_TILES, HALF], BF16)
                 for t in range(M_TILES):
                     cols = slice(t * P, (t + 1) * P)
-                    y_acc = mx_psum.tile([P, HALF], F32)
+                    y_acc = mx_psum.tile([P, HALF], F32, tag="mx")
                     for g in range(C_PASSES):
                         nc.tensor.matmul_mx(
                             out=y_acc[:],
@@ -194,14 +149,16 @@ def tile_merge_pa_t_kernel(
                             stop=(g == C_PASSES - 1),
                         )
                     nc.scalar.activation(
-                        out=y_grouped[:, :, t], in_=y_acc[:], func=ACT.Identity,
+                        out=y_rows[:, t, :], in_=y_acc[:], func=ACT.Identity,
                         bias=bias[:, t : t + 1], scale=0.5,
                     )
+                y_grouped = single.tile([P, HALF, PACK], BF16, align_bytes=64)
+                nc.scalar.copy(out=y_grouped[:], in_=y_rows[:].rearrange("p t x -> p x t"))
                 return y_grouped
 
             def project(half, y_grouped):
                 b, h = divmod(half, 2)
-                top = 1 + h * HALF_ROWS
+                rows = slice(1 + h * HALF_ROWS, 1 + (h + 1) * HALF_ROWS)
                 y_codes = work.tile([P, HALF], U32, align_bytes=64)
                 y_scales = work.tile([P, HALF], U8, align_bytes=64)
                 nc.vector.quantize_mx(
@@ -209,9 +166,8 @@ def tile_merge_pa_t_kernel(
                     scales=y_scales[:],
                     in_=y_grouped[:].rearrange("p x t -> p (x t)"),
                 )
-                qkv = []
                 for s in range(3):
-                    proj = mx_psum.tile([P, HALF_ROWS, W2], F32)
+                    proj = mx_psum.tile([P, HALF_ROWS, W2], F32, tag="mx")
                     nc.tensor.matmul_mx(
                         out=proj[:].rearrange("p r w -> p (r w)"),
                         lhsT=wqkv_codes[:, s, :].bitcast(FP8X4),
@@ -221,83 +177,132 @@ def tile_merge_pa_t_kernel(
                         start=True,
                         stop=True,
                     )
-                    qkv.append(proj)
-                q_acc, k_acc, v_acc = qkv
-                rows = slice(top, top + HALF_ROWS)
-                nc.scalar.copy(
-                    out=q_all[:, b, h * HALF : (h + 1) * HALF],
-                    in_=q_acc[:].rearrange("p r w -> p (r w)"),
+                    if s == 0:
+                        nc.scalar.copy(
+                            out=q_sets[:, b % SETS, h * HALF : (h + 1) * HALF],
+                            in_=proj[:].rearrange("p r w -> p (r w)"),
+                        )
+                    elif s == 1:
+                        nc.scalar.copy(out=k_ring[:, b % SETS, rows, 1 : W2 + 1], in_=proj[:])
+                    else:
+                        v_set = v_moved[:, b % SETS]
+                        nc.scalar.copy(out=v_set[:, 0, rows, 1:W2], in_=proj[:, :, 0 : W2 - 1])
+                        nc.scalar.copy(out=v_set[:, 1, rows, :], in_=proj[:])
+                        nc.scalar.copy(out=v_set[:, 2, rows, 0 : W2 - 1], in_=proj[:, :, 1:W2])
+
+            with tc.tile_pool(name="stage", bufs=1) as stage:
+                w1_rows = stage.tile([P, M_TILES, C], BF16)
+                nc.scalar.dma_start(
+                    out=w1_rows[:], in_=w_c1.rearrange("(n t) c -> n t c", t=M_TILES)
                 )
-                nc.scalar.copy(out=k_ring[:, b, rows, 1 : W2 + 1], in_=k_acc[:])
-                nc.scalar.copy(out=v_moved[:, b, 0, rows, 1:W2], in_=v_acc[:, :, 0 : W2 - 1])
-                nc.scalar.copy(out=v_moved[:, b, 1, rows, :], in_=v_acc[:])
-                nc.scalar.copy(out=v_moved[:, b, 2, rows, 0 : W2 - 1], in_=v_acc[:, :, 1:W2])
+                wqkv_rows = stage.tile([P, 3, M], BF16)
+                for s, w_s in enumerate((w_q, w_k, w_v)):
+                    nc.scalar.dma_start(out=wqkv_rows[:, s, :], in_=w_s)
+                w1_sorted = stage.tile([P, M_TILES, C_PASSES, PACK, P], BF16)
+                w1_grouped = stage.tile([P, C_PASSES, M_TILES, P, PACK], BF16, align_bytes=64)
+                for t in range(M_TILES):
+                    nc.scalar.copy(
+                        out=w1_sorted[:, t],
+                        in_=w1_rows[:, t, :].rearrange("n (g p j) -> n g j p", g=C_PASSES, j=PACK),
+                    )
+                    for g in range(C_PASSES):
+                        turned = mx_psum.tile([P, PACK, P], BF16, tag="mx")
+                        for j in range(PACK):
+                            nc.tensor.transpose(
+                                turned[:, j, :], w1_sorted[:, t, g, j, :], ident_bf16[:]
+                            )
+                        nc.scalar.copy(
+                            out=w1_grouped[:, g, t], in_=turned[:].rearrange("p j n -> p n j")
+                        )
+                wqkv_sorted = stage.tile([P, 3, PACK, P], BF16)
+                wqkv_grouped = stage.tile([P, 3, O, PACK], BF16, align_bytes=64)
+                nc.scalar.copy(
+                    out=wqkv_sorted[:], in_=wqkv_rows[:].rearrange("o s (p j) -> o s j p", j=PACK)
+                )
+                for s in range(3):
+                    turned = mx_psum.tile([P, PACK, P], BF16, tag="mx")
+                    for j in range(PACK):
+                        nc.tensor.transpose(turned[:, j, :], wqkv_sorted[:, s, j, :], ident_bf16[:])
+                    nc.scalar.copy(
+                        out=wqkv_grouped[:, s], in_=turned[:].rearrange("p j o -> p o j")
+                    )
+                ll_grouped = haar(0)
+                for g in range(C_PASSES):
+                    nc.vector.quantize_mx(
+                        out=w1_codes[:, g, :].bitcast(FP8X4),
+                        scales=w1_scales[:, g, :],
+                        in_=w1_grouped[:, g].rearrange("p t n j -> p (t n j)"),
+                    )
+                for s in range(3):
+                    nc.vector.quantize_mx(
+                        out=wqkv_codes[:, s, :].bitcast(FP8X4),
+                        scales=wqkv_scales[:, s, :],
+                        in_=wqkv_grouped[:, s].rearrange("p o j -> p (o j)"),
+                    )
 
-            y_waiting = None
-            for half in range(N_HALVES + 1):
-                if half < N_HALVES:
-                    ll_grouped = haar(half)
-                if half == 0:
-                    quantise_weights()
-                if half >= 1:
-                    project(half - 1, y_waiting)
-                if half < N_HALVES:
-                    y_waiting = first_convolution(ll_grouped)
-
-        with ExitStack() as back:
-            z_pool = back.enter_context(tc.tile_pool(name="z_pool", bufs=2, reuse_waits="tile"))
-            tree = back.enter_context(tc.tile_pool(name="tree", bufs=1, reuse_waits="tile"))
-            e_pool = back.enter_context(tc.tile_pool(name="e_pool", bufs=N_OFF + 1, reuse_waits="tile"))
-            prod_pool = back.enter_context(tc.tile_pool(name="prod_pool", bufs=3, reuse_waits="tile"))
-            pair = back.enter_context(tc.tile_pool(name="pair", bufs=2, reuse_waits="tile"))
-            result = back.enter_context(tc.tile_pool(name="result", bufs=1, reuse_waits="tile"))
-            back_psum = back.enter_context(tc.psum_pool(name="back_psum", bufs=2, reuse_waits="tile"))
-
-            att = result.tile([P, N_HALVES, HALF], F32)
-            stats = result.tile([P, N_HALVES, 6], F32)
+            z_pool = stream.enter_context(tc.tile_pool(name="z_pool", bufs=2, reuse_waits="tile"))
+            e_pool = stream.enter_context(
+                tc.tile_pool(name="e_pool", bufs=N_OFF, reuse_waits="tile")
+            )
+            prod_pool = stream.enter_context(
+                tc.tile_pool(name="prod_pool", bufs=3, reuse_waits="tile")
+            )
+            turn_psum = stream.enter_context(tc.psum_pool(name="turn_psum", bufs=2))
+            sum_psum = stream.enter_context(tc.psum_pool(name="sum_psum", bufs=1))
 
             def scores(half):
                 b, h = divmod(half, 2)
                 top = h * HALF_ROWS
-                q_half = q_all[:, b, h * HALF : (h + 1) * HALF].rearrange("p (r w) -> p r w", w=W2)
+                q_half = q_sets[:, b % SETS, h * HALF : (h + 1) * HALF].rearrange(
+                    "p (r w) -> p r w", w=W2
+                )
                 z = z_pool.tile([P, N_OFF, HALF], F32)
                 for d, (di, dj) in enumerate(OFFSETS):
                     nc.vector.tensor_tensor(
                         out=z[:, d, :].rearrange("p (r w) -> p r w", w=W2),
                         in0=q_half,
-                        in1=k_ring[:, b, top + di : top + di + HALF_ROWS, dj : dj + W2],
+                        in1=k_ring[:, b % SETS, top + di : top + di + HALF_ROWS, dj : dj + W2],
                         op=ALU.mult,
                     )
-                max4 = tree.tile([P, 4, HALF], F32)
-                nc.vector.tensor_tensor(out=max4[:], in0=z[:, 0:4, :], in1=z[:, 4:8, :], op=ALU.max)
-                max2 = tree.tile([P, 2, HALF], F32)
+                tree = single.tile([P, 4, HALF], F32)
+                nc.vector.tensor_tensor(out=tree[:], in0=z[:, 0:4, :], in1=z[:, 4:8, :], op=ALU.max)
                 nc.vector.tensor_tensor(
-                    out=max2[:], in0=max4[:, 0:2, :], in1=max4[:, 2:4, :], op=ALU.max
+                    out=tree[:, 0:2, :], in0=tree[:, 0:2, :], in1=tree[:, 2:4, :], op=ALU.max
                 )
-                max1 = tree.tile([P, HALF], F32)
                 nc.vector.tensor_tensor(
-                    out=max1[:], in0=max2[:, 0, :], in1=max2[:, 1, :], op=ALU.max
+                    out=tree[:, 0, :], in0=tree[:, 0, :], in1=tree[:, 1, :], op=ALU.max
                 )
-                z_max = tree.tile([P, HALF], F32)
-                nc.vector.tensor_tensor(out=z_max[:], in0=max1[:], in1=z[:, 8, :], op=ALU.max)
-                neg_max = pair.tile([P, HALF], F32)
-                nc.scalar.mul(out=neg_max[:], in_=z_max[:], mul=-1.0)
+                z_max = tree[:, 1:2, :]
+                nc.vector.tensor_tensor(
+                    out=z_max, in0=tree[:, 0:1, :], in1=z[:, 8:9, :], op=ALU.max
+                )
+                neg_max = work.tile([P, HALF], F32)
+                nc.scalar.mul(out=neg_max[:], in_=tree[:, 1, :], mul=-1.0)
+                nc.vector.tensor_tensor(
+                    out=z[:, 0:VECTOR_SHIFTS, :],
+                    in0=z[:, 0:VECTOR_SHIFTS, :],
+                    in1=z_max.to_broadcast([P, VECTOR_SHIFTS, HALF]),
+                    op=ALU.subtract,
+                )
                 return z, neg_max
 
             def weights(z, neg_max):
                 e_tiles = []
-                e_sum = back_psum.tile([P, HALF], F32)
+                e_sum = sum_psum.tile([P, HALF], F32)
                 for d in range(N_OFF + 1):
                     if d < N_OFF:
-                        shifted = back_psum.tile([P, BLOCKS, P], F32)
+                        shifted = turn_psum.tile([P, BLOCKS, P], F32)
                         for blk in range(BLOCKS):
                             cols = slice(blk * P, (blk + 1) * P)
+                            alone = d < VECTOR_SHIFTS
                             add_transposed(
-                                nc, shifted[:, blk, :], z[:, d, cols], ident_f32[:], True, False
+                                nc, shifted[:, blk, :], z[:, d, cols], ident_f32[:], True, alone
                             )
-                            add_transposed(
-                                nc, shifted[:, blk, :], neg_max[:, cols], ident_f32[:], False, True
-                            )
+                            if not alone:
+                                add_transposed(
+                                    nc, shifted[:, blk, :], neg_max[:, cols], ident_f32[:],
+                                    False, True,
+                                )
                         e_t = e_pool.tile([P, BLOCKS, P], F32)
                         nc.scalar.activation(out=e_t[:], in_=shifted[:], func=ACT.Exp)
                         e_tiles.append(e_t)
@@ -309,26 +314,26 @@ def tile_merge_pa_t_kernel(
                                 d - 1 == 0 and blk == 0,
                                 d - 1 == N_OFF - 1 and blk == BLOCKS - 1,
                             )
-                log_sum = pair.tile([P, HALF], F32)
+                log_sum = single.tile([P, HALF], F32)
                 nc.scalar.activation(out=log_sum[:], in_=e_sum[:], func=ACT.Ln)
-                inv_sum = pair.tile([P, HALF], F32)
+                inv_sum = work.tile([P, HALF], F32)
                 nc.scalar.activation(out=inv_sum[:], in_=log_sum[:], func=ACT.Exp, scale=-1.0)
                 return e_tiles, inv_sum
 
             def mix(half, e_tiles, inv_sum):
                 b, h = divmod(half, 2)
                 top = h * HALF_ROWS
-                ev_sum = back_psum.tile([P, HALF], F32)
+                ev_sum = sum_psum.tile([P, HALF], F32)
                 prods = []
                 for d in range(N_OFF + 1):
                     if d < N_OFF:
                         di, dj = OFFSETS[d]
-                        v_t = back_psum.tile([P, BLOCKS, P], F32)
+                        v_t = turn_psum.tile([P, BLOCKS, P], F32)
                         for blk in range(BLOCKS):
                             row = top + blk * BLOCK_ROWS + di
                             nc.tensor.transpose(
                                 v_t[:, blk, :],
-                                v_moved[:, b, dj, row : row + BLOCK_ROWS, :].rearrange(
+                                v_moved[:, b % SETS, dj, row : row + BLOCK_ROWS, :].rearrange(
                                     "p r w -> p (r w)"
                                 ),
                                 ident_f32[:],
@@ -351,46 +356,54 @@ def tile_merge_pa_t_kernel(
                 )
                 nc.vector.bn_stats(out=stats[:, half, :], in_=att[:, half, :])
 
-            ready = weights(*scores(0))
-            for half in range(N_HALVES):
-                if half + 1 < N_HALVES:
-                    scored = scores(half + 1)
-                mix(half, *ready)
-                if half + 1 < N_HALVES:
-                    ready = weights(*scored)
+            for step in range(N_HALVES + LEAD):
+                t = step - LEAD
+                if 1 <= step <= N_HALVES:
+                    project(step - 1, y_grouped)
+                if 0 <= t:
+                    e_tiles, inv_sum = weights(z, neg_max)
+                if 1 <= step < N_HALVES:
+                    ll_grouped = haar(step)
+                if step < N_HALVES:
+                    y_grouped = first_convolution(ll_grouped)
+                if 0 <= t + 1 < N_HALVES:
+                    z, neg_max = scores(t + 1)
+                if 0 <= t:
+                    mix(t, e_tiles, inv_sum)
 
-            mean_var = result.tile([P, 2], F32)
-            nc.vector.bn_aggr(out=mean_var[:], in_=stats[:].rearrange("p t s -> p (t s)"))
-            var_eps = result.tile([P, 1], F32)
-            nc.vector.tensor_scalar_add(out=var_eps[:], in0=mean_var[:, 1:2], scalar1=BN_EPS)
-            std = result.tile([P, 1], F32)
-            nc.scalar.sqrt(out=std[:], in_=var_eps[:])
-            inv_std = result.tile([P, 1], F32)
-            nc.vector.reciprocal(out=inv_std[:], in_=std[:])
-            gain = result.tile([P, 1], F32)
-            nc.vector.tensor_mul(out=gain[:], in0=gamma[:], in1=inv_std[:])
-            mean_gain = result.tile([P, 1], F32)
-            nc.vector.tensor_mul(out=mean_gain[:], in0=mean_var[:, 0:1], in1=gain[:])
-            shift = result.tile([P, 1], F32)
-            nc.vector.tensor_sub(out=shift[:], in0=beta[:], in1=mean_gain[:])
-            slope_gain = result.tile([P, 1], F32)
-            nc.vector.tensor_mul(out=slope_gain[:], in0=slope[:], in1=gain[:])
-            slope_shift = result.tile([P, 1], F32)
-            nc.vector.tensor_mul(out=slope_shift[:], in0=slope[:], in1=shift[:])
+        last = whole.enter_context(tc.tile_pool(name="last", bufs=2, reuse_waits="tile"))
+        mean_var = last.tile([P, 2], F32)
+        nc.vector.bn_aggr(out=mean_var[:], in_=stats[:].rearrange("p t s -> p (t s)"))
+        var_eps = last.tile([P, 1], F32)
+        nc.vector.tensor_scalar_add(out=var_eps[:], in0=mean_var[:, 1:2], scalar1=BN_EPS)
+        std = last.tile([P, 1], F32)
+        nc.scalar.sqrt(out=std[:], in_=var_eps[:])
+        inv_std = last.tile([P, 1], F32)
+        nc.vector.reciprocal(out=inv_std[:], in_=std[:])
+        gain = last.tile([P, 1], F32)
+        nc.vector.tensor_mul(out=gain[:], in0=gamma[:], in1=inv_std[:])
+        mean_gain = last.tile([P, 1], F32)
+        nc.vector.tensor_mul(out=mean_gain[:], in0=mean_var[:, 0:1], in1=gain[:])
+        shift = last.tile([P, 1], F32)
+        nc.vector.tensor_sub(out=shift[:], in0=beta[:], in1=mean_gain[:])
+        slope_gain = last.tile([P, 1], F32)
+        nc.vector.tensor_mul(out=slope_gain[:], in0=slope[:], in1=gain[:])
+        slope_shift = last.tile([P, 1], F32)
+        nc.vector.tensor_mul(out=slope_shift[:], in0=slope[:], in1=shift[:])
 
-            for b in range(B):
-                att_b = att[:, 2 * b : 2 * b + 2, :].rearrange("p t x -> p (t x)")
-                positive = pair.tile([P, H2 * W2], F32)
-                nc.scalar.activation(
-                    out=positive[:], in_=att_b, func=ACT.Relu, bias=shift[:], scale=gain[:]
-                )
-                final = pair.tile([P, H2 * W2], F32)
-                nc.vector.tensor_scalar(
-                    out=final[:], in0=att_b, scalar1=slope_gain[:], scalar2=slope_shift[:],
-                    op0=ALU.mult, op1=ALU.add,
-                )
-                nc.vector.scalar_tensor_tensor(
-                    out=final[:], in0=positive[:], scalar=one_minus_slope[:], in1=final[:],
-                    op0=ALU.mult, op1=ALU.add,
-                )
-                nc.sync.dma_start(out=out[b].rearrange("o i j -> o (i j)"), in_=final[:])
+        for b in range(B):
+            att_b = att[:, 2 * b : 2 * b + 2, :].rearrange("p t x -> p (t x)")
+            positive = last.tile([P, H2 * W2], F32)
+            nc.scalar.activation(
+                out=positive[:], in_=att_b, func=ACT.Relu, bias=shift[:], scale=gain[:]
+            )
+            final = last.tile([P, H2 * W2], F32)
+            nc.vector.tensor_scalar(
+                out=final[:], in0=att_b, scalar1=slope_gain[:], scalar2=slope_shift[:],
+                op0=ALU.mult, op1=ALU.add,
+            )
+            nc.vector.scalar_tensor_tensor(
+                out=final[:], in0=positive[:], scalar=one_minus_slope[:], in1=final[:],
+                op0=ALU.mult, op1=ALU.add,
+            )
+            nc.sync.dma_start(out=out[b].rearrange("o i j -> o (i j)"), in_=final[:])

@@ -26,12 +26,11 @@ N_HALVES = B * H2 * W2 // HALF
 PIECE_ROWS = 8
 PIECE = PIECE_ROWS * W2
 BLOCKS = HALF // P
-BLOCK_ROWS = P // W2
-OFFSETS = [(di, dj) for di in range(3) for dj in range(3)]
-N_OFF = len(OFFSETS)
+KS = 3
 SETS = 2
-LEAD = 3
-VECTOR_SHIFTS = 4
+LEAD = 2
+TAPS = [(a, c) for a in range(2) for c in range(2)]
+HALF_ON_TENSOR = 1
 
 FLOPS = 2 * B * H2 * W2 * (M * C + 3 * O * M)
 
@@ -60,12 +59,9 @@ def tile_merge_pa_t_kernel(
 
         q_sets = keep.tile([P, SETS, H2 * W2], F32)
         k_ring = keep.tile([P, SETS, H2 + 2, W2 + 2], F32)
-        v_moved = keep.tile([P, SETS, 3, H2 + 2, W2], F32)
+        v_ring = keep.tile([P, SETS, H2 + 2, W2 + 2], F32)
         nc.gpsimd.memset(k_ring[:], 0.0)
-        nc.gpsimd.memset(v_moved[:, :, :, 0, :], 0.0)
-        nc.gpsimd.memset(v_moved[:, :, :, H2 + 1, :], 0.0)
-        nc.gpsimd.memset(v_moved[:, :, 0, :, 0:8], 0.0)
-        nc.gpsimd.memset(v_moved[:, :, 2, :, W2 - 8 : W2], 0.0)
+        nc.gpsimd.memset(v_ring[:], 0.0)
 
         att = keep.tile([P, N_HALVES, HALF], F32)
         stats = keep.tile([P, N_HALVES, 6], F32)
@@ -100,8 +96,11 @@ def tile_merge_pa_t_kernel(
             def haar(half):
                 b, h = divmod(half, 2)
                 ll_grouped = work.tile([P, C_PASSES, HALF, PACK], BF16, align_bytes=64)
-                for g in range(C_PASSES):
-                    for s in range(HALF_ROWS // PIECE_ROWS):
+                pieces = [(g, s) for g in range(C_PASSES) for s in range(HALF // PIECE)]
+                row_sums = []
+                for i in range(len(pieces) + 1):
+                    if i < len(pieces):
+                        g, s = pieces[i]
                         row = 2 * (h * HALF_ROWS + s * PIECE_ROWS)
                         x_piece = x_pool.tile([P, PACK, 2 * PIECE_ROWS * W], BF16)
                         nc.sync.dma_start(
@@ -115,7 +114,10 @@ def tile_merge_pa_t_kernel(
                         nc.vector.tensor_tensor(
                             out=row_sum[:], in0=rows[:, :, 0, :], in1=rows[:, :, 1, :], op=ALU.add
                         )
-                        pairs = row_sum[:].rearrange(
+                        row_sums.append(row_sum)
+                    if i >= 1:
+                        g, s = pieces[i - 1]
+                        pairs = row_sums[i - 1][:].rearrange(
                             "p (j r) (w two) -> p j (r w) two", j=PACK, two=2
                         )
                         nc.vector.tensor_tensor(
@@ -124,6 +126,40 @@ def tile_merge_pa_t_kernel(
                             in1=pairs[:, :, :, 1].rearrange("p j x -> p x j"),
                             op=ALU.add,
                         )
+                return ll_grouped
+
+            def haar_by_matmul(half, early):
+                b, h = divmod(half, 2)
+                ll_grouped = work.tile([P, C_PASSES, HALF, PACK], BF16, align_bytes=64)
+                for g in range(C_PASSES):
+                    for s in range(HALF // PIECE):
+                        row = 2 * (h * HALF_ROWS + s * PIECE_ROWS)
+                        x_early = early.tile([P, PACK, 2 * PIECE_ROWS * W], BF16)
+                        nc.sync.dma_start(
+                            out=x_early[:],
+                            in_=x[
+                                b, g * K_PASS : (g + 1) * K_PASS, row : row + 2 * PIECE_ROWS, :
+                            ].rearrange("(p j) r w -> p j (r w)", j=PACK),
+                        )
+                        pixels = x_early[:].rearrange(
+                            "p j (r a w c) -> p j r a w c", a=2, w=W2, c=2
+                        )
+                        for first in range(0, PACK, 2):
+                            total = mx_psum.tile([P, 2, PIECE_ROWS, W2], F32, tag="mx")
+                            for tap, (a, c) in enumerate(TAPS):
+                                nc.tensor.matmul(
+                                    out=total[:],
+                                    lhsT=ident_bf16[:],
+                                    rhs=pixels[:, first : first + 2, :, a, :, c],
+                                    start=(tap == 0),
+                                    stop=(tap == len(TAPS) - 1),
+                                )
+                            nc.scalar.copy(
+                                out=ll_grouped[
+                                    :, g, s * PIECE : (s + 1) * PIECE, first : first + 2
+                                ],
+                                in_=total[:].rearrange("p j r w -> p (r w) j"),
+                            )
                 return ll_grouped
 
             def first_convolution(ll_grouped):
@@ -185,12 +221,11 @@ def tile_merge_pa_t_kernel(
                     elif s == 1:
                         nc.scalar.copy(out=k_ring[:, b % SETS, rows, 1 : W2 + 1], in_=proj[:])
                     else:
-                        v_set = v_moved[:, b % SETS]
-                        nc.scalar.copy(out=v_set[:, 0, rows, 1:W2], in_=proj[:, :, 0 : W2 - 1])
-                        nc.scalar.copy(out=v_set[:, 1, rows, :], in_=proj[:])
-                        nc.scalar.copy(out=v_set[:, 2, rows, 0 : W2 - 1], in_=proj[:, :, 1:W2])
+                        nc.scalar.copy(out=v_ring[:, b % SETS, rows, 1 : W2 + 1], in_=proj[:])
 
-            with tc.tile_pool(name="stage", bufs=1) as stage:
+            with tc.tile_pool(name="stage", bufs=1) as stage, tc.tile_pool(
+                name="early", bufs=3
+            ) as early:
                 w1_rows = stage.tile([P, M_TILES, C], BF16)
                 nc.scalar.dma_start(
                     out=w1_rows[:], in_=w_c1.rearrange("(n t) c -> n t c", t=M_TILES)
@@ -226,7 +261,7 @@ def tile_merge_pa_t_kernel(
                     nc.scalar.copy(
                         out=wqkv_grouped[:, s], in_=turned[:].rearrange("p j o -> p o j")
                     )
-                ll_grouped = haar(0)
+                ll_first = [haar(0), haar_by_matmul(HALF_ON_TENSOR, early)]
                 for g in range(C_PASSES):
                     nc.vector.quantize_mx(
                         out=w1_codes[:, g, :].bitcast(FP8X4),
@@ -241,135 +276,103 @@ def tile_merge_pa_t_kernel(
                     )
 
             z_pool = stream.enter_context(tc.tile_pool(name="z_pool", bufs=2, reuse_waits="tile"))
-            e_pool = stream.enter_context(
-                tc.tile_pool(name="e_pool", bufs=N_OFF, reuse_waits="tile")
-            )
             prod_pool = stream.enter_context(
                 tc.tile_pool(name="prod_pool", bufs=3, reuse_waits="tile")
             )
-            turn_psum = stream.enter_context(tc.psum_pool(name="turn_psum", bufs=2))
-            sum_psum = stream.enter_context(tc.psum_pool(name="sum_psum", bufs=1))
+            sum_psum = stream.enter_context(tc.psum_pool(name="sum_psum", bufs=2))
+            turn_psum = stream.enter_context(tc.psum_pool(name="turn_psum", bufs=1))
 
-            def scores(half):
+            def add_over_window(total, terms, di):
+                for dj in range(KS):
+                    for blk in range(BLOCKS):
+                        cols = slice(blk * P, (blk + 1) * P)
+                        add_transposed(
+                            nc, total[:, cols], terms[:, dj, cols], ident_f32[:],
+                            di == 0 and dj == 0 and blk == 0,
+                            di == KS - 1 and dj == KS - 1 and blk == BLOCKS - 1,
+                        )
+
+            def attend(half):
                 b, h = divmod(half, 2)
                 top = h * HALF_ROWS
                 q_half = q_sets[:, b % SETS, h * HALF : (h + 1) * HALF].rearrange(
                     "p (r w) -> p r w", w=W2
                 )
-                z = z_pool.tile([P, N_OFF, HALF], F32)
-                for d, (di, dj) in enumerate(OFFSETS):
+                z = z_pool.tile([P, KS, KS, HALF], F32)
+                z_rough = single.tile([P, KS, KS, HALF], BF16)
+                for di in range(KS):
+                    for dj in range(KS):
+                        nc.vector.tensor_tensor(
+                            out=z[:, di, dj, :].rearrange("p (r w) -> p r w", w=W2),
+                            in0=q_half,
+                            in1=k_ring[:, b % SETS, top + di : top + di + HALF_ROWS, dj : dj + W2],
+                            op=ALU.mult,
+                        )
+                    nc.scalar.copy(out=z_rough[:, di], in_=z[:, di])
+                tree = single.tile([P, KS, HALF], BF16)
+                nc.vector.tensor_tensor(
+                    out=tree[:], in0=z_rough[:, 0], in1=z_rough[:, 1], op=ALU.max
+                )
+                nc.vector.tensor_tensor(out=tree[:], in0=tree[:], in1=z_rough[:, 2], op=ALU.max)
+                for dj in range(1, KS):
                     nc.vector.tensor_tensor(
-                        out=z[:, d, :].rearrange("p (r w) -> p r w", w=W2),
-                        in0=q_half,
-                        in1=k_ring[:, b % SETS, top + di : top + di + HALF_ROWS, dj : dj + W2],
-                        op=ALU.mult,
+                        out=tree[:, 0, :], in0=tree[:, 0, :], in1=tree[:, dj, :], op=ALU.max
                     )
-                tree = single.tile([P, 4, HALF], F32)
-                nc.vector.tensor_tensor(out=tree[:], in0=z[:, 0:4, :], in1=z[:, 4:8, :], op=ALU.max)
-                nc.vector.tensor_tensor(
-                    out=tree[:, 0:2, :], in0=tree[:, 0:2, :], in1=tree[:, 2:4, :], op=ALU.max
-                )
-                nc.vector.tensor_tensor(
-                    out=tree[:, 0, :], in0=tree[:, 0, :], in1=tree[:, 1, :], op=ALU.max
-                )
-                z_max = tree[:, 1:2, :]
-                nc.vector.tensor_tensor(
-                    out=z_max, in0=tree[:, 0:1, :], in1=z[:, 8:9, :], op=ALU.max
-                )
-                neg_max = work.tile([P, HALF], F32)
-                nc.scalar.mul(out=neg_max[:], in_=tree[:, 1, :], mul=-1.0)
-                nc.vector.tensor_tensor(
-                    out=z[:, 0:VECTOR_SHIFTS, :],
-                    in0=z[:, 0:VECTOR_SHIFTS, :],
-                    in1=z_max.to_broadcast([P, VECTOR_SHIFTS, HALF]),
-                    op=ALU.subtract,
-                )
-                return z, neg_max
-
-            def weights(z, neg_max):
-                e_tiles = []
                 e_sum = sum_psum.tile([P, HALF], F32)
-                for d in range(N_OFF + 1):
-                    if d < N_OFF:
-                        shifted = turn_psum.tile([P, BLOCKS, P], F32)
-                        for blk in range(BLOCKS):
-                            cols = slice(blk * P, (blk + 1) * P)
-                            alone = d < VECTOR_SHIFTS
-                            add_transposed(
-                                nc, shifted[:, blk, :], z[:, d, cols], ident_f32[:], True, alone
-                            )
-                            if not alone:
-                                add_transposed(
-                                    nc, shifted[:, blk, :], neg_max[:, cols], ident_f32[:],
-                                    False, True,
-                                )
-                        e_t = e_pool.tile([P, BLOCKS, P], F32)
-                        nc.scalar.activation(out=e_t[:], in_=shifted[:], func=ACT.Exp)
-                        e_tiles.append(e_t)
-                    if d >= 1:
-                        for blk in range(BLOCKS):
-                            add_transposed(
-                                nc, e_sum[:, blk * P : (blk + 1) * P], e_tiles[d - 1][:, blk, :],
-                                ident_f32[:],
-                                d - 1 == 0 and blk == 0,
-                                d - 1 == N_OFF - 1 and blk == BLOCKS - 1,
-                            )
+                ev_sum = sum_psum.tile([P, HALF], F32)
+                for di in range(KS):
+                    nc.vector.tensor_tensor(
+                        out=z[:, di],
+                        in0=z[:, di],
+                        in1=tree[:, 0:1, :].to_broadcast([P, KS, HALF]),
+                        op=ALU.subtract,
+                    )
+                    nc.scalar.activation(out=z[:, di], in_=z[:, di], func=ACT.Exp)
+                for di in range(KS):
+                    add_over_window(e_sum, z[:, di], di)
+                    prod = prod_pool.tile([P, KS, HALF], F32)
+                    for dj in range(KS):
+                        nc.vector.tensor_tensor(
+                            out=prod[:, dj, :].rearrange("p (r w) -> p r w", w=W2),
+                            in0=z[:, di, dj, :].rearrange("p (r w) -> p r w", w=W2),
+                            in1=v_ring[:, b % SETS, top + di : top + di + HALF_ROWS, dj : dj + W2],
+                            op=ALU.mult,
+                        )
+                    add_over_window(ev_sum, prod, di)
+                return e_sum, ev_sum
+
+            def finish(half, e_sum, ev_sum):
                 log_sum = single.tile([P, HALF], F32)
                 nc.scalar.activation(out=log_sum[:], in_=e_sum[:], func=ACT.Ln)
                 inv_sum = work.tile([P, HALF], F32)
                 nc.scalar.activation(out=inv_sum[:], in_=log_sum[:], func=ACT.Exp, scale=-1.0)
-                return e_tiles, inv_sum
-
-            def mix(half, e_tiles, inv_sum):
-                b, h = divmod(half, 2)
-                top = h * HALF_ROWS
-                ev_sum = sum_psum.tile([P, HALF], F32)
-                prods = []
-                for d in range(N_OFF + 1):
-                    if d < N_OFF:
-                        di, dj = OFFSETS[d]
-                        v_t = turn_psum.tile([P, BLOCKS, P], F32)
-                        for blk in range(BLOCKS):
-                            row = top + blk * BLOCK_ROWS + di
-                            nc.tensor.transpose(
-                                v_t[:, blk, :],
-                                v_moved[:, b % SETS, dj, row : row + BLOCK_ROWS, :].rearrange(
-                                    "p r w -> p (r w)"
-                                ),
-                                ident_f32[:],
-                            )
-                        prod = prod_pool.tile([P, BLOCKS, P], F32)
-                        nc.vector.tensor_tensor(
-                            out=prod[:], in0=e_tiles[d][:], in1=v_t[:], op=ALU.mult
-                        )
-                        prods.append(prod)
-                    if d >= 1:
-                        for blk in range(BLOCKS):
-                            add_transposed(
-                                nc, ev_sum[:, blk * P : (blk + 1) * P], prods[d - 1][:, blk, :],
-                                ident_f32[:],
-                                d - 1 == 0 and blk == 0,
-                                d - 1 == N_OFF - 1 and blk == BLOCKS - 1,
-                            )
+                att_turned = work.tile([P, HALF], F32)
                 nc.vector.tensor_tensor(
-                    out=att[:, half, :], in0=ev_sum[:], in1=inv_sum[:], op=ALU.mult
+                    out=att_turned[:], in0=ev_sum[:], in1=inv_sum[:], op=ALU.mult
                 )
+                att_back = turn_psum.tile([P, HALF], F32)
+                for blk in range(BLOCKS):
+                    cols = slice(blk * P, (blk + 1) * P)
+                    nc.tensor.transpose(att_back[:, cols], att_turned[:, cols], ident_f32[:])
+                nc.scalar.copy(out=att[:, half, :], in_=att_back[:])
                 nc.vector.bn_stats(out=stats[:, half, :], in_=att[:, half, :])
 
-            for step in range(N_HALVES + LEAD):
+            for step in range(N_HALVES + LEAD + 1):
                 t = step - LEAD
                 if 1 <= step <= N_HALVES:
                     project(step - 1, y_grouped)
-                if 0 <= t:
-                    e_tiles, inv_sum = weights(z, neg_max)
-                if 1 <= step < N_HALVES:
+                if 0 <= t < N_HALVES:
+                    sums = attend(t)
+                if len(ll_first) <= step < N_HALVES:
                     ll_grouped = haar(step)
+                elif step < len(ll_first):
+                    ll_grouped = ll_first[step]
                 if step < N_HALVES:
                     y_grouped = first_convolution(ll_grouped)
-                if 0 <= t + 1 < N_HALVES:
-                    z, neg_max = scores(t + 1)
-                if 0 <= t:
-                    mix(t, e_tiles, inv_sum)
+                if 1 <= t:
+                    finish(t - 1, e_sum, ev_sum)
+                if 0 <= t < N_HALVES:
+                    e_sum, ev_sum = sums
 
         last = whole.enter_context(tc.tile_pool(name="last", bufs=2, reuse_waits="tile"))
         mean_var = last.tile([P, 2], F32)

@@ -28,7 +28,7 @@ PIECE = PIECE_ROWS * W2
 BLOCKS = HALF // P
 KS = 3
 SETS = 2
-LEAD = 2
+LEAD = 3
 TAPS = [(a, c) for a in range(2) for c in range(2)]
 HALF_ON_TENSOR = 1
 
@@ -58,10 +58,13 @@ def tile_merge_pa_t_kernel(
         bias = keep.tile([P, M_TILES], F32)
 
         q_sets = keep.tile([P, SETS, H2 * W2], F32)
-        k_ring = keep.tile([P, SETS, H2 + 2, W2 + 2], F32)
-        v_ring = keep.tile([P, SETS, H2 + 2, W2 + 2], F32)
-        nc.gpsimd.memset(k_ring[:], 0.0)
-        nc.gpsimd.memset(v_ring[:], 0.0)
+        k_moved = keep.tile([P, SETS, KS, H2 + 2, W2], F32)
+        v_moved = keep.tile([P, SETS, KS, H2 + 2, W2], F32)
+        for moved in (k_moved, v_moved):
+            nc.gpsimd.memset(moved[:, :, :, 0, :], 0.0)
+            nc.gpsimd.memset(moved[:, :, :, H2 + 1, :], 0.0)
+            nc.gpsimd.memset(moved[:, :, 0, :, 0:8], 0.0)
+            nc.gpsimd.memset(moved[:, :, KS - 1, :, W2 - 8 : W2], 0.0)
 
         att = keep.tile([P, N_HALVES, HALF], F32)
         stats = keep.tile([P, N_HALVES, 6], F32)
@@ -218,13 +221,14 @@ def tile_merge_pa_t_kernel(
                             out=q_sets[:, b % SETS, h * HALF : (h + 1) * HALF],
                             in_=proj[:].rearrange("p r w -> p (r w)"),
                         )
-                    elif s == 1:
-                        nc.scalar.copy(out=k_ring[:, b % SETS, rows, 1 : W2 + 1], in_=proj[:])
                     else:
-                        nc.scalar.copy(out=v_ring[:, b % SETS, rows, 1 : W2 + 1], in_=proj[:])
+                        planes = (k_moved if s == 1 else v_moved)[:, b % SETS]
+                        nc.scalar.copy(out=planes[:, 0, rows, 1:W2], in_=proj[:, :, 0 : W2 - 1])
+                        nc.scalar.copy(out=planes[:, 1, rows, :], in_=proj[:])
+                        nc.scalar.copy(out=planes[:, 2, rows, 0 : W2 - 1], in_=proj[:, :, 1:W2])
 
             with tc.tile_pool(name="stage", bufs=1) as stage, tc.tile_pool(
-                name="early", bufs=3
+                name="early", bufs=2
             ) as early:
                 w1_rows = stage.tile([P, M_TILES, C], BF16)
                 nc.scalar.dma_start(
@@ -292,23 +296,29 @@ def tile_merge_pa_t_kernel(
                             di == KS - 1 and dj == KS - 1 and blk == BLOCKS - 1,
                         )
 
-            def attend(half):
+            def window_row(moved, half, di):
                 b, h = divmod(half, 2)
-                top = h * HALF_ROWS
-                q_half = q_sets[:, b % SETS, h * HALF : (h + 1) * HALF].rearrange(
-                    "p (r w) -> p r w", w=W2
+                top = h * HALF_ROWS + di
+                return moved[:, b % SETS, :, top : top + HALF_ROWS, :].rearrange(
+                    "p c r w -> p c (r w)"
                 )
+
+            def scores(half):
+                b, h = divmod(half, 2)
+                q_half = q_sets[:, b % SETS, h * HALF : (h + 1) * HALF]
                 z = z_pool.tile([P, KS, KS, HALF], F32)
                 z_rough = single.tile([P, KS, KS, HALF], BF16)
                 for di in range(KS):
-                    for dj in range(KS):
-                        nc.vector.tensor_tensor(
-                            out=z[:, di, dj, :].rearrange("p (r w) -> p r w", w=W2),
-                            in0=q_half,
-                            in1=k_ring[:, b % SETS, top + di : top + di + HALF_ROWS, dj : dj + W2],
-                            op=ALU.mult,
-                        )
+                    nc.vector.tensor_tensor(
+                        out=z[:, di],
+                        in0=q_half.unsqueeze(1).to_broadcast([P, KS, HALF]),
+                        in1=window_row(k_moved, half, di),
+                        op=ALU.mult,
+                    )
                     nc.scalar.copy(out=z_rough[:, di], in_=z[:, di])
+                return z, z_rough
+
+            def weights(z, z_rough):
                 tree = single.tile([P, KS, HALF], BF16)
                 nc.vector.tensor_tensor(
                     out=tree[:], in0=z_rough[:, 0], in1=z_rough[:, 1], op=ALU.max
@@ -318,42 +328,40 @@ def tile_merge_pa_t_kernel(
                     nc.vector.tensor_tensor(
                         out=tree[:, 0, :], in0=tree[:, 0, :], in1=tree[:, dj, :], op=ALU.max
                     )
+                z_all = z[:].rearrange("p a c x -> p (a c) x")
+                nc.vector.tensor_tensor(
+                    out=z_all,
+                    in0=z_all,
+                    in1=tree[:, 0:1, :].to_broadcast([P, KS * KS, HALF]),
+                    op=ALU.subtract,
+                )
                 e_sum = sum_psum.tile([P, HALF], F32)
+                for di in range(KS):
+                    nc.scalar.activation(out=z[:, di], in_=z[:, di], func=ACT.Exp)
+                    add_over_window(e_sum, z[:, di], di)
+                return e_sum
+
+            def mix(half, e):
                 ev_sum = sum_psum.tile([P, HALF], F32)
                 for di in range(KS):
-                    nc.vector.tensor_tensor(
-                        out=z[:, di],
-                        in0=z[:, di],
-                        in1=tree[:, 0:1, :].to_broadcast([P, KS, HALF]),
-                        op=ALU.subtract,
-                    )
-                    nc.scalar.activation(out=z[:, di], in_=z[:, di], func=ACT.Exp)
-                for di in range(KS):
-                    add_over_window(e_sum, z[:, di], di)
                     prod = prod_pool.tile([P, KS, HALF], F32)
-                    for dj in range(KS):
-                        nc.vector.tensor_tensor(
-                            out=prod[:, dj, :].rearrange("p (r w) -> p r w", w=W2),
-                            in0=z[:, di, dj, :].rearrange("p (r w) -> p r w", w=W2),
-                            in1=v_ring[:, b % SETS, top + di : top + di + HALF_ROWS, dj : dj + W2],
-                            op=ALU.mult,
-                        )
+                    nc.vector.tensor_tensor(
+                        out=prod[:], in0=e[:, di], in1=window_row(v_moved, half, di), op=ALU.mult
+                    )
                     add_over_window(ev_sum, prod, di)
-                return e_sum, ev_sum
+                return ev_sum
 
             def finish(half, e_sum, ev_sum):
-                log_sum = single.tile([P, HALF], F32)
-                nc.scalar.activation(out=log_sum[:], in_=e_sum[:], func=ACT.Ln)
-                inv_sum = work.tile([P, HALF], F32)
-                nc.scalar.activation(out=inv_sum[:], in_=log_sum[:], func=ACT.Exp, scale=-1.0)
-                att_turned = work.tile([P, HALF], F32)
+                quotient = work.tile([P, HALF], F32)
+                nc.scalar.activation(out=quotient[:], in_=e_sum[:], func=ACT.Ln)
+                nc.scalar.activation(out=quotient[:], in_=quotient[:], func=ACT.Exp, scale=-1.0)
                 nc.vector.tensor_tensor(
-                    out=att_turned[:], in0=ev_sum[:], in1=inv_sum[:], op=ALU.mult
+                    out=quotient[:], in0=ev_sum[:], in1=quotient[:], op=ALU.mult
                 )
                 att_back = turn_psum.tile([P, HALF], F32)
                 for blk in range(BLOCKS):
                     cols = slice(blk * P, (blk + 1) * P)
-                    nc.tensor.transpose(att_back[:, cols], att_turned[:, cols], ident_f32[:])
+                    nc.tensor.transpose(att_back[:, cols], quotient[:, cols], ident_f32[:])
                 nc.scalar.copy(out=att[:, half, :], in_=att_back[:])
                 nc.vector.bn_stats(out=stats[:, half, :], in_=att[:, half, :])
 
@@ -362,17 +370,19 @@ def tile_merge_pa_t_kernel(
                 if 1 <= step <= N_HALVES:
                     project(step - 1, y_grouped)
                 if 0 <= t < N_HALVES:
-                    sums = attend(t)
+                    e, e_sum = z, weights(z, z_rough)
+                if 0 <= t + 1 < N_HALVES:
+                    z, z_rough = scores(t + 1)
+                if 1 <= t:
+                    finish(t - 1, sums[0], sums[1])
+                if 0 <= t < N_HALVES:
+                    sums = (e_sum, mix(t, e))
                 if len(ll_first) <= step < N_HALVES:
                     ll_grouped = haar(step)
                 elif step < len(ll_first):
                     ll_grouped = ll_first[step]
                 if step < N_HALVES:
                     y_grouped = first_convolution(ll_grouped)
-                if 1 <= t:
-                    finish(t - 1, e_sum, ev_sum)
-                if 0 <= t < N_HALVES:
-                    e_sum, ev_sum = sums
 
         last = whole.enter_context(tc.tile_pool(name="last", bufs=2, reuse_waits="tile"))
         mean_var = last.tile([P, 2], F32)

@@ -29,6 +29,7 @@ BLOCKS = HALF // P
 KS = 3
 SETS = 2
 LEAD = 3
+RUN = 4
 TAPS = [(a, c) for a in range(2) for c in range(2)]
 HALF_ON_TENSOR = 1
 
@@ -100,7 +101,7 @@ def tile_merge_pa_t_kernel(
                 b, h = divmod(half, 2)
                 ll_grouped = work.tile([P, C_PASSES, HALF, PACK], BF16, align_bytes=64)
                 pieces = [(g, s) for g in range(C_PASSES) for s in range(HALF // PIECE)]
-                row_sums = []
+                col_sums = []
                 for i in range(len(pieces) + 1):
                     if i < len(pieces):
                         g, s = pieces[i]
@@ -112,21 +113,27 @@ def tile_merge_pa_t_kernel(
                                 b, g * K_PASS : (g + 1) * K_PASS, row : row + 2 * PIECE_ROWS, :
                             ].rearrange("(p j) r w -> p j (r w)", j=PACK),
                         )
-                        rows = x_piece[:].rearrange("p j (r two w) -> p (j r) two w", two=2, w=W)
-                        row_sum = work.tile([P, PACK * PIECE_ROWS, W], F32)
-                        nc.vector.tensor_tensor(
-                            out=row_sum[:], in0=rows[:, :, 0, :], in1=rows[:, :, 1, :], op=ALU.add
+                        pixels = x_piece[:].rearrange(
+                            "p j (r a w c) -> p j r a w c", a=2, w=W2, c=2
                         )
-                        row_sums.append(row_sum)
+                        col_sum = work.tile([P, 2, PACK, PIECE], F32)
+                        for a in range(2):
+                            nc.vector.tensor_tensor(
+                                out=col_sum[:, a].rearrange("p j (r w) -> p j r w", w=W2),
+                                in0=pixels[:, :, :, a, :, 0],
+                                in1=pixels[:, :, :, a, :, 1],
+                                op=ALU.add,
+                            )
+                        col_sums.append(col_sum)
                     if i >= 1:
                         g, s = pieces[i - 1]
-                        pairs = row_sums[i - 1][:].rearrange(
-                            "p (j r) (w two) -> p j (r w) two", j=PACK, two=2
-                        )
+                        planes = col_sums[i - 1][:].rearrange("p a j (n i) -> p a n j i", i=RUN)
                         nc.vector.tensor_tensor(
-                            out=ll_grouped[:, g, s * PIECE : (s + 1) * PIECE, :],
-                            in0=pairs[:, :, :, 0].rearrange("p j x -> p x j"),
-                            in1=pairs[:, :, :, 1].rearrange("p j x -> p x j"),
+                            out=ll_grouped[:, g, s * PIECE : (s + 1) * PIECE, :].rearrange(
+                                "p (n i) j -> p n j i", i=RUN
+                            ),
+                            in0=planes[:, 0],
+                            in1=planes[:, 1],
                             op=ALU.add,
                         )
                 return ll_grouped

@@ -327,21 +327,31 @@ def tile_merge_pa_t_kernel(
 
             def weights(z, z_rough):
                 tree = single.tile([P, KS, HALF], BF16)
-                nc.vector.tensor_tensor(
-                    out=tree[:], in0=z_rough[:, 0], in1=z_rough[:, 1], op=ALU.max
-                )
-                nc.vector.tensor_tensor(out=tree[:], in0=tree[:], in1=z_rough[:, 2], op=ALU.max)
-                for dj in range(1, KS):
+                sides = (slice(0, HALF // 2), slice(HALF // 2, HALF))
+                for side in sides:
                     nc.vector.tensor_tensor(
-                        out=tree[:, 0, :], in0=tree[:, 0, :], in1=tree[:, dj, :], op=ALU.max
+                        out=tree[:, :, side], in0=z_rough[:, 0, :, side],
+                        in1=z_rough[:, 1, :, side], op=ALU.max,
                     )
+                for side in sides:
+                    nc.vector.tensor_tensor(
+                        out=tree[:, :, side], in0=tree[:, :, side], in1=z_rough[:, 2, :, side],
+                        op=ALU.max,
+                    )
+                for dj in range(1, KS):
+                    for side in sides:
+                        nc.vector.tensor_tensor(
+                            out=tree[:, 0, side], in0=tree[:, 0, side], in1=tree[:, dj, side],
+                            op=ALU.max,
+                        )
                 z_all = z[:].rearrange("p a c x -> p (a c) x")
-                nc.vector.tensor_tensor(
-                    out=z_all,
-                    in0=z_all,
-                    in1=tree[:, 0:1, :].to_broadcast([P, KS * KS, HALF]),
-                    op=ALU.subtract,
-                )
+                for side in sides:
+                    nc.vector.tensor_tensor(
+                        out=z_all[:, :, side],
+                        in0=z_all[:, :, side],
+                        in1=tree[:, 0:1, side].to_broadcast([P, KS * KS, HALF // 2]),
+                        op=ALU.subtract,
+                    )
                 e_sum = sum_psum.tile([P, HALF], F32)
                 for di in range(KS):
                     nc.scalar.activation(out=z[:, di], in_=z[:, di], func=ACT.Exp)

@@ -32,6 +32,11 @@ LEAD = 3
 RUN = 4
 TAPS = [(a, c) for a in range(2) for c in range(2)]
 HALF_ON_TENSOR = 1
+PINNED = (
+    mybir.EngineType.DVE, mybir.EngineType.Pool, mybir.EngineType.Activation, mybir.EngineType.PE,
+)
+PINNED_FROM = 2
+FIRST_ON_GPSIMD = 3
 
 FLOPS = 2 * B * H2 * W2 * (M * C + 3 * O * M)
 
@@ -58,7 +63,6 @@ def tile_merge_pa_t_kernel(
         wqkv_scales = keep.tile([P, 3, O], U8, align_bytes=64)
         bias = keep.tile([P, M_TILES], F32)
 
-        q_sets = keep.tile([P, SETS, H2 * W2], F32)
         k_moved = keep.tile([P, SETS, KS, H2 + 2, W2], F32)
         v_moved = keep.tile([P, SETS, KS, H2 + 2, W2], F32)
         for moved in (k_moved, v_moved):
@@ -93,84 +97,84 @@ def tile_merge_pa_t_kernel(
 
         with ExitStack() as stream:
             x_pool = stream.enter_context(tc.tile_pool(name="x_pool", bufs=3))
+            col_pool = stream.enter_context(tc.tile_pool(name="col_pool", bufs=4))
             work = stream.enter_context(tc.tile_pool(name="work", bufs=2))
             single = stream.enter_context(tc.tile_pool(name="single", bufs=1))
             mx_psum = stream.enter_context(tc.psum_pool(name="mx_psum", bufs=2))
+            pieces = [(g, s) for g in range(C_PASSES) for s in range(HALF // PIECE)]
 
-            def haar(half):
+            def load_piece(pool, half, g, s):
                 b, h = divmod(half, 2)
-                ll_grouped = work.tile([P, C_PASSES, HALF, PACK], BF16, align_bytes=64)
-                pieces = [(g, s) for g in range(C_PASSES) for s in range(HALF // PIECE)]
+                row = 2 * (h * HALF_ROWS + s * PIECE_ROWS)
+                x_piece = pool.tile([P, PACK, 2 * PIECE_ROWS * W], BF16)
+                nc.sync.dma_start(
+                    out=x_piece[:],
+                    in_=x[
+                        b, g * K_PASS : (g + 1) * K_PASS, row : row + 2 * PIECE_ROWS, :
+                    ].rearrange("(p j) r w -> p j (r w)", j=PACK),
+                )
+                return x_piece[:].rearrange("p j (r a w c) -> p j r a w c", a=2, w=W2, c=2)
+
+            def add_columns(half, g, s):
+                pixels = load_piece(x_pool, half, g, s)
+                col_sum = col_pool.tile([P, 2, PACK, PIECE], F32)
+                for a in range(2):
+                    nc.vector.tensor_tensor(
+                        out=col_sum[:, a].rearrange("p j (r w) -> p j r w", w=W2),
+                        in0=pixels[:, :, :, a, :, 0],
+                        in1=pixels[:, :, :, a, :, 1],
+                        op=ALU.add,
+                    )
+                return col_sum
+
+            def add_rows_on_vector(ll_grouped, g, s, col_sum):
+                planes = col_sum[:].rearrange("p a j (n i) -> p a n j i", i=RUN)
+                nc.vector.tensor_tensor(
+                    out=ll_grouped[:, g, s * PIECE : (s + 1) * PIECE, :].rearrange(
+                        "p (n i) j -> p n j i", i=RUN
+                    ),
+                    in0=planes[:, 0],
+                    in1=planes[:, 1],
+                    op=ALU.add,
+                )
+
+            def add_rows_on_gpsimd(ll_grouped, g, s, col_sum):
+                planes = col_sum[:].rearrange("p a j x -> p a x j")
+                nc.gpsimd.tensor_tensor(
+                    out=ll_grouped[:, g, s * PIECE : (s + 1) * PIECE, :],
+                    in0=planes[:, 0],
+                    in1=planes[:, 1],
+                    op=ALU.add,
+                )
+
+            def haar_on_vector(ll_grouped, half, some_pieces):
                 col_sums = []
-                for i in range(len(pieces) + 1):
-                    if i < len(pieces):
-                        g, s = pieces[i]
-                        row = 2 * (h * HALF_ROWS + s * PIECE_ROWS)
-                        x_piece = x_pool.tile([P, PACK, 2 * PIECE_ROWS * W], BF16)
-                        nc.sync.dma_start(
-                            out=x_piece[:],
-                            in_=x[
-                                b, g * K_PASS : (g + 1) * K_PASS, row : row + 2 * PIECE_ROWS, :
-                            ].rearrange("(p j) r w -> p j (r w)", j=PACK),
-                        )
-                        pixels = x_piece[:].rearrange(
-                            "p j (r a w c) -> p j r a w c", a=2, w=W2, c=2
-                        )
-                        col_sum = work.tile([P, 2, PACK, PIECE], F32)
-                        for a in range(2):
-                            nc.vector.tensor_tensor(
-                                out=col_sum[:, a].rearrange("p j (r w) -> p j r w", w=W2),
-                                in0=pixels[:, :, :, a, :, 0],
-                                in1=pixels[:, :, :, a, :, 1],
-                                op=ALU.add,
-                            )
-                        col_sums.append(col_sum)
+                for i in range(len(some_pieces) + 1):
+                    if i < len(some_pieces):
+                        col_sums.append(add_columns(half, some_pieces[i][0], some_pieces[i][1]))
                     if i >= 1:
-                        g, s = pieces[i - 1]
-                        planes = col_sums[i - 1][:].rearrange("p a j (n i) -> p a n j i", i=RUN)
-                        nc.vector.tensor_tensor(
-                            out=ll_grouped[:, g, s * PIECE : (s + 1) * PIECE, :].rearrange(
-                                "p (n i) j -> p n j i", i=RUN
-                            ),
-                            in0=planes[:, 0],
-                            in1=planes[:, 1],
-                            op=ALU.add,
+                        add_rows_on_vector(
+                            ll_grouped, some_pieces[i - 1][0], some_pieces[i - 1][1],
+                            col_sums[i - 1],
                         )
-                return ll_grouped
 
-            def haar_by_matmul(half, early):
-                b, h = divmod(half, 2)
-                ll_grouped = work.tile([P, C_PASSES, HALF, PACK], BF16, align_bytes=64)
-                for g in range(C_PASSES):
-                    for s in range(HALF // PIECE):
-                        row = 2 * (h * HALF_ROWS + s * PIECE_ROWS)
-                        x_early = early.tile([P, PACK, 2 * PIECE_ROWS * W], BF16)
-                        nc.sync.dma_start(
-                            out=x_early[:],
-                            in_=x[
-                                b, g * K_PASS : (g + 1) * K_PASS, row : row + 2 * PIECE_ROWS, :
-                            ].rearrange("(p j) r w -> p j (r w)", j=PACK),
-                        )
-                        pixels = x_early[:].rearrange(
-                            "p j (r a w c) -> p j r a w c", a=2, w=W2, c=2
-                        )
-                        for first in range(0, PACK, 2):
-                            total = mx_psum.tile([P, 2, PIECE_ROWS, W2], F32, tag="mx")
-                            for tap, (a, c) in enumerate(TAPS):
-                                nc.tensor.matmul(
-                                    out=total[:],
-                                    lhsT=ident_bf16[:],
-                                    rhs=pixels[:, first : first + 2, :, a, :, c],
-                                    start=(tap == 0),
-                                    stop=(tap == len(TAPS) - 1),
-                                )
-                            nc.scalar.copy(
-                                out=ll_grouped[
-                                    :, g, s * PIECE : (s + 1) * PIECE, first : first + 2
-                                ],
-                                in_=total[:].rearrange("p j r w -> p (r w) j"),
+            def haar_by_matmul(ll_grouped, half, some_pieces, early):
+                for g, s in some_pieces:
+                    pixels = load_piece(early, half, g, s)
+                    for first in range(0, PACK, 2):
+                        total = mx_psum.tile([P, 2, PIECE_ROWS, W2], F32, tag="mx")
+                        for tap, (a, c) in enumerate(TAPS):
+                            nc.tensor.matmul(
+                                out=total[:],
+                                lhsT=ident_bf16[:],
+                                rhs=pixels[:, first : first + 2, :, a, :, c],
+                                start=(tap == 0),
+                                stop=(tap == len(TAPS) - 1),
                             )
-                return ll_grouped
+                        nc.scalar.copy(
+                            out=ll_grouped[:, g, s * PIECE : (s + 1) * PIECE, first : first + 2],
+                            in_=total[:].rearrange("p j r w -> p (r w) j"),
+                        )
 
             def first_convolution(ll_grouped):
                 ll_codes = work.tile([P, C_PASSES, HALF], U32, align_bytes=64)
@@ -202,6 +206,19 @@ def tile_merge_pa_t_kernel(
                 nc.scalar.copy(out=y_grouped[:], in_=y_rows[:].rearrange("p t x -> p x t"))
                 return y_grouped
 
+            def projection(s, y_quantised):
+                proj = mx_psum.tile([P, HALF_ROWS, W2], F32, tag="mx")
+                nc.tensor.matmul_mx(
+                    out=proj[:].rearrange("p r w -> p (r w)"),
+                    lhsT=wqkv_codes[:, s, :].bitcast(FP8X4),
+                    lhsT_scale=wqkv_scales[:, s, :],
+                    rhs=y_quantised[0][:].bitcast(FP8X4),
+                    rhs_scale=y_quantised[1][:],
+                    start=True,
+                    stop=True,
+                )
+                return proj
+
             def project(half, y_grouped):
                 b, h = divmod(half, 2)
                 rows = slice(1 + h * HALF_ROWS, 1 + (h + 1) * HALF_ROWS)
@@ -212,28 +229,15 @@ def tile_merge_pa_t_kernel(
                     scales=y_scales[:],
                     in_=y_grouped[:].rearrange("p x t -> p (x t)"),
                 )
-                for s in range(3):
-                    proj = mx_psum.tile([P, HALF_ROWS, W2], F32, tag="mx")
-                    nc.tensor.matmul_mx(
-                        out=proj[:].rearrange("p r w -> p (r w)"),
-                        lhsT=wqkv_codes[:, s, :].bitcast(FP8X4),
-                        lhsT_scale=wqkv_scales[:, s, :],
-                        rhs=y_codes[:].bitcast(FP8X4),
-                        rhs_scale=y_scales[:],
-                        start=True,
-                        stop=True,
-                    )
-                    if s == 0:
-                        nc.scalar.copy(
-                            out=q_sets[:, b % SETS, h * HALF : (h + 1) * HALF],
-                            in_=proj[:].rearrange("p r w -> p (r w)"),
-                        )
-                    else:
-                        planes = (k_moved if s == 1 else v_moved)[:, b % SETS]
-                        nc.scalar.copy(out=planes[:, 0, rows, 1:W2], in_=proj[:, :, 0 : W2 - 1])
-                        nc.scalar.copy(out=planes[:, 1, rows, :], in_=proj[:])
-                        nc.scalar.copy(out=planes[:, 2, rows, 0 : W2 - 1], in_=proj[:, :, 1:W2])
+                for s in (1, 2):
+                    proj = projection(s, (y_codes, y_scales))
+                    planes = (k_moved if s == 1 else v_moved)[:, b % SETS]
+                    nc.scalar.copy(out=planes[:, 0, rows, 1:W2], in_=proj[:, :, 0 : W2 - 1])
+                    nc.scalar.copy(out=planes[:, 1, rows, :], in_=proj[:])
+                    nc.scalar.copy(out=planes[:, 2, rows, 0 : W2 - 1], in_=proj[:, :, 1:W2])
+                return y_codes, y_scales
 
+            ll_tiles = {}
             with tc.tile_pool(name="stage", bufs=1) as stage, tc.tile_pool(
                 name="early", bufs=2
             ) as early:
@@ -272,7 +276,12 @@ def tile_merge_pa_t_kernel(
                     nc.scalar.copy(
                         out=wqkv_grouped[:, s], in_=turned[:].rearrange("p j o -> p o j")
                     )
-                ll_first = [haar(0), haar_by_matmul(HALF_ON_TENSOR, early)]
+                for half in range(2):
+                    ll_grouped = work.tile([P, C_PASSES, HALF, PACK], BF16, align_bytes=64)
+                    ll_tiles[half] = ll_grouped
+                haar_on_vector(ll_tiles[0], 0, pieces)
+                haar_by_matmul(ll_tiles[HALF_ON_TENSOR], HALF_ON_TENSOR, pieces[:-1], early)
+                haar_on_vector(ll_tiles[HALF_ON_TENSOR], HALF_ON_TENSOR, pieces[-1:])
                 for g in range(C_PASSES):
                     nc.vector.quantize_mx(
                         out=w1_codes[:, g, :].bitcast(FP8X4),
@@ -290,8 +299,10 @@ def tile_merge_pa_t_kernel(
             prod_pool = stream.enter_context(
                 tc.tile_pool(name="prod_pool", bufs=3, reuse_waits="tile")
             )
-            sum_psum = stream.enter_context(tc.psum_pool(name="sum_psum", bufs=2))
+            sum_psum = stream.enter_context(tc.psum_pool(name="sum_psum", bufs=1))
             turn_psum = stream.enter_context(tc.psum_pool(name="turn_psum", bufs=1))
+            max_psum = stream.enter_context(tc.psum_pool(name="max_psum", bufs=1))
+            sides = (slice(0, HALF // 2), slice(HALF // 2, HALF))
 
             def add_over_window(total, terms, di):
                 for dj in range(KS):
@@ -310,11 +321,11 @@ def tile_merge_pa_t_kernel(
                     "p c r w -> p c (r w)"
                 )
 
-            def scores(half):
-                b, h = divmod(half, 2)
-                q_half = q_sets[:, b % SETS, h * HALF : (h + 1) * HALF]
+            def query(y_quantised):
+                return projection(0, y_quantised)[:].rearrange("p r w -> p (r w)")
+
+            def scores(half, q_half):
                 z = z_pool.tile([P, KS, KS, HALF], F32)
-                z_rough = single.tile([P, KS, KS, HALF], BF16)
                 for di in range(KS):
                     nc.vector.tensor_tensor(
                         out=z[:, di],
@@ -322,12 +333,16 @@ def tile_merge_pa_t_kernel(
                         in1=window_row(k_moved, half, di),
                         op=ALU.mult,
                     )
-                    nc.scalar.copy(out=z_rough[:, di], in_=z[:, di])
-                return z, z_rough
+                return z
 
-            def weights(z, z_rough):
+            def round_scores(z):
+                z_rough = single.tile([P, KS, KS, HALF], BF16)
+                for di in range(KS):
+                    nc.scalar.copy(out=z_rough[:, di], in_=z[:, di])
+                return z_rough
+
+            def maximum(z_rough):
                 tree = single.tile([P, KS, HALF], BF16)
-                sides = (slice(0, HALF // 2), slice(HALF // 2, HALF))
                 for side in sides:
                     nc.vector.tensor_tensor(
                         out=tree[:, :, side], in0=z_rough[:, 0, :, side],
@@ -344,19 +359,25 @@ def tile_merge_pa_t_kernel(
                             out=tree[:, 0, side], in0=tree[:, 0, side], in1=tree[:, dj, side],
                             op=ALU.max,
                         )
+                z_max = max_psum.tile([P, HALF], F32)
+                nc.tensor.matmul(
+                    out=z_max[:], lhsT=ident_bf16[:], rhs=tree[:, 0, :], start=True, stop=True
+                )
+                return z_max
+
+            def subtract(z, z_max):
                 z_all = z[:].rearrange("p a c x -> p (a c) x")
                 for side in sides:
                     nc.vector.tensor_tensor(
                         out=z_all[:, :, side],
                         in0=z_all[:, :, side],
-                        in1=tree[:, 0:1, side].to_broadcast([P, KS * KS, HALF // 2]),
+                        in1=z_max[:, side].unsqueeze(1).to_broadcast([P, KS * KS, HALF // 2]),
                         op=ALU.subtract,
                     )
-                e_sum = sum_psum.tile([P, HALF], F32)
-                for di in range(KS):
-                    nc.scalar.activation(out=z[:, di], in_=z[:, di], func=ACT.Exp)
-                    add_over_window(e_sum, z[:, di], di)
-                return e_sum
+
+            def exponential(z, e_sum, di):
+                nc.scalar.activation(out=z[:, di], in_=z[:, di], func=ACT.Exp)
+                add_over_window(e_sum, z[:, di], di)
 
             def mix(half, e):
                 ev_sum = sum_psum.tile([P, HALF], F32)
@@ -368,10 +389,13 @@ def tile_merge_pa_t_kernel(
                     add_over_window(ev_sum, prod, di)
                 return ev_sum
 
-            def finish(half, e_sum, ev_sum):
-                quotient = work.tile([P, HALF], F32)
+            def invert(e_sum):
+                quotient = single.tile([P, HALF], F32)
                 nc.scalar.activation(out=quotient[:], in_=e_sum[:], func=ACT.Ln)
                 nc.scalar.activation(out=quotient[:], in_=quotient[:], func=ACT.Exp, scale=-1.0)
+                return quotient
+
+            def divide(quotient, ev_sum):
                 nc.vector.tensor_tensor(
                     out=quotient[:], in0=ev_sum[:], in1=quotient[:], op=ALU.mult
                 )
@@ -379,27 +403,65 @@ def tile_merge_pa_t_kernel(
                 for blk in range(BLOCKS):
                     cols = slice(blk * P, (blk + 1) * P)
                     nc.tensor.transpose(att_back[:, cols], quotient[:, cols], ident_f32[:])
-                nc.scalar.copy(out=att[:, half, :], in_=att_back[:])
-                nc.vector.bn_stats(out=stats[:, half, :], in_=att[:, half, :])
+                return att_back
 
-            for step in range(N_HALVES + LEAD + 1):
+            halves = range(N_HALVES)
+            col_tiles, y_tiles, y_mx, z_tiles, max_tiles, ev_sums, inverses = {}, {}, {}, {}, {}, {}, {}
+
+            def one_step(step):
                 t = step - LEAD
-                if 1 <= step <= N_HALVES:
-                    project(step - 1, y_grouped)
-                if 0 <= t < N_HALVES:
-                    e, e_sum = z, weights(z, z_rough)
-                if 0 <= t + 1 < N_HALVES:
-                    z, z_rough = scores(t + 1)
-                if 1 <= t:
-                    finish(t - 1, sums[0], sums[1])
-                if 0 <= t < N_HALVES:
-                    sums = (e_sum, mix(t, e))
-                if len(ll_first) <= step < N_HALVES:
-                    ll_grouped = haar(step)
-                elif step < len(ll_first):
-                    ll_grouped = ll_first[step]
-                if step < N_HALVES:
-                    y_grouped = first_convolution(ll_grouped)
+                if t + 1 in halves:
+                    q_half = query(y_mx[t + 1])
+                if t in halves:
+                    subtract(z_tiles[t], max_tiles[t])
+                if t - 1 in halves:
+                    att_back = divide(inverses[t - 1], ev_sums[t - 1])
+                if t in halves:
+                    e_sum = sum_psum.tile([P, HALF], F32)
+                    exponential(z_tiles[t], e_sum, 0)
+                    exponential(z_tiles[t], e_sum, 1)
+                if t - 1 in halves:
+                    nc.scalar.copy(out=att[:, t - 1, :], in_=att_back[:])
+                if t in halves:
+                    exponential(z_tiles[t], e_sum, 2)
+                if t + 1 in halves:
+                    z_tiles[t + 1] = scores(t + 1, q_half)
+                if t - 1 in halves:
+                    nc.vector.bn_stats(out=stats[:, t - 1, :], in_=att[:, t - 1, :])
+                if t + 1 in halves:
+                    z_rough = round_scores(z_tiles[t + 1])
+                if step in col_tiles:
+                    ll_grouped = work.tile([P, C_PASSES, HALF, PACK], BF16, align_bytes=64)
+                    ll_tiles[step] = ll_grouped
+                    for i in reversed(range(len(pieces))):
+                        add_rows_on_gpsimd(
+                            ll_grouped, pieces[i][0], pieces[i][1], col_tiles[step][i]
+                        )
+                if t in halves:
+                    ev_sums[t] = mix(t, z_tiles[t])
+                if step in halves:
+                    y_tiles[step] = first_convolution(ll_tiles[step])
+                if t + 1 in halves:
+                    max_tiles[t + 1] = maximum(z_rough)
+                if t in halves:
+                    inverses[t] = invert(e_sum)
+                ahead = step + 1
+                if ahead in halves and ahead >= FIRST_ON_GPSIMD:
+                    col_tiles[ahead] = [add_columns(ahead, g, s) for g, s in pieces[:-1]]
+                elif ahead in halves and ahead > HALF_ON_TENSOR:
+                    ll_grouped = work.tile([P, C_PASSES, HALF, PACK], BF16, align_bytes=64)
+                    ll_tiles[ahead] = ll_grouped
+                    haar_on_vector(ll_grouped, ahead, pieces)
+                if step in halves:
+                    y_mx[step] = project(step, y_tiles[step])
+                if ahead in col_tiles:
+                    col_tiles[ahead].append(add_columns(ahead, pieces[-1][0], pieces[-1][1]))
+
+            for step in range(PINNED_FROM):
+                one_step(step)
+            with tc.manual_schedule(engines=set(PINNED)):
+                for step in range(PINNED_FROM, N_HALVES + LEAD + 1):
+                    one_step(step)
 
         last = whole.enter_context(tc.tile_pool(name="last", bufs=2, reuse_waits="tile"))
         mean_var = last.tile([P, 2], F32)

@@ -35,8 +35,8 @@ HALF_ON_TENSOR = 1
 PINNED = (
     mybir.EngineType.DVE, mybir.EngineType.Pool, mybir.EngineType.Activation, mybir.EngineType.PE,
 )
-PINNED_FROM = 2
-FIRST_ON_GPSIMD = 3
+PINNED_FROM = 3
+ROWS_ON_GPSIMD = 2
 
 FLOPS = 2 * B * H2 * W2 * (M * C + 3 * O * M)
 
@@ -72,6 +72,8 @@ def tile_merge_pa_t_kernel(
             nc.gpsimd.memset(moved[:, :, KS - 1, :, W2 - 8 : W2], 0.0)
 
         att = keep.tile([P, N_HALVES, HALF], F32)
+        warm = keep.tile([P, 1], F32)
+        nc.gpsimd.memset(warm[:], 1.0)
         stats = keep.tile([P, N_HALVES, 6], F32)
 
         bias_bf16 = keep.tile([P, M_TILES], BF16)
@@ -97,7 +99,7 @@ def tile_merge_pa_t_kernel(
 
         with ExitStack() as stream:
             x_pool = stream.enter_context(tc.tile_pool(name="x_pool", bufs=3))
-            col_pool = stream.enter_context(tc.tile_pool(name="col_pool", bufs=4))
+            col_pool = stream.enter_context(tc.tile_pool(name="col_pool", bufs=2))
             work = stream.enter_context(tc.tile_pool(name="work", bufs=2))
             single = stream.enter_context(tc.tile_pool(name="single", bufs=1))
             mx_psum = stream.enter_context(tc.psum_pool(name="mx_psum", bufs=2))
@@ -133,15 +135,6 @@ def tile_merge_pa_t_kernel(
                     out=ll_grouped[:, g, s * PIECE : (s + 1) * PIECE, :].rearrange(
                         "p (n i) j -> p n j i", i=RUN
                     ),
-                    in0=planes[:, 0],
-                    in1=planes[:, 1],
-                    op=ALU.add,
-                )
-
-            def add_rows_on_gpsimd(ll_grouped, g, s, col_sum):
-                planes = col_sum[:].rearrange("p a j x -> p a x j")
-                nc.gpsimd.tensor_tensor(
-                    out=ll_grouped[:, g, s * PIECE : (s + 1) * PIECE, :],
                     in0=planes[:, 0],
                     in1=planes[:, 1],
                     op=ALU.add,
@@ -365,29 +358,24 @@ def tile_merge_pa_t_kernel(
                 )
                 return z_max
 
-            def subtract(z, z_max):
-                z_all = z[:].rearrange("p a c x -> p (a c) x")
-                for side in sides:
-                    nc.vector.tensor_tensor(
-                        out=z_all[:, :, side],
-                        in0=z_all[:, :, side],
-                        in1=z_max[:, side].unsqueeze(1).to_broadcast([P, KS * KS, HALF // 2]),
-                        op=ALU.subtract,
-                    )
+            def subtract(z, z_max, di):
+                nc.vector.tensor_tensor(
+                    out=z[:, di],
+                    in0=z[:, di],
+                    in1=z_max[:].unsqueeze(1).to_broadcast([P, KS, HALF]),
+                    op=ALU.subtract,
+                )
 
             def exponential(z, e_sum, di):
                 nc.scalar.activation(out=z[:, di], in_=z[:, di], func=ACT.Exp)
                 add_over_window(e_sum, z[:, di], di)
 
-            def mix(half, e):
-                ev_sum = sum_psum.tile([P, HALF], F32)
-                for di in range(KS):
-                    prod = prod_pool.tile([P, KS, HALF], F32)
-                    nc.vector.tensor_tensor(
-                        out=prod[:], in0=e[:, di], in1=window_row(v_moved, half, di), op=ALU.mult
-                    )
-                    add_over_window(ev_sum, prod, di)
-                return ev_sum
+            def mix(engine, half, e, ev_sum, di):
+                prod = prod_pool.tile([P, KS, HALF], F32)
+                engine.tensor_tensor(
+                    out=prod[:], in0=e[:, di], in1=window_row(v_moved, half, di), op=ALU.mult
+                )
+                add_over_window(ev_sum, prod, di)
 
             def invert(e_sum):
                 quotient = single.tile([P, HALF], F32)
@@ -406,56 +394,53 @@ def tile_merge_pa_t_kernel(
                 return att_back
 
             halves = range(N_HALVES)
-            col_tiles, y_tiles, y_mx, z_tiles, max_tiles, ev_sums, inverses = {}, {}, {}, {}, {}, {}, {}
+            y_tiles, y_mx, z_tiles, max_tiles, ev_sums, inverses = {}, {}, {}, {}, {}, {}
 
             def one_step(step):
                 t = step - LEAD
                 if t + 1 in halves:
                     q_half = query(y_mx[t + 1])
-                if t in halves:
-                    subtract(z_tiles[t], max_tiles[t])
                 if t - 1 in halves:
                     att_back = divide(inverses[t - 1], ev_sums[t - 1])
                 if t in halves:
                     e_sum = sum_psum.tile([P, HALF], F32)
-                    exponential(z_tiles[t], e_sum, 0)
-                    exponential(z_tiles[t], e_sum, 1)
+                    ev_sum = sum_psum.tile([P, HALF], F32)
+                    ev_sums[t] = ev_sum
+                    for di in range(ROWS_ON_GPSIMD):
+                        subtract(z_tiles[t], max_tiles[t], di)
+                        exponential(z_tiles[t], e_sum, di)
                 if t - 1 in halves:
                     nc.scalar.copy(out=att[:, t - 1, :], in_=att_back[:])
                 if t in halves:
-                    exponential(z_tiles[t], e_sum, 2)
+                    for di in range(ROWS_ON_GPSIMD, KS):
+                        subtract(z_tiles[t], max_tiles[t], di)
+                        exponential(z_tiles[t], e_sum, di)
+                    for di in range(ROWS_ON_GPSIMD):
+                        mix(nc.gpsimd, t, z_tiles[t], ev_sum, di)
                 if t + 1 in halves:
                     z_tiles[t + 1] = scores(t + 1, q_half)
+                    z_rough = round_scores(z_tiles[t + 1])
                 if t - 1 in halves:
                     nc.vector.bn_stats(out=stats[:, t - 1, :], in_=att[:, t - 1, :])
-                if t + 1 in halves:
-                    z_rough = round_scores(z_tiles[t + 1])
-                if step in col_tiles:
-                    ll_grouped = work.tile([P, C_PASSES, HALF, PACK], BF16, align_bytes=64)
-                    ll_tiles[step] = ll_grouped
-                    for i in reversed(range(len(pieces))):
-                        add_rows_on_gpsimd(
-                            ll_grouped, pieces[i][0], pieces[i][1], col_tiles[step][i]
-                        )
                 if t in halves:
-                    ev_sums[t] = mix(t, z_tiles[t])
+                    for di in range(ROWS_ON_GPSIMD, KS):
+                        mix(nc.vector, t, z_tiles[t], ev_sum, di)
+                    inverses[t] = invert(e_sum)
+                if t == N_HALVES - 1:
+                    nc.scalar.sqrt(out=warm[:], in_=warm[:])
                 if step in halves:
                     y_tiles[step] = first_convolution(ll_tiles[step])
                 if t + 1 in halves:
                     max_tiles[t + 1] = maximum(z_rough)
-                if t in halves:
-                    inverses[t] = invert(e_sum)
                 ahead = step + 1
-                if ahead in halves and ahead >= FIRST_ON_GPSIMD:
-                    col_tiles[ahead] = [add_columns(ahead, g, s) for g, s in pieces[:-1]]
-                elif ahead in halves and ahead > HALF_ON_TENSOR:
+                if ahead in halves and ahead > HALF_ON_TENSOR:
                     ll_grouped = work.tile([P, C_PASSES, HALF, PACK], BF16, align_bytes=64)
                     ll_tiles[ahead] = ll_grouped
-                    haar_on_vector(ll_grouped, ahead, pieces)
+                    haar_on_vector(ll_grouped, ahead, pieces[:2])
                 if step in halves:
                     y_mx[step] = project(step, y_tiles[step])
-                if ahead in col_tiles:
-                    col_tiles[ahead].append(add_columns(ahead, pieces[-1][0], pieces[-1][1]))
+                if ahead in halves and ahead > HALF_ON_TENSOR:
+                    haar_on_vector(ll_grouped, ahead, pieces[2:])
 
             for step in range(PINNED_FROM):
                 one_step(step)

@@ -36,7 +36,7 @@ PINNED = (
     mybir.EngineType.DVE, mybir.EngineType.Pool, mybir.EngineType.Activation, mybir.EngineType.PE,
 )
 PINNED_FROM = 3
-ROWS_ON_GPSIMD = 2
+ROWS_AT_ONCE = 2
 
 FLOPS = 2 * B * H2 * W2 * (M * C + 3 * O * M)
 
@@ -293,6 +293,7 @@ def tile_merge_pa_t_kernel(
                 tc.tile_pool(name="prod_pool", bufs=3, reuse_waits="tile")
             )
             sum_psum = stream.enter_context(tc.psum_pool(name="sum_psum", bufs=1))
+            ev_psum = stream.enter_context(tc.psum_pool(name="ev_psum", bufs=2))
             turn_psum = stream.enter_context(tc.psum_pool(name="turn_psum", bufs=1))
             max_psum = stream.enter_context(tc.psum_pool(name="max_psum", bufs=1))
             sides = (slice(0, HALF // 2), slice(HALF // 2, HALF))
@@ -356,7 +357,7 @@ def tile_merge_pa_t_kernel(
                 nc.tensor.matmul(
                     out=z_max[:], lhsT=ident_bf16[:], rhs=tree[:, 0, :], start=True, stop=True
                 )
-                return z_max
+                return z_max, tree[:, 0, HALF - 1 : HALF]
 
             def subtract(z, z_max, di):
                 nc.vector.tensor_tensor(
@@ -396,42 +397,53 @@ def tile_merge_pa_t_kernel(
             halves = range(N_HALVES)
             y_tiles, y_mx, z_tiles, max_tiles, ev_sums, inverses = {}, {}, {}, {}, {}, {}
 
+            def after_vector(written):
+                if written.dtype == BF16:
+                    fence = single.tile([P, 1], BF16, name="fence_bf16")
+                else:
+                    fence = single.tile([P, 1], U32, name="fence_u32")
+                nc.gpsimd.tensor_copy(out=fence[:], in_=written)
+
+            last_written = {}
+
             def one_step(step):
                 t = step - LEAD
+                last = N_HALVES - 1
                 if t + 1 in halves:
                     q_half = query(y_mx[t + 1])
-                if t - 1 in halves:
-                    att_back = divide(inverses[t - 1], ev_sums[t - 1])
+                if t - 1 in halves and t - 1 < last:
+                    after_vector(last_written[step - 1])
+                    for di in range(ROWS_AT_ONCE, KS):
+                        mix(nc.gpsimd, t - 1, z_tiles[t - 1], ev_sums[t - 1], di)
                 if t in halves:
+                    at_once = ROWS_AT_ONCE if t < last else 1
                     e_sum = sum_psum.tile([P, HALF], F32)
-                    ev_sum = sum_psum.tile([P, HALF], F32)
+                    ev_sum = ev_psum.tile([P, HALF], F32)
                     ev_sums[t] = ev_sum
-                    for di in range(ROWS_ON_GPSIMD):
+                    for di in range(KS):
                         subtract(z_tiles[t], max_tiles[t], di)
                         exponential(z_tiles[t], e_sum, di)
-                if t - 1 in halves:
-                    nc.scalar.copy(out=att[:, t - 1, :], in_=att_back[:])
-                if t in halves:
-                    for di in range(ROWS_ON_GPSIMD, KS):
-                        subtract(z_tiles[t], max_tiles[t], di)
-                        exponential(z_tiles[t], e_sum, di)
-                    for di in range(ROWS_ON_GPSIMD):
+                    for di in range(at_once):
                         mix(nc.gpsimd, t, z_tiles[t], ev_sum, di)
                 if t + 1 in halves:
                     z_tiles[t + 1] = scores(t + 1, q_half)
                     z_rough = round_scores(z_tiles[t + 1])
                 if t - 1 in halves:
-                    nc.vector.bn_stats(out=stats[:, t - 1, :], in_=att[:, t - 1, :])
-                if t in halves:
-                    for di in range(ROWS_ON_GPSIMD, KS):
+                    att_back = divide(inverses[t - 1], ev_sums[t - 1])
+                    nc.scalar.copy(out=att[:, t - 1, :], in_=att_back[:])
+                if t == last:
+                    for di in range(at_once, KS):
                         mix(nc.vector, t, z_tiles[t], ev_sum, di)
-                    inverses[t] = invert(e_sum)
-                if t == N_HALVES - 1:
-                    nc.scalar.sqrt(out=warm[:], in_=warm[:])
                 if step in halves:
                     y_tiles[step] = first_convolution(ll_tiles[step])
                 if t + 1 in halves:
-                    max_tiles[t + 1] = maximum(z_rough)
+                    max_tiles[t + 1], last_written[step] = maximum(z_rough)
+                if t - 1 in halves:
+                    nc.vector.bn_stats(out=stats[:, t - 1, :], in_=att[:, t - 1, :])
+                if t in halves:
+                    inverses[t] = invert(e_sum)
+                if t == last:
+                    nc.scalar.sqrt(out=warm[:], in_=warm[:])
                 ahead = step + 1
                 if ahead in halves and ahead > HALF_ON_TENSOR:
                     ll_grouped = work.tile([P, C_PASSES, HALF, PACK], BF16, align_bytes=64)
@@ -439,8 +451,10 @@ def tile_merge_pa_t_kernel(
                     haar_on_vector(ll_grouped, ahead, pieces[:2])
                 if step in halves:
                     y_mx[step] = project(step, y_tiles[step])
+                    last_written[step] = y_mx[step][0][:, HALF - 1 : HALF]
                 if ahead in halves and ahead > HALF_ON_TENSOR:
                     haar_on_vector(ll_grouped, ahead, pieces[2:])
+                    last_written[step] = ll_grouped[:, C_PASSES - 1, HALF - 1, PACK - 1 : PACK]
 
             for step in range(PINNED_FROM):
                 one_step(step)

@@ -36,7 +36,6 @@ PINNED = (
     mybir.EngineType.DVE, mybir.EngineType.Pool, mybir.EngineType.Activation, mybir.EngineType.PE,
 )
 PINNED_FROM = 3
-ROWS_AT_ONCE = 2
 
 FLOPS = 2 * B * H2 * W2 * (M * C + 3 * O * M)
 
@@ -371,12 +370,12 @@ def tile_merge_pa_t_kernel(
                 nc.scalar.activation(out=z[:, di], in_=z[:, di], func=ACT.Exp)
                 add_over_window(e_sum, z[:, di], di)
 
-            def mix(engine, half, e, ev_sum, di):
+            def weigh(engine, half, e, di):
                 prod = prod_pool.tile([P, KS, HALF], F32)
                 engine.tensor_tensor(
                     out=prod[:], in0=e[:, di], in1=window_row(v_moved, half, di), op=ALU.mult
                 )
-                add_over_window(ev_sum, prod, di)
+                return prod
 
             def invert(e_sum):
                 quotient = single.tile([P, HALF], F32)
@@ -409,52 +408,66 @@ def tile_merge_pa_t_kernel(
             def one_step(step):
                 t = step - LEAD
                 last = N_HALVES - 1
+                ahead = step + 1
+                front = ahead in halves and ahead > HALF_ON_TENSOR
                 if t + 1 in halves:
                     q_half = query(y_mx[t + 1])
-                if t - 1 in halves and t - 1 < last:
+                late = t - 1 in halves and t - 1 < last
+                if late:
                     after_vector(last_written[step - 1])
-                    for di in range(ROWS_AT_ONCE, KS):
-                        mix(nc.gpsimd, t - 1, z_tiles[t - 1], ev_sums[t - 1], di)
+                    late_prod = weigh(nc.gpsimd, t - 1, z_tiles[t - 1], KS - 1)
                 if t in halves:
-                    at_once = ROWS_AT_ONCE if t < last else 1
+                    at_once = KS - 1 if t < last else 1
                     e_sum = sum_psum.tile([P, HALF], F32)
                     ev_sum = ev_psum.tile([P, HALF], F32)
                     ev_sums[t] = ev_sum
                     for di in range(KS):
                         subtract(z_tiles[t], max_tiles[t], di)
                         exponential(z_tiles[t], e_sum, di)
-                    for di in range(at_once):
-                        mix(nc.gpsimd, t, z_tiles[t], ev_sum, di)
+                        if di == 0 and late:
+                            add_over_window(ev_sums[t - 1], late_prod, KS - 1)
+                    prods = [weigh(nc.gpsimd, t, z_tiles[t], di) for di in range(at_once)]
                 if t + 1 in halves:
                     z_tiles[t + 1] = scores(t + 1, q_half)
                     z_rough = round_scores(z_tiles[t + 1])
                 if t - 1 in halves:
                     att_back = divide(inverses[t - 1], ev_sums[t - 1])
                     nc.scalar.copy(out=att[:, t - 1, :], in_=att_back[:])
+                if t - 2 in halves:
+                    nc.vector.bn_stats(out=stats[:, t - 2, :], in_=att[:, t - 2, :])
                 if t == last:
-                    for di in range(at_once, KS):
-                        mix(nc.vector, t, z_tiles[t], ev_sum, di)
+                    prods.extend([weigh(nc.vector, t, z_tiles[t], di) for di in range(at_once, KS)])
                 if step in halves:
                     y_tiles[step] = first_convolution(ll_tiles[step])
+                if t in halves:
+                    for di in range(len(prods)):
+                        add_over_window(ev_sum, prods[di], di)
+                if front:
+                    ll_grouped = work.tile([P, C_PASSES, HALF, PACK], BF16, align_bytes=64)
+                    ll_tiles[ahead] = ll_grouped
+                    col_sums = [add_columns(ahead, pieces[0][0], pieces[0][1])]
                 if t + 1 in halves:
                     max_tiles[t + 1], last_written[step] = maximum(z_rough)
-                if t - 1 in halves:
-                    nc.vector.bn_stats(out=stats[:, t - 1, :], in_=att[:, t - 1, :])
                 if t in halves:
                     inverses[t] = invert(e_sum)
                 if t == last:
                     nc.scalar.sqrt(out=warm[:], in_=warm[:])
-                ahead = step + 1
-                if ahead in halves and ahead > HALF_ON_TENSOR:
-                    ll_grouped = work.tile([P, C_PASSES, HALF, PACK], BF16, align_bytes=64)
-                    ll_tiles[ahead] = ll_grouped
-                    haar_on_vector(ll_grouped, ahead, pieces[:2])
+                if front:
+                    col_sums.append(add_columns(ahead, pieces[1][0], pieces[1][1]))
+                    add_rows_on_vector(ll_grouped, pieces[0][0], pieces[0][1], col_sums[0])
                 if step in halves:
                     y_mx[step] = project(step, y_tiles[step])
                     last_written[step] = y_mx[step][0][:, HALF - 1 : HALF]
-                if ahead in halves and ahead > HALF_ON_TENSOR:
-                    haar_on_vector(ll_grouped, ahead, pieces[2:])
+                if front:
+                    for i in range(2, len(pieces) + 1):
+                        if i < len(pieces):
+                            col_sums.append(add_columns(ahead, pieces[i][0], pieces[i][1]))
+                        add_rows_on_vector(
+                            ll_grouped, pieces[i - 1][0], pieces[i - 1][1], col_sums[i - 1]
+                        )
                     last_written[step] = ll_grouped[:, C_PASSES - 1, HALF - 1, PACK - 1 : PACK]
+                if t - 1 == last:
+                    nc.vector.bn_stats(out=stats[:, last, :], in_=att[:, last, :])
 
             for step in range(PINNED_FROM):
                 one_step(step)

@@ -17,6 +17,7 @@ BN_EPS = 1e-5
 
 P = 128
 PACK = 4
+PAIRS = PACK // 2
 K_PASS = P * PACK
 C_PASSES = C // K_PASS
 M_TILES = M // P
@@ -28,14 +29,17 @@ PIECE = PIECE_ROWS * W2
 BLOCKS = HALF // P
 KS = 3
 SETS = 2
+PUT_OFF = N_HALVES - 4
 LEAD = 3
 RUN = 4
+PAD = 4
+PITCH = W2 + PAD
 TAPS = [(a, c) for a in range(2) for c in range(2)]
 HALF_ON_TENSOR = 1
 PINNED = (
     mybir.EngineType.DVE, mybir.EngineType.Pool, mybir.EngineType.Activation, mybir.EngineType.PE,
 )
-PINNED_FROM = 3
+ADD, TAKE_OUT, TURN_BACK, PUT = range(4)
 
 FLOPS = 2 * B * H2 * W2 * (M * C + 3 * O * M)
 
@@ -62,13 +66,12 @@ def tile_merge_pa_t_kernel(
         wqkv_scales = keep.tile([P, 3, O], U8, align_bytes=64)
         bias = keep.tile([P, M_TILES], F32)
 
-        k_moved = keep.tile([P, SETS, KS, H2 + 2, W2], F32)
-        v_moved = keep.tile([P, SETS, KS, H2 + 2, W2], F32)
+        k_moved = keep.tile([P, SETS, KS, H2 + 2, PITCH], F32)
+        v_moved = keep.tile([P, SETS, KS, H2 + 2, PITCH], F32)
         for moved in (k_moved, v_moved):
-            nc.gpsimd.memset(moved[:, :, :, 0, :], 0.0)
-            nc.gpsimd.memset(moved[:, :, :, H2 + 1, :], 0.0)
-            nc.gpsimd.memset(moved[:, :, 0, :, 0:8], 0.0)
-            nc.gpsimd.memset(moved[:, :, KS - 1, :, W2 - 8 : W2], 0.0)
+            nc.gpsimd.memset(moved[:, :, :, 0, 0:W2], 0.0)
+            nc.gpsimd.memset(moved[:, :, :, H2 + 1, 0:W2], 0.0)
+            nc.gpsimd.memset(moved[:, :, 1, :, W2:PITCH], 0.0)
 
         att = keep.tile([P, N_HALVES, HALF], F32)
         warm = keep.tile([P, 1], F32)
@@ -87,21 +90,27 @@ def tile_merge_pa_t_kernel(
         beta = keep.tile([P, 1], F32)
         slope = keep.tile([P, 1], F32)
         one_minus_slope = keep.tile([P, 1], F32)
-        nc.vector.tensor_copy(out=bias[:], in_=bias_bf16[:])
-        nc.vector.tensor_copy(out=gamma[:], in_=gamma_bf16[:])
-        nc.vector.tensor_copy(out=beta[:], in_=beta_bf16[:])
-        nc.vector.tensor_copy(out=slope[:], in_=slope_bf16[:])
-        nc.vector.tensor_scalar(
-            out=one_minus_slope[:], in0=slope[:], scalar1=-1.0, scalar2=1.0,
-            op0=ALU.mult, op1=ALU.add,
-        )
+
+        def widen_constants():
+            nc.vector.tensor_copy(out=bias[:], in_=bias_bf16[:])
+            nc.vector.tensor_copy(out=gamma[:], in_=gamma_bf16[:])
+            nc.vector.tensor_copy(out=beta[:], in_=beta_bf16[:])
+            nc.vector.tensor_copy(out=slope[:], in_=slope_bf16[:])
+            nc.vector.tensor_scalar(
+                out=one_minus_slope[:], in0=slope[:], scalar1=-1.0, scalar2=1.0,
+                op0=ALU.mult, op1=ALU.add,
+            )
 
         with ExitStack() as stream:
-            x_pool = stream.enter_context(tc.tile_pool(name="x_pool", bufs=3))
-            col_pool = stream.enter_context(tc.tile_pool(name="col_pool", bufs=2))
+            stream.enter_context(tc.manual_schedule(engines=set(PINNED)))
+            x_pool = stream.enter_context(tc.tile_pool(name="x_pool", bufs=4))
+            col_pool = stream.enter_context(tc.tile_pool(name="col_pool", bufs=3))
             work = stream.enter_context(tc.tile_pool(name="work", bufs=2))
+            quotient_pool = stream.enter_context(tc.tile_pool(name="quotient_pool", bufs=2))
             single = stream.enter_context(tc.tile_pool(name="single", bufs=1))
+            haar_pool = stream.enter_context(tc.tile_pool(name="haar_pool", bufs=2))
             mx_psum = stream.enter_context(tc.psum_pool(name="mx_psum", bufs=2))
+            haar_psum = stream.enter_context(tc.psum_pool(name="haar_psum", bufs=2))
             pieces = [(g, s) for g in range(C_PASSES) for s in range(HALF // PIECE)]
 
             def load_piece(pool, half, g, s):
@@ -139,38 +148,91 @@ def tile_merge_pa_t_kernel(
                     op=ALU.add,
                 )
 
-            def haar_on_vector(ll_grouped, half, some_pieces):
-                col_sums = []
-                for i in range(len(some_pieces) + 1):
-                    if i < len(some_pieces):
-                        col_sums.append(add_columns(half, some_pieces[i][0], some_pieces[i][1]))
-                    if i >= 1:
-                        add_rows_on_vector(
-                            ll_grouped, some_pieces[i - 1][0], some_pieces[i - 1][1],
-                            col_sums[i - 1],
+            def add_rows_on_tensor(ll_grouped, g, s, col_sum):
+                turned, rounded = [], []
+
+                def add():
+                    for blk in range(PIECE // P):
+                        total = haar_psum.tile([P, PACK, P], F32, tag="haar")
+                        for a in range(2):
+                            for j in range(PACK):
+                                add_transposed(
+                                    nc, total[:, j, :], col_sum[:, a, j, blk * P : (blk + 1) * P],
+                                    ident_f32[:], a == 0 and j == 0, a == 1 and j == PACK - 1,
+                                )
+                        turned.append(total)
+
+                def take_out():
+                    for blk in range(PIECE // P):
+                        pairs = haar_pool.tile([P, PAIRS, P, 2], BF16, tag="pairs")
+                        nc.scalar.copy(
+                            out=pairs[:],
+                            in_=turned[blk][:].rearrange("x (u e) p -> x u p e", e=2),
                         )
+                        rounded.append(pairs)
+
+                def turn_back():
+                    words = haar_psum.tile([P, PIECE // P, PAIRS, P], F32, tag="haar")
+                    for blk in range(PIECE // P):
+                        row_words = rounded[blk][:].rearrange("x u p e -> x (u p e)").bitcast(F32)
+                        for u in range(PAIRS):
+                            nc.tensor.transpose(
+                                words[:, blk, u, :], row_words[:, u * P : (u + 1) * P], ident_f32[:]
+                            )
+                    turned.append(words)
+
+                def put():
+                    first = (g * HALF + s * PIECE) * PAIRS
+                    nc.scalar.copy(
+                        out=ll_grouped[:].rearrange("p g x j -> p (g x j)").bitcast(F32)[
+                            :, first : first + PIECE * PAIRS
+                        ].rearrange("p (b x u) -> p b x u", x=P, u=PAIRS),
+                        in_=turned[-1][:].rearrange("p b u x -> p b x u"),
+                    )
+
+                return add, take_out, turn_back, put
+
+            ll_tiles, col_sums, on_tensor = {}, {}, {}
+
+            def open_half(half):
+                ll_grouped = work.tile([P, C_PASSES, HALF, PACK], BF16, align_bytes=64)
+                ll_tiles[half] = ll_grouped
+
+            def columns(half, i):
+                g, s = pieces[i]
+                col_sums[half, i] = add_columns(half, g, s)
+                on_tensor[half, i] = add_rows_on_tensor(ll_tiles[half], g, s, col_sums[half, i])
+
+            def rows(half, i):
+                g, s = pieces[i]
+                add_rows_on_vector(ll_tiles[half], g, s, col_sums[half, i])
+
+            def part(half, i, which):
+                on_tensor[half, i][which]()
 
             def haar_by_matmul(ll_grouped, half, some_pieces, early):
                 for g, s in some_pieces:
                     pixels = load_piece(early, half, g, s)
-                    for first in range(0, PACK, 2):
-                        total = mx_psum.tile([P, 2, PIECE_ROWS, W2], F32, tag="mx")
+                    some_rows = PIECE_ROWS // 2
+                    for top in range(0, PIECE_ROWS, some_rows):
+                        total = mx_psum.tile([P, PACK, some_rows, W2], F32, tag="mx")
                         for tap, (a, c) in enumerate(TAPS):
                             nc.tensor.matmul(
                                 out=total[:],
                                 lhsT=ident_bf16[:],
-                                rhs=pixels[:, first : first + 2, :, a, :, c],
+                                rhs=pixels[:, :, top : top + some_rows, a, :, c],
                                 start=(tap == 0),
                                 stop=(tap == len(TAPS) - 1),
                             )
+                        first = s * PIECE + top * W2
                         nc.scalar.copy(
-                            out=ll_grouped[:, g, s * PIECE : (s + 1) * PIECE, first : first + 2],
+                            out=ll_grouped[:, g, first : first + some_rows * W2, :],
                             in_=total[:].rearrange("p j r w -> p (r w) j"),
                         )
 
             def first_convolution(ll_grouped):
-                ll_codes = work.tile([P, C_PASSES, HALF], U32, align_bytes=64)
-                ll_scales = work.tile([P, C_PASSES, HALF], U8, align_bytes=64)
+                ll_codes = single.tile([P, C_PASSES, HALF], U32, align_bytes=64)
+                ll_scales = single.tile([P, C_PASSES, HALF], U8, align_bytes=64)
                 nc.vector.quantize_mx(
                     out=ll_codes[:].rearrange("p g x -> p (g x)").bitcast(FP8X4),
                     scales=ll_scales[:].rearrange("p g x -> p (g x)"),
@@ -194,8 +256,11 @@ def tile_merge_pa_t_kernel(
                         out=y_rows[:, t, :], in_=y_acc[:], func=ACT.Identity,
                         bias=bias[:, t : t + 1], scale=0.5,
                     )
+                return y_rows
+
+            def interleave(copy, y_rows):
                 y_grouped = single.tile([P, HALF, PACK], BF16, align_bytes=64)
-                nc.scalar.copy(out=y_grouped[:], in_=y_rows[:].rearrange("p t x -> p x t"))
+                copy(out=y_grouped[:], in_=y_rows[:].rearrange("p t x -> p x t"))
                 return y_grouped
 
             def projection(s, y_quantised):
@@ -224,14 +289,34 @@ def tile_merge_pa_t_kernel(
                 for s in (1, 2):
                     proj = projection(s, (y_codes, y_scales))
                     planes = (k_moved if s == 1 else v_moved)[:, b % SETS]
-                    nc.scalar.copy(out=planes[:, 0, rows, 1:W2], in_=proj[:, :, 0 : W2 - 1])
-                    nc.scalar.copy(out=planes[:, 1, rows, :], in_=proj[:])
-                    nc.scalar.copy(out=planes[:, 2, rows, 0 : W2 - 1], in_=proj[:, :, 1:W2])
+                    nc.scalar.copy(out=planes[:, 1, rows, 0:W2], in_=proj[:])
+                    flat = planes.rearrange("p c r w -> p c (r w)")
+                    first, end = rows.start * PITCH, rows.stop * PITCH - PAD
+                    for plane, step in ((0, -1), (2, 1)):
+                        nc.sync.dma_start(
+                            out=flat[:, plane, first:end], in_=flat[:, 1, first + step : end + step]
+                        )
                 return y_codes, y_scales
 
-            ll_tiles = {}
+            def turn_words(dst, dst_first, words, firsts):
+                turned = mx_psum.tile([P, len(firsts), PAIRS, P], F32, tag="mx")
+                for i, first in enumerate(firsts):
+                    for u in range(PAIRS):
+                        nc.tensor.transpose(
+                            turned[:, i, u, :],
+                            words[:, first + u : first + PAIRS * P : PAIRS],
+                            ident_f32[:],
+                        )
+                n_words = len(firsts) * PAIRS * P
+                nc.scalar.copy(
+                    out=dst[:, dst_first : dst_first + n_words].rearrange(
+                        "p (i n u) -> p i n u", n=P, u=PAIRS
+                    ),
+                    in_=turned[:].rearrange("p i u n -> p i n u"),
+                )
+
             with tc.tile_pool(name="stage", bufs=1) as stage, tc.tile_pool(
-                name="early", bufs=2
+                name="early", bufs=3
             ) as early:
                 w1_rows = stage.tile([P, M_TILES, C], BF16)
                 nc.scalar.dma_start(
@@ -240,46 +325,46 @@ def tile_merge_pa_t_kernel(
                 wqkv_rows = stage.tile([P, 3, M], BF16)
                 for s, w_s in enumerate((w_q, w_k, w_v)):
                     nc.scalar.dma_start(out=wqkv_rows[:, s, :], in_=w_s)
-                w1_sorted = stage.tile([P, M_TILES, C_PASSES, PACK, P], BF16)
                 w1_grouped = stage.tile([P, C_PASSES, M_TILES, P, PACK], BF16, align_bytes=64)
-                for t in range(M_TILES):
-                    nc.scalar.copy(
-                        out=w1_sorted[:, t],
-                        in_=w1_rows[:, t, :].rearrange("n (g p j) -> n g j p", g=C_PASSES, j=PACK),
-                    )
-                    for g in range(C_PASSES):
-                        turned = mx_psum.tile([P, PACK, P], BF16, tag="mx")
-                        for j in range(PACK):
-                            nc.tensor.transpose(
-                                turned[:, j, :], w1_sorted[:, t, g, j, :], ident_bf16[:]
-                            )
-                        nc.scalar.copy(
-                            out=w1_grouped[:, g, t], in_=turned[:].rearrange("p j n -> p n j")
-                        )
-                wqkv_sorted = stage.tile([P, 3, PACK, P], BF16)
                 wqkv_grouped = stage.tile([P, 3, O, PACK], BF16, align_bytes=64)
-                nc.scalar.copy(
-                    out=wqkv_sorted[:], in_=wqkv_rows[:].rearrange("o s (p j) -> o s j p", j=PACK)
-                )
-                for s in range(3):
-                    turned = mx_psum.tile([P, PACK, P], BF16, tag="mx")
-                    for j in range(PACK):
-                        nc.tensor.transpose(turned[:, j, :], wqkv_sorted[:, s, j, :], ident_bf16[:])
-                    nc.scalar.copy(
-                        out=wqkv_grouped[:, s], in_=turned[:].rearrange("p j o -> p o j")
+                w1_words = w1_rows[:].rearrange("n t c -> n (t c)").bitcast(F32)
+                w1_words_out = w1_grouped[:].rearrange("p g t n j -> p (g t n j)").bitcast(F32)
+                for t in range(0, M_TILES, 2):
+                    for g in range(C_PASSES):
+                        turn_words(
+                            w1_words_out, (g * M_TILES + t) * PAIRS * P,
+                            w1_words, [(t + i) * C // 2 + g * PAIRS * P for i in range(2)],
+                        )
+                wqkv_words = wqkv_rows[:].rearrange("o s m -> o (s m)").bitcast(F32)
+                wqkv_words_out = wqkv_grouped[:].rearrange("p s o j -> p (s o j)").bitcast(F32)
+                for group in ((0, 1), (2,)):
+                    turn_words(
+                        wqkv_words_out, group[0] * PAIRS * O,
+                        wqkv_words, [s * PAIRS * P for s in group],
                     )
-                for half in range(2):
-                    ll_grouped = work.tile([P, C_PASSES, HALF, PACK], BF16, align_bytes=64)
-                    ll_tiles[half] = ll_grouped
-                haar_on_vector(ll_tiles[0], 0, pieces)
-                haar_by_matmul(ll_tiles[HALF_ON_TENSOR], HALF_ON_TENSOR, pieces[:-1], early)
-                haar_on_vector(ll_tiles[HALF_ON_TENSOR], HALF_ON_TENSOR, pieces[-1:])
+                open_half(0)
+                open_half(HALF_ON_TENSOR)
+                columns(0, 0)
+                columns(0, 1)
+                rows(0, 0)
+                columns(0, 2)
+                haar_by_matmul(ll_tiles[HALF_ON_TENSOR], HALF_ON_TENSOR, pieces[0:1], early)
+                rows(0, 1)
                 for g in range(C_PASSES):
                     nc.vector.quantize_mx(
                         out=w1_codes[:, g, :].bitcast(FP8X4),
                         scales=w1_scales[:, g, :],
                         in_=w1_grouped[:, g].rearrange("p t n j -> p (t n j)"),
                     )
+                columns(0, 3)
+                haar_by_matmul(ll_tiles[HALF_ON_TENSOR], HALF_ON_TENSOR, pieces[1:2], early)
+                rows(0, 2)
+                rows(0, 3)
+                widen_constants()
+                y_grouped = interleave(nc.scalar.copy, first_convolution(ll_tiles[0]))
+                haar_by_matmul(ll_tiles[HALF_ON_TENSOR], HALF_ON_TENSOR, pieces[2:3], early)
+                columns(HALF_ON_TENSOR, 3)
+                rows(HALF_ON_TENSOR, 3)
                 for s in range(3):
                     nc.vector.quantize_mx(
                         out=wqkv_codes[:, s, :].bitcast(FP8X4),
@@ -289,10 +374,10 @@ def tile_merge_pa_t_kernel(
 
             z_pool = stream.enter_context(tc.tile_pool(name="z_pool", bufs=2, reuse_waits="tile"))
             prod_pool = stream.enter_context(
-                tc.tile_pool(name="prod_pool", bufs=3, reuse_waits="tile")
+                tc.tile_pool(name="prod_pool", bufs=2, reuse_waits="tile")
             )
             sum_psum = stream.enter_context(tc.psum_pool(name="sum_psum", bufs=1))
-            ev_psum = stream.enter_context(tc.psum_pool(name="ev_psum", bufs=2))
+            ev_psum = stream.enter_context(tc.psum_pool(name="ev_psum", bufs=1))
             turn_psum = stream.enter_context(tc.psum_pool(name="turn_psum", bufs=1))
             max_psum = stream.enter_context(tc.psum_pool(name="max_psum", bufs=1))
             sides = (slice(0, HALF // 2), slice(HALF // 2, HALF))
@@ -310,40 +395,41 @@ def tile_merge_pa_t_kernel(
             def window_row(moved, half, di):
                 b, h = divmod(half, 2)
                 top = h * HALF_ROWS + di
-                return moved[:, b % SETS, :, top : top + HALF_ROWS, :].rearrange(
-                    "p c r w -> p c (r w)"
-                )
+                return moved[:, b % SETS, :, top : top + HALF_ROWS, 0:W2]
+
+            def by_rows(t):
+                return t.rearrange("p c (r w) -> p c r w", w=W2)
 
             def query(y_quantised):
-                return projection(0, y_quantised)[:].rearrange("p r w -> p (r w)")
+                return projection(0, y_quantised)
 
             def scores(half, q_half):
                 z = z_pool.tile([P, KS, KS, HALF], F32)
                 for di in range(KS):
                     nc.vector.tensor_tensor(
-                        out=z[:, di],
-                        in0=q_half.unsqueeze(1).to_broadcast([P, KS, HALF]),
+                        out=by_rows(z[:, di]),
+                        in0=q_half[:].unsqueeze(1).to_broadcast([P, KS, HALF_ROWS, W2]),
                         in1=window_row(k_moved, half, di),
                         op=ALU.mult,
                     )
                 return z
 
-            def round_scores(z):
+            def round_scores(z, n_rows):
                 z_rough = single.tile([P, KS, KS, HALF], BF16)
-                for di in range(KS):
+                for di in range(n_rows):
                     nc.scalar.copy(out=z_rough[:, di], in_=z[:, di])
-                return z_rough
+                return [(z_rough if di < n_rows else z)[:, di] for di in range(KS)]
 
-            def maximum(z_rough):
+            def maximum(z_rows):
                 tree = single.tile([P, KS, HALF], BF16)
                 for side in sides:
                     nc.vector.tensor_tensor(
-                        out=tree[:, :, side], in0=z_rough[:, 0, :, side],
-                        in1=z_rough[:, 1, :, side], op=ALU.max,
+                        out=tree[:, :, side], in0=z_rows[0][:, :, side],
+                        in1=z_rows[1][:, :, side], op=ALU.max,
                     )
                 for side in sides:
                     nc.vector.tensor_tensor(
-                        out=tree[:, :, side], in0=tree[:, :, side], in1=z_rough[:, 2, :, side],
+                        out=tree[:, :, side], in0=tree[:, :, side], in1=z_rows[2][:, :, side],
                         op=ALU.max,
                     )
                 for dj in range(1, KS):
@@ -370,23 +456,32 @@ def tile_merge_pa_t_kernel(
                 nc.scalar.activation(out=z[:, di], in_=z[:, di], func=ACT.Exp)
                 add_over_window(e_sum, z[:, di], di)
 
-            def weigh(engine, half, e, di):
-                prod = prod_pool.tile([P, KS, HALF], F32)
+            def weigh(engine, half, e, di, in_place=False):
+                if in_place:
+                    prod = e[:, di]
+                else:
+                    prod_tile = prod_pool.tile([P, KS, HALF], F32)
+                    prod = prod_tile[:]
                 engine.tensor_tensor(
-                    out=prod[:], in0=e[:, di], in1=window_row(v_moved, half, di), op=ALU.mult
+                    out=by_rows(prod), in0=by_rows(e[:, di]),
+                    in1=window_row(v_moved, half, di), op=ALU.mult,
                 )
                 return prod
 
-            def invert(e_sum):
-                quotient = single.tile([P, HALF], F32)
+            def logarithm(e_sum):
+                quotient = quotient_pool.tile([P, HALF], F32)
                 nc.scalar.activation(out=quotient[:], in_=e_sum[:], func=ACT.Ln)
-                nc.scalar.activation(out=quotient[:], in_=quotient[:], func=ACT.Exp, scale=-1.0)
                 return quotient
+
+            def invert(quotient):
+                nc.scalar.activation(out=quotient[:], in_=quotient[:], func=ACT.Exp, scale=-1.0)
 
             def divide(quotient, ev_sum):
                 nc.vector.tensor_tensor(
                     out=quotient[:], in0=ev_sum[:], in1=quotient[:], op=ALU.mult
                 )
+
+            def attention(quotient):
                 att_back = turn_psum.tile([P, HALF], F32)
                 for blk in range(BLOCKS):
                     cols = slice(blk * P, (blk + 1) * P)
@@ -394,7 +489,8 @@ def tile_merge_pa_t_kernel(
                 return att_back
 
             halves = range(N_HALVES)
-            y_tiles, y_mx, z_tiles, max_tiles, ev_sums, inverses = {}, {}, {}, {}, {}, {}
+            last = N_HALVES - 1
+            y_mx, z_tiles, max_tiles, e_sums, ev_sums, inverses = {}, {}, {}, {}, {}, {}
 
             def after_vector(written):
                 if written.dtype == BF16:
@@ -405,103 +501,210 @@ def tile_merge_pa_t_kernel(
 
             last_written = {}
 
-            def one_step(step):
+            def new_sum(pool, in_haar_bank):
+                if in_haar_bank:
+                    return haar_psum.tile([P, HALF], F32, tag="haar", name="long_sum")
+                return pool.tile([P, HALF], F32, name="window_sum")
+
+            def statistics(half, att_half):
+                nc.vector.bn_stats(out=stats[:, half, :], in_=att_half)
+
+            def weights(t, between):
+                e_sums[t] = new_sum(sum_psum, t == PUT_OFF)
+                for di in range(KS):
+                    subtract(z_tiles[t], max_tiles[t], di)
+                    exponential(z_tiles[t], e_sums[t], di)
+                    if di in between:
+                        between[di]()
+
+            def take_attention(h):
+                att_back = attention(inverses[h])
+                nc.scalar.copy(out=att[:, h, :], in_=att_back[:])
+
+            def put_late_row(t):
+                after_vector(last_written[t + LEAD])
+                late_prod = weigh(nc.gpsimd, t, z_tiles[t], KS - 1)
+                return lambda: add_over_window(ev_sums[t], late_prod, KS - 1)
+
+            def haar_step(step):
                 t = step - LEAD
-                last = N_HALVES - 1
                 ahead = step + 1
-                front = ahead in halves and ahead > HALF_ON_TENSOR
-                if t + 1 in halves:
+                q_half = query(y_mx[t + 1])
+                weights(t, {0: put_late_row(t - 1)} if t >= 1 else {})
+                prods = [weigh(nc.gpsimd, t, z_tiles[t], di) for di in range(KS - 1)]
+                z_tiles[t + 1] = scores(t + 1, q_half)
+                z_rows = round_scores(z_tiles[t + 1], KS)
+                if t >= 1:
+                    divide(inverses[t - 1], ev_sums[t - 1])
+                    take_attention(t - 1)
+                if t >= 2:
+                    statistics(t - 2, att[:, t - 2, :])
+                y_grouped = interleave(nc.scalar.copy, first_convolution(ll_tiles[step]))
+                ev_sums[t] = new_sum(ev_psum, False)
+                for di in range(len(prods)):
+                    add_over_window(ev_sums[t], prods[di], di)
+                open_half(ahead)
+                columns(ahead, 0)
+                part(ahead, 0, ADD)
+                max_tiles[t + 1], last_written[step] = maximum(z_rows)
+                inverses[t] = logarithm(e_sums[t])
+                part(ahead, 0, TAKE_OUT)
+                columns(ahead, 1)
+                y_mx[step] = project(step, y_grouped)
+                part(ahead, 0, TURN_BACK)
+                part(ahead, 0, PUT)
+                part(ahead, 1, ADD)
+                invert(inverses[t])
+                part(ahead, 1, TAKE_OUT)
+                columns(ahead, 2)
+                part(ahead, 1, TURN_BACK)
+                part(ahead, 1, PUT)
+                columns(ahead, 3)
+                rows(ahead, 2)
+                rows(ahead, 3)
+                last_written[step] = ll_tiles[ahead][:, C_PASSES - 1, HALF - 1, PACK - 1 : PACK]
+
+            def last_fronts():
+                for t in range(PUT_OFF, last):
                     q_half = query(y_mx[t + 1])
-                late = t - 1 in halves and t - 1 < last
-                if late:
-                    after_vector(last_written[step - 1])
-                    late_prod = weigh(nc.gpsimd, t - 1, z_tiles[t - 1], KS - 1)
-                if t in halves:
-                    at_once = KS - 1 if t < last else 1
-                    e_sum = sum_psum.tile([P, HALF], F32)
-                    ev_sum = ev_psum.tile([P, HALF], F32)
-                    ev_sums[t] = ev_sum
-                    for di in range(KS):
-                        subtract(z_tiles[t], max_tiles[t], di)
-                        exponential(z_tiles[t], e_sum, di)
-                        if di == 0 and late:
-                            add_over_window(ev_sums[t - 1], late_prod, KS - 1)
-                    prods = [weigh(nc.gpsimd, t, z_tiles[t], di) for di in range(at_once)]
-                if t + 1 in halves:
+                    weights(t, {0: put_late_row(t - 1)})
+                    prods = [weigh(nc.gpsimd, t, z_tiles[t], di) for di in range(KS - 1)]
                     z_tiles[t + 1] = scores(t + 1, q_half)
-                    z_rough = round_scores(z_tiles[t + 1])
-                if t - 1 in halves:
-                    att_back = divide(inverses[t - 1], ev_sums[t - 1])
-                    nc.scalar.copy(out=att[:, t - 1, :], in_=att_back[:])
-                if t - 2 in halves:
-                    nc.vector.bn_stats(out=stats[:, t - 2, :], in_=att[:, t - 2, :])
-                if t == last:
-                    prods.extend([weigh(nc.vector, t, z_tiles[t], di) for di in range(at_once, KS)])
-                if step in halves:
-                    y_tiles[step] = first_convolution(ll_tiles[step])
-                if t in halves:
+                    z_rows = round_scores(z_tiles[t + 1], KS - 1)
+                    if t == PUT_OFF:
+                        divide(inverses[t - 1], ev_sums[t - 1])
+                        take_attention(t - 1)
+                        statistics(t - 2, att[:, t - 2, :])
+                        y_rows = first_convolution(ll_tiles[last])
+                        max_tiles[t + 1], last_written[t + LEAD] = maximum(z_rows)
+                    if t == PUT_OFF + 1:
+                        statistics(t - 2, att[:, t - 2, :])
+                    if t == PUT_OFF + 2:
+                        divide(inverses[t - 2], ev_sums[t - 2])
+                        divide(inverses[t - 1], ev_sums[t - 1])
+                    ev_sums[t] = new_sum(ev_psum, t == PUT_OFF + 1)
                     for di in range(len(prods)):
-                        add_over_window(ev_sum, prods[di], di)
-                if front:
-                    ll_grouped = work.tile([P, C_PASSES, HALF, PACK], BF16, align_bytes=64)
-                    ll_tiles[ahead] = ll_grouped
-                    col_sums = [add_columns(ahead, pieces[0][0], pieces[0][1])]
-                if t + 1 in halves:
-                    max_tiles[t + 1], last_written[step] = maximum(z_rough)
-                if t in halves:
-                    inverses[t] = invert(e_sum)
-                if t == last:
-                    nc.scalar.sqrt(out=warm[:], in_=warm[:])
-                if front:
-                    col_sums.append(add_columns(ahead, pieces[1][0], pieces[1][1]))
-                    add_rows_on_vector(ll_grouped, pieces[0][0], pieces[0][1], col_sums[0])
-                if step in halves:
-                    y_mx[step] = project(step, y_tiles[step])
-                    last_written[step] = y_mx[step][0][:, HALF - 1 : HALF]
-                if front:
-                    for i in range(2, len(pieces) + 1):
-                        if i < len(pieces):
-                            col_sums.append(add_columns(ahead, pieces[i][0], pieces[i][1]))
-                        add_rows_on_vector(
-                            ll_grouped, pieces[i - 1][0], pieces[i - 1][1], col_sums[i - 1]
-                        )
-                    last_written[step] = ll_grouped[:, C_PASSES - 1, HALF - 1, PACK - 1 : PACK]
-                if t - 1 == last:
-                    nc.vector.bn_stats(out=stats[:, last, :], in_=att[:, last, :])
+                        add_over_window(ev_sums[t], prods[di], di)
+                        if di == 0 and t == PUT_OFF + 2:
+                            take_attention(t - 2)
+                    if t > PUT_OFF:
+                        max_tiles[t + 1], last_written[t + LEAD] = maximum(z_rows)
+                    if t == PUT_OFF:
+                        y_mx[last] = project(last, interleave(nc.vector.tensor_copy, y_rows))
+                        last_written[t + LEAD] = y_mx[last][0][:, HALF - 1 : HALF]
+                    if t == PUT_OFF + 1:
+                        for h in (t - 1, t):
+                            inverses[h] = logarithm(e_sums[h])
+                        for h in (t - 1, t):
+                            invert(inverses[h])
+                    if t == PUT_OFF + 2:
+                        inverses[t] = logarithm(e_sums[t])
+                        invert(inverses[t])
+                        take_attention(t - 1)
+                        row = weigh(nc.vector, t, z_tiles[t], KS - 1)
+                        add_over_window(ev_sums[t], row, KS - 1)
 
-            for step in range(PINNED_FROM):
-                one_step(step)
-            with tc.manual_schedule(engines=set(PINNED)):
-                for step in range(PINNED_FROM, N_HALVES + LEAD + 1):
-                    one_step(step)
+            def last_step():
+                weights(last, {})
+                e = z_tiles[last]
+                divide(inverses[last - 1], ev_sums[last - 1])
+                inverses[last] = logarithm(e_sums[last])
+                invert(inverses[last])
+                ev_sums[last] = new_sum(ev_psum, False)
+                for di in range(KS):
+                    prod = weigh(nc.vector, last, e, di, in_place=(di == KS - 1))
+                    add_over_window(ev_sums[last], prod, di)
+                    if di == 0:
+                        take_attention(last - 1)
+                for h in (last - 3, last - 2):
+                    statistics(h, att[:, h, :])
+                nc.scalar.sqrt(out=warm[:], in_=warm[:])
+                divide(inverses[last], ev_sums[last])
+                statistics(last - 1, att[:, last - 1, :])
+                att_back = attention(inverses[last])
+                statistics(last, att_back[:])
+                nc.scalar.copy(out=att[:, last, :], in_=att_back[:])
 
-        last = whole.enter_context(tc.tile_pool(name="last", bufs=2, reuse_waits="tile"))
-        mean_var = last.tile([P, 2], F32)
+            def head(y_grouped):
+                open_half(2)
+                columns(2, 0)
+                part(2, 0, ADD)
+                part(2, 0, TAKE_OUT)
+                y_mx[0] = project(0, y_grouped)
+                y_grouped = interleave(nc.scalar.copy, first_convolution(ll_tiles[1]))
+                columns(2, 1)
+                part(2, 0, TURN_BACK)
+                part(2, 0, PUT)
+                part(2, 1, ADD)
+                columns(2, 2)
+                columns(2, 3)
+                part(2, 1, TAKE_OUT)
+                y_mx[1] = project(1, y_grouped)
+                q_half = query(y_mx[0])
+                part(2, 1, TURN_BACK)
+                part(2, 1, PUT)
+                part(2, 2, ADD)
+                open_half(3)
+                columns(3, 2)
+                rows(3, 2)
+                part(2, 2, TAKE_OUT)
+                part(2, 2, TURN_BACK)
+                part(2, 2, PUT)
+                part(2, 3, ADD)
+                columns(3, 3)
+                rows(3, 3)
+                part(2, 3, TAKE_OUT)
+                part(2, 3, TURN_BACK)
+                part(2, 3, PUT)
+                z_tiles[0] = scores(0, q_half)
+                z_rows = round_scores(z_tiles[0], KS)
+                y_grouped = interleave(nc.scalar.copy, first_convolution(ll_tiles[2]))
+                columns(3, 0)
+                columns(3, 1)
+                part(3, 0, ADD)
+                part(3, 0, TAKE_OUT)
+                max_tiles[0], written = maximum(z_rows)
+                part(3, 0, TURN_BACK)
+                part(3, 0, PUT)
+                y_mx[2] = project(2, y_grouped)
+                part(3, 1, ADD)
+                part(3, 1, TAKE_OUT)
+                part(3, 1, TURN_BACK)
+                part(3, 1, PUT)
+
+            head(y_grouped)
+            for step in range(LEAD, N_HALVES - 1):
+                haar_step(step)
+            last_fronts()
+            last_step()
+
+        final_pool = whole.enter_context(tc.tile_pool(name="final_pool", bufs=4, reuse_waits="tile"))
+        mean_var = final_pool.tile([P, 2], F32)
         nc.vector.bn_aggr(out=mean_var[:], in_=stats[:].rearrange("p t s -> p (t s)"))
-        var_eps = last.tile([P, 1], F32)
+        var_eps = final_pool.tile([P, 1], F32)
         nc.vector.tensor_scalar_add(out=var_eps[:], in0=mean_var[:, 1:2], scalar1=BN_EPS)
-        std = last.tile([P, 1], F32)
+        std = final_pool.tile([P, 1], F32)
         nc.scalar.sqrt(out=std[:], in_=var_eps[:])
-        inv_std = last.tile([P, 1], F32)
+        inv_std = final_pool.tile([P, 1], F32)
         nc.vector.reciprocal(out=inv_std[:], in_=std[:])
-        gain = last.tile([P, 1], F32)
+        gain = final_pool.tile([P, 1], F32)
         nc.vector.tensor_mul(out=gain[:], in0=gamma[:], in1=inv_std[:])
-        mean_gain = last.tile([P, 1], F32)
+        mean_gain = final_pool.tile([P, 1], F32)
         nc.vector.tensor_mul(out=mean_gain[:], in0=mean_var[:, 0:1], in1=gain[:])
-        shift = last.tile([P, 1], F32)
+        shift = final_pool.tile([P, 1], F32)
         nc.vector.tensor_sub(out=shift[:], in0=beta[:], in1=mean_gain[:])
-        slope_gain = last.tile([P, 1], F32)
+        slope_gain = final_pool.tile([P, 1], F32)
         nc.vector.tensor_mul(out=slope_gain[:], in0=slope[:], in1=gain[:])
-        slope_shift = last.tile([P, 1], F32)
+        slope_shift = final_pool.tile([P, 1], F32)
         nc.vector.tensor_mul(out=slope_shift[:], in0=slope[:], in1=shift[:])
 
         for b in range(B):
             att_b = att[:, 2 * b : 2 * b + 2, :].rearrange("p t x -> p (t x)")
-            positive = last.tile([P, H2 * W2], F32)
+            positive = final_pool.tile([P, H2 * W2], F32)
             nc.scalar.activation(
                 out=positive[:], in_=att_b, func=ACT.Relu, bias=shift[:], scale=gain[:]
             )
-            final = last.tile([P, H2 * W2], F32)
+            final = final_pool.tile([P, H2 * W2], F32)
             nc.vector.tensor_scalar(
                 out=final[:], in0=att_b, scalar1=slope_gain[:], scalar2=slope_shift[:],
                 op0=ALU.mult, op1=ALU.add,

@@ -29,7 +29,6 @@ PIECE = PIECE_ROWS * W2
 BLOCKS = HALF // P
 KS = 3
 SETS = 2
-PUT_OFF = N_HALVES - 4
 LEAD = 3
 RUN = 4
 PAD = 4
@@ -103,7 +102,7 @@ def tile_merge_pa_t_kernel(
 
         with ExitStack() as stream:
             stream.enter_context(tc.manual_schedule(engines=set(PINNED)))
-            x_pool = stream.enter_context(tc.tile_pool(name="x_pool", bufs=4))
+            x_pool = stream.enter_context(tc.tile_pool(name="x_pool", bufs=3))
             col_pool = stream.enter_context(tc.tile_pool(name="col_pool", bufs=3))
             work = stream.enter_context(tc.tile_pool(name="work", bufs=2))
             quotient_pool = stream.enter_context(tc.tile_pool(name="quotient_pool", bufs=2))
@@ -374,11 +373,10 @@ def tile_merge_pa_t_kernel(
 
             z_pool = stream.enter_context(tc.tile_pool(name="z_pool", bufs=2, reuse_waits="tile"))
             prod_pool = stream.enter_context(
-                tc.tile_pool(name="prod_pool", bufs=2, reuse_waits="tile")
+                tc.tile_pool(name="prod_pool", bufs=3, reuse_waits="tile")
             )
             sum_psum = stream.enter_context(tc.psum_pool(name="sum_psum", bufs=1))
-            ev_psum = stream.enter_context(tc.psum_pool(name="ev_psum", bufs=1))
-            turn_psum = stream.enter_context(tc.psum_pool(name="turn_psum", bufs=1))
+            ev_psum = stream.enter_context(tc.psum_pool(name="ev_psum", bufs=2))
             max_psum = stream.enter_context(tc.psum_pool(name="max_psum", bufs=1))
             sides = (slice(0, HALF // 2), slice(HALF // 2, HALF))
 
@@ -482,7 +480,7 @@ def tile_merge_pa_t_kernel(
                 )
 
             def attention(quotient):
-                att_back = turn_psum.tile([P, HALF], F32)
+                att_back = mx_psum.tile([P, HALF], F32, tag="mx")
                 for blk in range(BLOCKS):
                     cols = slice(blk * P, (blk + 1) * P)
                     nc.tensor.transpose(att_back[:, cols], quotient[:, cols], ident_f32[:])
@@ -490,7 +488,7 @@ def tile_merge_pa_t_kernel(
 
             halves = range(N_HALVES)
             last = N_HALVES - 1
-            y_mx, z_tiles, max_tiles, e_sums, ev_sums, inverses = {}, {}, {}, {}, {}, {}
+            y_mx, z_tiles, max_tiles, ev_sums, inverses = {}, {}, {}, {}, {}
 
             def after_vector(written):
                 if written.dtype == BF16:
@@ -501,21 +499,17 @@ def tile_merge_pa_t_kernel(
 
             last_written = {}
 
-            def new_sum(pool, in_haar_bank):
-                if in_haar_bank:
-                    return haar_psum.tile([P, HALF], F32, tag="haar", name="long_sum")
-                return pool.tile([P, HALF], F32, name="window_sum")
-
             def statistics(half, att_half):
                 nc.vector.bn_stats(out=stats[:, half, :], in_=att_half)
 
             def weights(t, between):
-                e_sums[t] = new_sum(sum_psum, t == PUT_OFF)
+                e_sum = sum_psum.tile([P, HALF], F32)
                 for di in range(KS):
                     subtract(z_tiles[t], max_tiles[t], di)
-                    exponential(z_tiles[t], e_sums[t], di)
+                    exponential(z_tiles[t], e_sum, di)
                     if di in between:
                         between[di]()
+                return e_sum
 
             def take_attention(h):
                 att_back = attention(inverses[h])
@@ -526,100 +520,144 @@ def tile_merge_pa_t_kernel(
                 late_prod = weigh(nc.gpsimd, t, z_tiles[t], KS - 1)
                 return lambda: add_over_window(ev_sums[t], late_prod, KS - 1)
 
+            kept = {}
+
+            def logarithms(t, e_sum):
+                if t % 2 == 0 and t < last - 1:
+                    waiting = single.tile([P, HALF], F32)
+                    nc.scalar.copy(out=waiting[:], in_=e_sum[:])
+                    kept[t] = waiting
+                else:
+                    if t - 1 in kept:
+                        inverses[t - 1] = logarithm(kept[t - 1])
+                    inverses[t] = logarithm(e_sum)
+
+            def inversions(t):
+                if t % 2 == 1 or t >= last - 1:
+                    if t - 1 in kept:
+                        invert(inverses[t - 1])
+                    invert(inverses[t])
+
+            def sum_of_products(t, prods):
+                ev_sum = ev_psum.tile([P, HALF], F32)
+                ev_sums[t] = ev_sum
+                for di in range(len(prods)):
+                    add_over_window(ev_sum, prods[di], di)
+
             def haar_step(step):
                 t = step - LEAD
                 ahead = step + 1
                 q_half = query(y_mx[t + 1])
-                weights(t, {0: put_late_row(t - 1)} if t >= 1 else {})
+                e_sum = weights(t, {0: put_late_row(t - 1)} if t >= 1 else {})
+                if t >= 2 and t % 2 == 0:
+                    inversions(t - 1)
                 prods = [weigh(nc.gpsimd, t, z_tiles[t], di) for di in range(KS - 1)]
                 z_tiles[t + 1] = scores(t + 1, q_half)
                 z_rows = round_scores(z_tiles[t + 1], KS)
-                if t >= 1:
-                    divide(inverses[t - 1], ev_sums[t - 1])
-                    take_attention(t - 1)
-                if t >= 2:
-                    statistics(t - 2, att[:, t - 2, :])
+                if t >= 2 and t % 2 == 0:
+                    for h in (t - 2, t - 1):
+                        divide(inverses[h], ev_sums[h])
+                    for h in (t - 2, t - 1):
+                        take_attention(h)
+                if t >= 3 and t % 2 == 1:
+                    for h in (t - 3, t - 2):
+                        statistics(h, att[:, h, :])
                 y_grouped = interleave(nc.scalar.copy, first_convolution(ll_tiles[step]))
-                ev_sums[t] = new_sum(ev_psum, False)
-                for di in range(len(prods)):
-                    add_over_window(ev_sums[t], prods[di], di)
+                n_tensor = 2 if t == 0 else (2 if t % 2 == 0 else 1)
                 open_half(ahead)
                 columns(ahead, 0)
                 part(ahead, 0, ADD)
+                if t % 2 == 1:
+                    logarithms(t, e_sum)
                 max_tiles[t + 1], last_written[step] = maximum(z_rows)
-                inverses[t] = logarithm(e_sums[t])
                 part(ahead, 0, TAKE_OUT)
                 columns(ahead, 1)
+                if t % 2 == 0:
+                    logarithms(t, e_sum)
+                if n_tensor == 1:
+                    sum_of_products(t, prods)
                 y_mx[step] = project(step, y_grouped)
                 part(ahead, 0, TURN_BACK)
                 part(ahead, 0, PUT)
-                part(ahead, 1, ADD)
-                invert(inverses[t])
-                part(ahead, 1, TAKE_OUT)
+                if n_tensor >= 2:
+                    part(ahead, 1, ADD)
+                    part(ahead, 1, TAKE_OUT)
                 columns(ahead, 2)
-                part(ahead, 1, TURN_BACK)
-                part(ahead, 1, PUT)
+                if n_tensor >= 2:
+                    part(ahead, 1, TURN_BACK)
+                    part(ahead, 1, PUT)
+                if n_tensor >= 3:
+                    part(ahead, 2, ADD)
+                    part(ahead, 2, TAKE_OUT)
+                    part(ahead, 2, TURN_BACK)
+                    part(ahead, 2, PUT)
+                if n_tensor > 1:
+                    sum_of_products(t, prods)
+                if n_tensor < 2:
+                    rows(ahead, 1)
                 columns(ahead, 3)
-                rows(ahead, 2)
+                if n_tensor < 3:
+                    rows(ahead, 2)
                 rows(ahead, 3)
                 last_written[step] = ll_tiles[ahead][:, C_PASSES - 1, HALF - 1, PACK - 1 : PACK]
 
             def last_fronts():
-                for t in range(PUT_OFF, last):
+                for t in range(last - LEAD, last):
                     q_half = query(y_mx[t + 1])
-                    weights(t, {0: put_late_row(t - 1)})
+                    e_sum = weights(t, {0: put_late_row(t - 1)})
+                    if t % 2 == 0:
+                        inversions(t - 1)
                     prods = [weigh(nc.gpsimd, t, z_tiles[t], di) for di in range(KS - 1)]
                     z_tiles[t + 1] = scores(t + 1, q_half)
                     z_rows = round_scores(z_tiles[t + 1], KS - 1)
-                    if t == PUT_OFF:
-                        divide(inverses[t - 1], ev_sums[t - 1])
-                        take_attention(t - 1)
-                        statistics(t - 2, att[:, t - 2, :])
+                    if t % 2 == 0:
+                        for h in (t - 2, t - 1):
+                            divide(inverses[h], ev_sums[h])
+                    if t == last - LEAD:
+                        for h in (t - 2, t - 1):
+                            take_attention(h)
                         y_rows = first_convolution(ll_tiles[last])
                         max_tiles[t + 1], last_written[t + LEAD] = maximum(z_rows)
-                    if t == PUT_OFF + 1:
-                        statistics(t - 2, att[:, t - 2, :])
-                    if t == PUT_OFF + 2:
-                        divide(inverses[t - 2], ev_sums[t - 2])
-                        divide(inverses[t - 1], ev_sums[t - 1])
-                    ev_sums[t] = new_sum(ev_psum, t == PUT_OFF + 1)
-                    for di in range(len(prods)):
-                        add_over_window(ev_sums[t], prods[di], di)
-                        if di == 0 and t == PUT_OFF + 2:
-                            take_attention(t - 2)
-                    if t > PUT_OFF:
-                        max_tiles[t + 1], last_written[t + LEAD] = maximum(z_rows)
-                    if t == PUT_OFF:
                         y_mx[last] = project(last, interleave(nc.vector.tensor_copy, y_rows))
                         last_written[t + LEAD] = y_mx[last][0][:, HALF - 1 : HALF]
-                    if t == PUT_OFF + 1:
-                        for h in (t - 1, t):
-                            inverses[h] = logarithm(e_sums[h])
-                        for h in (t - 1, t):
-                            invert(inverses[h])
-                    if t == PUT_OFF + 2:
-                        inverses[t] = logarithm(e_sums[t])
-                        invert(inverses[t])
+                        sum_of_products(t, prods)
+                        logarithms(t, e_sum)
+                    if t == last - LEAD + 1:
+                        for h in (t - 3, t - 2):
+                            statistics(h, att[:, h, :])
+                        sum_of_products(t, prods[:1])
+                        max_tiles[t + 1], last_written[t + LEAD] = maximum(z_rows)
+                        add_over_window(ev_sums[t], prods[1], 1)
+                        logarithms(t, e_sum)
+                    if t == last - LEAD + 2:
+                        take_attention(t - 2)
+                        sum_of_products(t, prods)
+                        max_tiles[t + 1], last_written[t + LEAD] = maximum(z_rows)
+                        logarithms(t, e_sum)
+                        inversions(t)
                         take_attention(t - 1)
                         row = weigh(nc.vector, t, z_tiles[t], KS - 1)
                         add_over_window(ev_sums[t], row, KS - 1)
 
             def last_step():
-                weights(last, {})
+                e_sum = weights(last, {})
                 e = z_tiles[last]
                 divide(inverses[last - 1], ev_sums[last - 1])
-                inverses[last] = logarithm(e_sums[last])
-                invert(inverses[last])
-                ev_sums[last] = new_sum(ev_psum, False)
-                for di in range(KS):
-                    prod = weigh(nc.vector, last, e, di, in_place=(di == KS - 1))
-                    add_over_window(ev_sums[last], prod, di)
-                    if di == 0:
-                        take_attention(last - 1)
+                logarithms(last, e_sum)
+                inversions(last)
+                first_rows = [weigh(nc.vector, last, e, di) for di in range(2)]
+                nc.vector.tensor_tensor(
+                    out=first_rows[0], in0=first_rows[0], in1=first_rows[1], op=ALU.add
+                )
+                ev_sum = ev_psum.tile([P, HALF], F32)
+                add_over_window(ev_sum, first_rows[0], 0)
+                take_attention(last - 1)
+                last_row = weigh(nc.vector, last, e, KS - 1, in_place=True)
+                add_over_window(ev_sum, last_row, KS - 1)
                 for h in (last - 3, last - 2):
                     statistics(h, att[:, h, :])
                 nc.scalar.sqrt(out=warm[:], in_=warm[:])
-                divide(inverses[last], ev_sums[last])
+                divide(inverses[last], ev_sum)
                 statistics(last - 1, att[:, last - 1, :])
                 att_back = attention(inverses[last])
                 statistics(last, att_back[:])
@@ -637,40 +675,31 @@ def tile_merge_pa_t_kernel(
                 part(2, 0, PUT)
                 part(2, 1, ADD)
                 columns(2, 2)
-                columns(2, 3)
+                rows(2, 2)
                 part(2, 1, TAKE_OUT)
                 y_mx[1] = project(1, y_grouped)
                 q_half = query(y_mx[0])
                 part(2, 1, TURN_BACK)
                 part(2, 1, PUT)
-                part(2, 2, ADD)
+                columns(2, 3)
+                part(2, 3, ADD)
                 open_half(3)
                 columns(3, 2)
                 rows(3, 2)
-                part(2, 2, TAKE_OUT)
-                part(2, 2, TURN_BACK)
-                part(2, 2, PUT)
-                part(2, 3, ADD)
-                columns(3, 3)
-                rows(3, 3)
                 part(2, 3, TAKE_OUT)
                 part(2, 3, TURN_BACK)
                 part(2, 3, PUT)
+                columns(3, 3)
+                rows(3, 3)
                 z_tiles[0] = scores(0, q_half)
                 z_rows = round_scores(z_tiles[0], KS)
                 y_grouped = interleave(nc.scalar.copy, first_convolution(ll_tiles[2]))
                 columns(3, 0)
+                rows(3, 0)
                 columns(3, 1)
-                part(3, 0, ADD)
-                part(3, 0, TAKE_OUT)
+                rows(3, 1)
                 max_tiles[0], written = maximum(z_rows)
-                part(3, 0, TURN_BACK)
-                part(3, 0, PUT)
                 y_mx[2] = project(2, y_grouped)
-                part(3, 1, ADD)
-                part(3, 1, TAKE_OUT)
-                part(3, 1, TURN_BACK)
-                part(3, 1, PUT)
 
             head(y_grouped)
             for step in range(LEAD, N_HALVES - 1):
@@ -698,19 +727,34 @@ def tile_merge_pa_t_kernel(
         slope_shift = final_pool.tile([P, 1], F32)
         nc.vector.tensor_mul(out=slope_shift[:], in0=slope[:], in1=shift[:])
 
-        for b in range(B):
+        positives, finals = [], []
+
+        def sides_of_slope(b):
             att_b = att[:, 2 * b : 2 * b + 2, :].rearrange("p t x -> p (t x)")
             positive = final_pool.tile([P, H2 * W2], F32)
             nc.scalar.activation(
                 out=positive[:], in_=att_b, func=ACT.Relu, bias=shift[:], scale=gain[:]
             )
             final = final_pool.tile([P, H2 * W2], F32)
-            nc.vector.tensor_scalar(
-                out=final[:], in0=att_b, scalar1=slope_gain[:], scalar2=slope_shift[:],
-                op0=ALU.mult, op1=ALU.add,
-            )
+            if b < B - 1:
+                nc.vector.tensor_scalar(
+                    out=final[:], in0=att_b, scalar1=slope_gain[:], scalar2=slope_shift[:],
+                    op0=ALU.mult, op1=ALU.add,
+                )
+            else:
+                nc.scalar.activation(
+                    out=final[:], in_=att_b, func=ACT.Identity,
+                    bias=slope_shift[:], scale=slope_gain[:],
+                )
+            positives.append(positive)
+            finals.append(final)
+
+        sides_of_slope(0)
+        for b in range(B):
+            if b + 1 < B:
+                sides_of_slope(b + 1)
             nc.vector.scalar_tensor_tensor(
-                out=final[:], in0=positive[:], scalar=one_minus_slope[:], in1=final[:],
+                out=finals[b][:], in0=positives[b][:], scalar=one_minus_slope[:], in1=finals[b][:],
                 op0=ALU.mult, op1=ALU.add,
             )
-            nc.sync.dma_start(out=out[b].rearrange("o i j -> o (i j)"), in_=final[:])
+            nc.sync.dma_start(out=out[b].rearrange("o i j -> o (i j)"), in_=finals[b][:])

@@ -112,28 +112,34 @@ def tile_merge_pa_t_kernel(
             haar_psum = stream.enter_context(tc.psum_pool(name="haar_psum", bufs=2))
             pieces = [(g, s) for g in range(C_PASSES) for s in range(HALF // PIECE)]
 
-            def load_piece(pool, half, g, s):
+            def load_piece(pool, half, g, s, n_loads=1):
                 b, h = divmod(half, 2)
                 row = 2 * (h * HALF_ROWS + s * PIECE_ROWS)
+                n_rows = 2 * PIECE_ROWS // n_loads
                 x_piece = pool.tile([P, PACK, 2 * PIECE_ROWS * W], BF16)
-                nc.sync.dma_start(
-                    out=x_piece[:],
-                    in_=x[
-                        b, g * K_PASS : (g + 1) * K_PASS, row : row + 2 * PIECE_ROWS, :
-                    ].rearrange("(p j) r w -> p j (r w)", j=PACK),
-                )
+                for top in range(0, 2 * PIECE_ROWS, n_rows):
+                    nc.sync.dma_start(
+                        out=x_piece[:, :, top * W : (top + n_rows) * W],
+                        in_=x[
+                            b, g * K_PASS : (g + 1) * K_PASS, row + top : row + top + n_rows, :
+                        ].rearrange("(p j) r w -> p j (r w)", j=PACK),
+                    )
                 return x_piece[:].rearrange("p j (r a w c) -> p j r a w c", a=2, w=W2, c=2)
 
-            def add_columns(half, g, s):
-                pixels = load_piece(x_pool, half, g, s)
+            def add_columns(half, g, s, n_loads=1):
+                pixels = load_piece(x_pool, half, g, s, n_loads)
                 col_sum = col_pool.tile([P, 2, PACK, PIECE], F32)
-                for a in range(2):
-                    nc.vector.tensor_tensor(
-                        out=col_sum[:, a].rearrange("p j (r w) -> p j r w", w=W2),
-                        in0=pixels[:, :, :, a, :, 0],
-                        in1=pixels[:, :, :, a, :, 1],
-                        op=ALU.add,
-                    )
+                n_rows = PIECE_ROWS // n_loads
+                for top in range(0, PIECE_ROWS, n_rows):
+                    for a in range(2):
+                        nc.vector.tensor_tensor(
+                            out=col_sum[:, a].rearrange("p j (r w) -> p j r w", w=W2)[
+                                :, :, top : top + n_rows, :
+                            ],
+                            in0=pixels[:, :, top : top + n_rows, a, :, 0],
+                            in1=pixels[:, :, top : top + n_rows, a, :, 1],
+                            op=ALU.add,
+                        )
                 return col_sum
 
             def add_rows_on_vector(ll_grouped, g, s, col_sum):
@@ -197,9 +203,9 @@ def tile_merge_pa_t_kernel(
                 ll_grouped = work.tile([P, C_PASSES, HALF, PACK], BF16, align_bytes=64)
                 ll_tiles[half] = ll_grouped
 
-            def columns(half, i):
+            def columns(half, i, n_loads=1):
                 g, s = pieces[i]
-                col_sums[half, i] = add_columns(half, g, s)
+                col_sums[half, i] = add_columns(half, g, s, n_loads)
                 on_tensor[half, i] = add_rows_on_tensor(ll_tiles[half], g, s, col_sums[half, i])
 
             def rows(half, i):
@@ -318,51 +324,53 @@ def tile_merge_pa_t_kernel(
                 name="early", bufs=3
             ) as early:
                 w1_rows = stage.tile([P, M_TILES, C], BF16)
-                nc.scalar.dma_start(
-                    out=w1_rows[:], in_=w_c1.rearrange("(n t) c -> n t c", t=M_TILES)
-                )
                 wqkv_rows = stage.tile([P, 3, M], BF16)
                 for s, w_s in enumerate((w_q, w_k, w_v)):
                     nc.scalar.dma_start(out=wqkv_rows[:, s, :], in_=w_s)
                 w1_grouped = stage.tile([P, C_PASSES, M_TILES, P, PACK], BF16, align_bytes=64)
                 wqkv_grouped = stage.tile([P, 3, O, PACK], BF16, align_bytes=64)
-                w1_words = w1_rows[:].rearrange("n t c -> n (t c)").bitcast(F32)
-                w1_words_out = w1_grouped[:].rearrange("p g t n j -> p (g t n j)").bitcast(F32)
-                for t in range(0, M_TILES, 2):
-                    for g in range(C_PASSES):
-                        turn_words(
-                            w1_words_out, (g * M_TILES + t) * PAIRS * P,
-                            w1_words, [(t + i) * C // 2 + g * PAIRS * P for i in range(2)],
-                        )
-                wqkv_words = wqkv_rows[:].rearrange("o s m -> o (s m)").bitcast(F32)
-                wqkv_words_out = wqkv_grouped[:].rearrange("p s o j -> p (s o j)").bitcast(F32)
-                for group in ((0, 1), (2,)):
-                    turn_words(
-                        wqkv_words_out, group[0] * PAIRS * O,
-                        wqkv_words, [s * PAIRS * P for s in group],
+                def turn_weights():
+                    nc.sync.dma_start(
+                        out=w1_rows[:], in_=w_c1.rearrange("(n t) c -> n t c", t=M_TILES)
                     )
+                    w1_words = w1_rows[:].rearrange("n t c -> n (t c)").bitcast(F32)
+                    w1_words_out = w1_grouped[:].rearrange("p g t n j -> p (g t n j)").bitcast(F32)
+                    for t in range(0, M_TILES, 2):
+                        for g in range(C_PASSES):
+                            turn_words(
+                                w1_words_out, (g * M_TILES + t) * PAIRS * P,
+                                w1_words, [(t + i) * C // 2 + g * PAIRS * P for i in range(2)],
+                            )
+                    wqkv_words = wqkv_rows[:].rearrange("o s m -> o (s m)").bitcast(F32)
+                    wqkv_words_out = wqkv_grouped[:].rearrange("p s o j -> p (s o j)").bitcast(F32)
+                    for group in ((0, 1), (2,)):
+                        turn_words(
+                            wqkv_words_out, group[0] * PAIRS * O,
+                            wqkv_words, [s * PAIRS * P for s in group],
+                        )
+
                 open_half(0)
                 open_half(HALF_ON_TENSOR)
-                columns(0, 0)
-                columns(0, 1)
+                columns(0, 0, n_loads=2)
                 rows(0, 0)
-                columns(0, 2)
-                haar_by_matmul(ll_tiles[HALF_ON_TENSOR], HALF_ON_TENSOR, pieces[0:1], early)
+                widen_constants()
+                columns(0, 1)
                 rows(0, 1)
+                columns(0, 2)
+                turn_weights()
+                rows(0, 2)
+                columns(0, 3)
+                haar_by_matmul(ll_tiles[HALF_ON_TENSOR], HALF_ON_TENSOR, pieces[:2], early)
+                rows(0, 3)
                 for g in range(C_PASSES):
                     nc.vector.quantize_mx(
                         out=w1_codes[:, g, :].bitcast(FP8X4),
                         scales=w1_scales[:, g, :],
                         in_=w1_grouped[:, g].rearrange("p t n j -> p (t n j)"),
                     )
-                columns(0, 3)
-                haar_by_matmul(ll_tiles[HALF_ON_TENSOR], HALF_ON_TENSOR, pieces[1:2], early)
-                rows(0, 2)
-                rows(0, 3)
-                widen_constants()
                 y_grouped = interleave(nc.scalar.copy, first_convolution(ll_tiles[0]))
-                haar_by_matmul(ll_tiles[HALF_ON_TENSOR], HALF_ON_TENSOR, pieces[2:3], early)
                 columns(HALF_ON_TENSOR, 3)
+                haar_by_matmul(ll_tiles[HALF_ON_TENSOR], HALF_ON_TENSOR, pieces[2:-1], early)
                 rows(HALF_ON_TENSOR, 3)
                 for s in range(3):
                     nc.vector.quantize_mx(
@@ -676,12 +684,12 @@ def tile_merge_pa_t_kernel(
                 part(2, 1, ADD)
                 columns(2, 2)
                 rows(2, 2)
+                columns(2, 3)
                 part(2, 1, TAKE_OUT)
                 y_mx[1] = project(1, y_grouped)
                 q_half = query(y_mx[0])
                 part(2, 1, TURN_BACK)
                 part(2, 1, PUT)
-                columns(2, 3)
                 part(2, 3, ADD)
                 open_half(3)
                 columns(3, 2)
@@ -707,7 +715,7 @@ def tile_merge_pa_t_kernel(
             last_fronts()
             last_step()
 
-        final_pool = whole.enter_context(tc.tile_pool(name="final_pool", bufs=4, reuse_waits="tile"))
+        final_pool = whole.enter_context(tc.tile_pool(name="final_pool", bufs=5, reuse_waits="tile"))
         mean_var = final_pool.tile([P, 2], F32)
         nc.vector.bn_aggr(out=mean_var[:], in_=stats[:].rearrange("p t s -> p (t s)"))
         var_eps = final_pool.tile([P, 1], F32)
@@ -727,34 +735,39 @@ def tile_merge_pa_t_kernel(
         slope_shift = final_pool.tile([P, 1], F32)
         nc.vector.tensor_mul(out=slope_shift[:], in0=slope[:], in1=shift[:])
 
+        flat = att[:].rearrange("p t x -> p (t x)")
+        rows_of_out = out.rearrange("b o i j -> o b (i j)")
+        parts = [(b, 0, H2 * W2) for b in range(B - 1)] + [(B - 1, k * HALF, HALF) for k in range(2)]
         positives, finals = [], []
 
-        def sides_of_slope(b):
-            att_b = att[:, 2 * b : 2 * b + 2, :].rearrange("p t x -> p (t x)")
+        def sides_of_slope(b, first, n):
+            att_part = flat[:, b * H2 * W2 + first : b * H2 * W2 + first + n]
             positive = final_pool.tile([P, H2 * W2], F32)
             nc.scalar.activation(
-                out=positive[:], in_=att_b, func=ACT.Relu, bias=shift[:], scale=gain[:]
+                out=positive[:, :n], in_=att_part, func=ACT.Relu, bias=shift[:], scale=gain[:]
             )
             final = final_pool.tile([P, H2 * W2], F32)
             if b < B - 1:
                 nc.vector.tensor_scalar(
-                    out=final[:], in0=att_b, scalar1=slope_gain[:], scalar2=slope_shift[:],
+                    out=final[:, :n], in0=att_part, scalar1=slope_gain[:], scalar2=slope_shift[:],
                     op0=ALU.mult, op1=ALU.add,
                 )
             else:
                 nc.scalar.activation(
-                    out=final[:], in_=att_b, func=ACT.Identity,
+                    out=final[:, :n], in_=att_part, func=ACT.Identity,
                     bias=slope_shift[:], scale=slope_gain[:],
                 )
             positives.append(positive)
             finals.append(final)
 
-        sides_of_slope(0)
-        for b in range(B):
-            if b + 1 < B:
-                sides_of_slope(b + 1)
+        sides_of_slope(parts[0][0], parts[0][1], parts[0][2])
+        for i, (b, first, n) in enumerate(parts):
+            if i + 1 < len(parts):
+                sides_of_slope(parts[i + 1][0], parts[i + 1][1], parts[i + 1][2])
             nc.vector.scalar_tensor_tensor(
-                out=finals[b][:], in0=positives[b][:], scalar=one_minus_slope[:], in1=finals[b][:],
-                op0=ALU.mult, op1=ALU.add,
+                out=finals[i][:, :n], in0=positives[i][:, :n], scalar=one_minus_slope[:],
+                in1=finals[i][:, :n], op0=ALU.mult, op1=ALU.add,
             )
-            nc.sync.dma_start(out=out[b].rearrange("o i j -> o (i j)"), in_=finals[b][:])
+            nc.sync.dma_start(
+                out=rows_of_out[:, b, first : first + n], in_=finals[i][:, :n]
+            )

@@ -112,32 +112,31 @@ def tile_merge_pa_t_kernel(
             haar_psum = stream.enter_context(tc.psum_pool(name="haar_psum", bufs=2))
             pieces = [(g, s) for g in range(C_PASSES) for s in range(HALF // PIECE)]
 
-            def load_piece(pool, half, g, s, n_loads=1):
+            def load_piece(pool, half, g, s, part=0, n_parts=1):
                 b, h = divmod(half, 2)
-                row = 2 * (h * HALF_ROWS + s * PIECE_ROWS)
-                n_rows = 2 * PIECE_ROWS // n_loads
-                x_piece = pool.tile([P, PACK, 2 * PIECE_ROWS * W], BF16)
-                for top in range(0, 2 * PIECE_ROWS, n_rows):
-                    nc.sync.dma_start(
-                        out=x_piece[:, :, top * W : (top + n_rows) * W],
-                        in_=x[
-                            b, g * K_PASS : (g + 1) * K_PASS, row + top : row + top + n_rows, :
-                        ].rearrange("(p j) r w -> p j (r w)", j=PACK),
-                    )
+                n_rows = 2 * PIECE_ROWS // n_parts
+                row = 2 * (h * HALF_ROWS + s * PIECE_ROWS) + part * n_rows
+                x_piece = pool.tile([P, PACK, n_rows * W], BF16)
+                nc.sync.dma_start(
+                    out=x_piece[:],
+                    in_=x[b, g * K_PASS : (g + 1) * K_PASS, row : row + n_rows, :].rearrange(
+                        "(p j) r w -> p j (r w)", j=PACK
+                    ),
+                )
                 return x_piece[:].rearrange("p j (r a w c) -> p j r a w c", a=2, w=W2, c=2)
 
-            def add_columns(half, g, s, n_loads=1):
-                pixels = load_piece(x_pool, half, g, s, n_loads)
+            def add_columns(half, g, s, n_parts=1):
                 col_sum = col_pool.tile([P, 2, PACK, PIECE], F32)
-                n_rows = PIECE_ROWS // n_loads
-                for top in range(0, PIECE_ROWS, n_rows):
+                n_rows = PIECE_ROWS // n_parts
+                for part in range(n_parts):
+                    pixels = load_piece(x_pool, half, g, s, part, n_parts)
                     for a in range(2):
                         nc.vector.tensor_tensor(
                             out=col_sum[:, a].rearrange("p j (r w) -> p j r w", w=W2)[
-                                :, :, top : top + n_rows, :
+                                :, :, part * n_rows : (part + 1) * n_rows, :
                             ],
-                            in0=pixels[:, :, top : top + n_rows, a, :, 0],
-                            in1=pixels[:, :, top : top + n_rows, a, :, 1],
+                            in0=pixels[:, :, :, a, :, 0],
+                            in1=pixels[:, :, :, a, :, 1],
                             op=ALU.add,
                         )
                 return col_sum
@@ -203,9 +202,9 @@ def tile_merge_pa_t_kernel(
                 ll_grouped = work.tile([P, C_PASSES, HALF, PACK], BF16, align_bytes=64)
                 ll_tiles[half] = ll_grouped
 
-            def columns(half, i, n_loads=1):
+            def columns(half, i, n_parts=1):
                 g, s = pieces[i]
-                col_sums[half, i] = add_columns(half, g, s, n_loads)
+                col_sums[half, i] = add_columns(half, g, s, n_parts)
                 on_tensor[half, i] = add_rows_on_tensor(ll_tiles[half], g, s, col_sums[half, i])
 
             def rows(half, i):
@@ -351,7 +350,7 @@ def tile_merge_pa_t_kernel(
 
                 open_half(0)
                 open_half(HALF_ON_TENSOR)
-                columns(0, 0, n_loads=2)
+                columns(0, 0, n_parts=2)
                 rows(0, 0)
                 widen_constants()
                 columns(0, 1)
@@ -703,9 +702,12 @@ def tile_merge_pa_t_kernel(
                 z_rows = round_scores(z_tiles[0], KS)
                 y_grouped = interleave(nc.scalar.copy, first_convolution(ll_tiles[2]))
                 columns(3, 0)
-                rows(3, 0)
+                part(3, 0, ADD)
+                part(3, 0, TAKE_OUT)
                 columns(3, 1)
                 rows(3, 1)
+                part(3, 0, TURN_BACK)
+                part(3, 0, PUT)
                 max_tiles[0], written = maximum(z_rows)
                 y_mx[2] = project(2, y_grouped)
 

@@ -89,6 +89,10 @@ def tile_merge_pa_t_kernel(
         beta = keep.tile([P, 1], F32)
         slope = keep.tile([P, 1], F32)
         one_minus_slope = keep.tile([P, 1], F32)
+        eps = keep.tile([P, 1], F32)
+        minus_gamma = keep.tile([P, 1], F32)
+        slope_gamma = keep.tile([P, 1], F32)
+        slope_beta = keep.tile([P, 1], F32)
 
         def widen_constants():
             nc.vector.tensor_copy(out=bias[:], in_=bias_bf16[:])
@@ -99,6 +103,15 @@ def tile_merge_pa_t_kernel(
                 out=one_minus_slope[:], in0=slope[:], scalar1=-1.0, scalar2=1.0,
                 op0=ALU.mult, op1=ALU.add,
             )
+            nc.vector.tensor_scalar(
+                out=eps[:], in0=slope[:], scalar1=0.0, scalar2=BN_EPS, op0=ALU.mult, op1=ALU.add
+            )
+            nc.vector.tensor_scalar(
+                out=minus_gamma[:], in0=gamma[:], scalar1=-1.0, scalar2=0.0,
+                op0=ALU.mult, op1=ALU.add,
+            )
+            nc.vector.tensor_mul(out=slope_gamma[:], in0=slope[:], in1=gamma[:])
+            nc.vector.tensor_mul(out=slope_beta[:], in0=slope[:], in1=beta[:])
 
         with ExitStack() as stream:
             stream.enter_context(tc.manual_schedule(engines=set(PINNED)))
@@ -583,13 +596,16 @@ def tile_merge_pa_t_kernel(
                     logarithms(t, e_sum)
                 if n_tensor == 1:
                     sum_of_products(t, prods)
+                if t % 2 == 0 and t > 0:
+                    columns(ahead, 2)
                 y_mx[step] = project(step, y_grouped)
                 part(ahead, 0, TURN_BACK)
                 part(ahead, 0, PUT)
                 if n_tensor >= 2:
                     part(ahead, 1, ADD)
                     part(ahead, 1, TAKE_OUT)
-                columns(ahead, 2)
+                if t % 2 == 1 or t == 0:
+                    columns(ahead, 2)
                 if n_tensor >= 2:
                     part(ahead, 1, TURN_BACK)
                     part(ahead, 1, PUT)
@@ -663,7 +679,7 @@ def tile_merge_pa_t_kernel(
                 add_over_window(ev_sum, last_row, KS - 1)
                 for h in (last - 3, last - 2):
                     statistics(h, att[:, h, :])
-                nc.scalar.sqrt(out=warm[:], in_=warm[:])
+                nc.scalar.activation(out=warm[:], in_=warm[:], func=ACT.Abs_reciprocal_sqrt)
                 divide(inverses[last], ev_sum)
                 statistics(last - 1, att[:, last - 1, :])
                 att_back = attention(inverses[last])
@@ -720,22 +736,28 @@ def tile_merge_pa_t_kernel(
         final_pool = whole.enter_context(tc.tile_pool(name="final_pool", bufs=5, reuse_waits="tile"))
         mean_var = final_pool.tile([P, 2], F32)
         nc.vector.bn_aggr(out=mean_var[:], in_=stats[:].rearrange("p t s -> p (t s)"))
-        var_eps = final_pool.tile([P, 1], F32)
-        nc.vector.tensor_scalar_add(out=var_eps[:], in0=mean_var[:, 1:2], scalar1=BN_EPS)
-        std = final_pool.tile([P, 1], F32)
-        nc.scalar.sqrt(out=std[:], in_=var_eps[:])
         inv_std = final_pool.tile([P, 1], F32)
-        nc.vector.reciprocal(out=inv_std[:], in_=std[:])
-        gain = final_pool.tile([P, 1], F32)
-        nc.vector.tensor_mul(out=gain[:], in0=gamma[:], in1=inv_std[:])
-        mean_gain = final_pool.tile([P, 1], F32)
-        nc.vector.tensor_mul(out=mean_gain[:], in0=mean_var[:, 0:1], in1=gain[:])
+        nc.scalar.activation(
+            out=inv_std[:], in_=mean_var[:, 1:2], func=ACT.Abs_reciprocal_sqrt, bias=eps[:]
+        )
+        mean_gamma = final_pool.tile([P, 1], F32)
+        nc.vector.tensor_mul(out=mean_gamma[:], in0=mean_var[:, 0:1], in1=minus_gamma[:])
+        slope_mean_gamma = final_pool.tile([P, 1], F32)
+        nc.vector.tensor_mul(out=slope_mean_gamma[:], in0=slope[:], in1=mean_gamma[:])
         shift = final_pool.tile([P, 1], F32)
-        nc.vector.tensor_sub(out=shift[:], in0=beta[:], in1=mean_gain[:])
-        slope_gain = final_pool.tile([P, 1], F32)
-        nc.vector.tensor_mul(out=slope_gain[:], in0=slope[:], in1=gain[:])
         slope_shift = final_pool.tile([P, 1], F32)
-        nc.vector.tensor_mul(out=slope_shift[:], in0=slope[:], in1=shift[:])
+        gain = final_pool.tile([P, 1], F32)
+        slope_gain = final_pool.tile([P, 1], F32)
+        nc.vector.tensor_mul(out=gain[:], in0=gamma[:], in1=inv_std[:])
+        nc.vector.tensor_scalar(
+            out=shift[:], in0=mean_gamma[:], scalar1=inv_std[:], scalar2=beta[:],
+            op0=ALU.mult, op1=ALU.add,
+        )
+        nc.vector.tensor_mul(out=slope_gain[:], in0=slope_gamma[:], in1=inv_std[:])
+        nc.vector.tensor_scalar(
+            out=slope_shift[:], in0=slope_mean_gamma[:], scalar1=inv_std[:], scalar2=slope_beta[:],
+            op0=ALU.mult, op1=ALU.add,
+        )
 
         flat = att[:].rearrange("p t x -> p (t x)")
         rows_of_out = out.rearrange("b o i j -> o b (i j)")

@@ -474,16 +474,19 @@ def tile_merge_pa_t_kernel(
                 nc.scalar.activation(out=z[:, di], in_=z[:, di], func=ACT.Exp)
                 add_over_window(e_sum, z[:, di], di)
 
-            def weigh(engine, half, e, di, in_place=False):
+            def weigh_columns(engine, half, e, di, prod, djs):
+                engine.tensor_tensor(
+                    out=by_rows(prod)[:, djs], in0=by_rows(e[:, di])[:, djs],
+                    in1=window_row(v_moved, half, di)[:, djs], op=ALU.mult,
+                )
+
+            def weigh(engine, half, e, di, in_place=False, n=KS):
                 if in_place:
                     prod = e[:, di]
                 else:
                     prod_tile = prod_pool.tile([P, KS, HALF], F32)
                     prod = prod_tile[:]
-                engine.tensor_tensor(
-                    out=by_rows(prod), in0=by_rows(e[:, di]),
-                    in1=window_row(v_moved, half, di), op=ALU.mult,
-                )
+                weigh_columns(engine, half, e, di, prod, slice(0, n))
                 return prod
 
             def logarithm(e_sum):
@@ -571,7 +574,10 @@ def tile_merge_pa_t_kernel(
                 e_sum = weights(t, {0: put_late_row(t - 1)} if t >= 1 else {})
                 if t >= 2 and t % 2 == 0:
                     inversions(t - 1)
-                prods = [weigh(nc.gpsimd, t, z_tiles[t], di) for di in range(KS - 1)]
+                prods = [
+                    weigh(nc.gpsimd, t, z_tiles[t], di, n=KS - 1 if t < 2 and di == 1 else KS)
+                    for di in range(KS - 1)
+                ]
                 z_tiles[t + 1] = scores(t + 1, q_half)
                 z_rows = round_scores(z_tiles[t + 1], KS)
                 if t >= 2 and t % 2 == 0:
@@ -582,6 +588,8 @@ def tile_merge_pa_t_kernel(
                 if t >= 3 and t % 2 == 1:
                     for h in (t - 3, t - 2):
                         statistics(h, att[:, h, :])
+                if t < 2:
+                    weigh_columns(nc.vector, t, z_tiles[t], 1, prods[1], slice(KS - 1, KS))
                 y_grouped = interleave(nc.scalar.copy, first_convolution(ll_tiles[step]))
                 n_tensor = 2 if t == 0 else (2 if t % 2 == 0 else 1)
                 open_half(ahead)
@@ -632,7 +640,7 @@ def tile_merge_pa_t_kernel(
                         inversions(t - 1)
                     prods = [weigh(nc.gpsimd, t, z_tiles[t], di) for di in range(KS - 1)]
                     z_tiles[t + 1] = scores(t + 1, q_half)
-                    z_rows = round_scores(z_tiles[t + 1], KS - 1)
+                    z_rows = round_scores(z_tiles[t + 1], KS if t == last - LEAD + 1 else KS - 1)
                     if t % 2 == 0:
                         for h in (t - 2, t - 1):
                             divide(inverses[h], ev_sums[h])
@@ -718,12 +726,9 @@ def tile_merge_pa_t_kernel(
                 z_rows = round_scores(z_tiles[0], KS)
                 y_grouped = interleave(nc.scalar.copy, first_convolution(ll_tiles[2]))
                 columns(3, 0)
-                part(3, 0, ADD)
-                part(3, 0, TAKE_OUT)
+                rows(3, 0)
                 columns(3, 1)
                 rows(3, 1)
-                part(3, 0, TURN_BACK)
-                part(3, 0, PUT)
                 max_tiles[0], written = maximum(z_rows)
                 y_mx[2] = project(2, y_grouped)
 

@@ -502,8 +502,8 @@ def tile_merge_pa_t_kernel(
                     out=quotient[:], in0=ev_sum[:], in1=quotient[:], op=ALU.mult
                 )
 
-            def attention(quotient):
-                att_back = mx_psum.tile([P, HALF], F32, tag="mx")
+            def attention(quotient, pool=mx_psum, tag="mx"):
+                att_back = pool.tile([P, HALF], F32, tag=tag)
                 for blk in range(BLOCKS):
                     cols = slice(blk * P, (blk + 1) * P)
                     nc.tensor.transpose(att_back[:, cols], quotient[:, cols], ident_f32[:])
@@ -534,8 +534,8 @@ def tile_merge_pa_t_kernel(
                         between[di]()
                 return e_sum
 
-            def take_attention(h):
-                att_back = attention(inverses[h])
+            def take_attention(h, pool=mx_psum, tag="mx"):
+                att_back = attention(inverses[h], pool, tag)
                 nc.scalar.copy(out=att[:, h, :], in_=att_back[:])
 
             def put_late_row(t):
@@ -543,7 +543,7 @@ def tile_merge_pa_t_kernel(
                 late_prod = weigh(nc.gpsimd, t, z_tiles[t], KS - 1)
                 return lambda: add_over_window(ev_sums[t], late_prod, KS - 1)
 
-            kept = {}
+            kept, q_halves = {}, {}
 
             def logarithms(t, e_sum):
                 if t % 2 == 0 and t < last - 1:
@@ -567,11 +567,25 @@ def tile_merge_pa_t_kernel(
                 for di in range(len(prods)):
                     add_over_window(ev_sum, prods[di], di)
 
+            pending = []
+
+            def late_and_pending(t):
+                late = put_late_row(t - 1) if t >= 1 else None
+
+                def both():
+                    if late:
+                        late()
+                    while_pending = list(pending)
+                    pending.clear()
+                    for one in while_pending:
+                        one()
+                return both
+
             def haar_step(step):
                 t = step - LEAD
                 ahead = step + 1
-                q_half = query(y_mx[t + 1])
-                e_sum = weights(t, {0: put_late_row(t - 1)} if t >= 1 else {})
+                q_half = q_halves[t + 1]
+                e_sum = weights(t, {0: late_and_pending(t)})
                 if t >= 2 and t % 2 == 0:
                     inversions(t - 1)
                 prods = [
@@ -591,7 +605,7 @@ def tile_merge_pa_t_kernel(
                 if t < 2:
                     weigh_columns(nc.vector, t, z_tiles[t], 1, prods[1], slice(KS - 1, KS))
                 y_grouped = interleave(nc.scalar.copy, first_convolution(ll_tiles[step]))
-                n_tensor = 2 if t == 0 else (2 if t % 2 == 0 else 1)
+                n_tensor = 2
                 open_half(ahead)
                 columns(ahead, 0)
                 part(ahead, 0, ADD)
@@ -616,12 +630,13 @@ def tile_merge_pa_t_kernel(
                     columns(ahead, 2)
                 if n_tensor >= 2:
                     part(ahead, 1, TURN_BACK)
-                    part(ahead, 1, PUT)
+                    pending.append(lambda: part(ahead, 1, PUT))
                 if n_tensor >= 3:
                     part(ahead, 2, ADD)
                     part(ahead, 2, TAKE_OUT)
                     part(ahead, 2, TURN_BACK)
                     part(ahead, 2, PUT)
+                q_halves[t + 2] = query(y_mx[t + 2])
                 if n_tensor > 1:
                     sum_of_products(t, prods)
                 if n_tensor < 2:
@@ -634,8 +649,8 @@ def tile_merge_pa_t_kernel(
 
             def last_fronts():
                 for t in range(last - LEAD, last):
-                    q_half = query(y_mx[t + 1])
-                    e_sum = weights(t, {0: put_late_row(t - 1)})
+                    q_half = q_halves[t + 1]
+                    e_sum = weights(t, {0: late_and_pending(t)})
                     if t % 2 == 0:
                         inversions(t - 1)
                     prods = [weigh(nc.gpsimd, t, z_tiles[t], di) for di in range(KS - 1)]
@@ -645,20 +660,21 @@ def tile_merge_pa_t_kernel(
                         for h in (t - 2, t - 1):
                             divide(inverses[h], ev_sums[h])
                     if t == last - LEAD:
-                        for h in (t - 2, t - 1):
-                            take_attention(h)
                         y_rows = first_convolution(ll_tiles[last])
+                        for h in (t - 2, t - 1):
+                            take_attention(h, haar_psum, "haar")
                         max_tiles[t + 1], last_written[t + LEAD] = maximum(z_rows)
                         y_mx[last] = project(last, interleave(nc.vector.tensor_copy, y_rows))
                         last_written[t + LEAD] = y_mx[last][0][:, HALF - 1 : HALF]
+                        q_halves[t + 2] = query(y_mx[t + 2])
                         sum_of_products(t, prods)
                         logarithms(t, e_sum)
                     if t == last - LEAD + 1:
                         for h in (t - 3, t - 2):
                             statistics(h, att[:, h, :])
-                        sum_of_products(t, prods[:1])
                         max_tiles[t + 1], last_written[t + LEAD] = maximum(z_rows)
-                        add_over_window(ev_sums[t], prods[1], 1)
+                        q_halves[t + 2] = query(y_mx[t + 2])
+                        sum_of_products(t, prods)
                         logarithms(t, e_sum)
                     if t == last - LEAD + 2:
                         take_attention(t - 2)
@@ -731,6 +747,7 @@ def tile_merge_pa_t_kernel(
                 rows(3, 1)
                 max_tiles[0], written = maximum(z_rows)
                 y_mx[2] = project(2, y_grouped)
+                q_halves[1] = query(y_mx[1])
 
             head(y_grouped)
             for step in range(LEAD, N_HALVES - 1):

@@ -605,7 +605,7 @@ def tile_merge_pa_t_kernel(
                 if t < 2:
                     weigh_columns(nc.vector, t, z_tiles[t], 1, prods[1], slice(KS - 1, KS))
                 y_grouped = interleave(nc.scalar.copy, first_convolution(ll_tiles[step]))
-                n_tensor = 2
+                n_tensor = 2 if t == 0 else (2 if t % 2 == 0 else 1)
                 open_half(ahead)
                 columns(ahead, 0)
                 part(ahead, 0, ADD)

from contextlib import ExitStack

import concourse.mybir as mybir
from concourse.masks import make_identity

F32 = mybir.dt.float32
BF16 = mybir.dt.bfloat16
U32 = mybir.dt.uint32
U8 = mybir.dt.uint8
FP8X4 = mybir.dt.float8_e4m3fn_x4
ALU = mybir.AluOpType
ACT = mybir.ActivationFunctionType

B, C, M, O, H, W = 4, 1024, 512, 128, 64, 64
H2, W2 = H // 2, W // 2
BN_EPS = 1e-5

P = 128
PACK = 4
PAIRS = PACK // 2
K_PASS = P * PACK
C_PASSES = C // K_PASS
M_TILES = M // P
HALF = 512
HALF_ROWS = HALF // W2
N_HALVES = B * H2 * W2 // HALF
PIECE_ROWS = 8
PIECE = PIECE_ROWS * W2
BLOCKS = HALF // P
KS = 3
SETS = 2
LEAD = 3
RUN = 4
PAD = 4
PITCH = W2 + PAD
TAPS = [(a, c) for a in range(2) for c in range(2)]
HALF_ON_TENSOR = 1
PINNED = (
    mybir.EngineType.DVE, mybir.EngineType.Pool, mybir.EngineType.Activation, mybir.EngineType.PE,
)
ADD, TAKE_OUT, TURN_BACK, PUT = range(4)

FLOPS = 2 * B * H2 * W2 * (M * C + 3 * O * M)


def add_transposed(nc, out, in_, identity, start, stop):
    nc.tensor.matmul(out=out, lhsT=in_, rhs=identity, is_transpose=True, start=start, stop=stop)


def tile_merge_pa_t_kernel(
    tc, x, w_c1, b_c1, w_q, w_k, w_v, bn_gamma, bn_beta, prelu_a, out
):
    nc = tc.nc
    with ExitStack() as whole:
        keep = whole.enter_context(tc.tile_pool(name="keep", bufs=1))

        ident_f32 = keep.tile([P, P], F32)
        make_identity(nc, ident_f32[:])
        ident_bf16 = keep.tile([P, P], BF16)
        make_identity(nc, ident_bf16[:])

        w1_codes = keep.tile([P, C_PASSES, M], U32, align_bytes=64)
        w1_scales = keep.tile([P, C_PASSES, M], U8, align_bytes=64)
        wqkv_codes = keep.tile([P, 3, O], U32, align_bytes=64)
        wqkv_scales = keep.tile([P, 3, O], U8, align_bytes=64)
        bias = keep.tile([P, M_TILES], F32)

        k_moved = keep.tile([P, SETS, KS, H2 + 2, PITCH], F32)
        v_moved = keep.tile([P, SETS, KS, H2 + 2, PITCH], F32)
        for moved in (k_moved, v_moved):
            nc.gpsimd.memset(moved[:, :, :, 0, 0:W2], 0.0)
            nc.gpsimd.memset(moved[:, :, :, H2 + 1, 0:W2], 0.0)
            nc.gpsimd.memset(moved[:, :, 1, :, W2:PITCH], 0.0)

        att = keep.tile([P, N_HALVES, HALF], F32)
        warm = keep.tile([P, 1], F32)
        nc.gpsimd.memset(warm[:], 1.0)
        stats = keep.tile([P, N_HALVES, 6], F32)

        bias_bf16 = keep.tile([P, M_TILES], BF16)
        nc.scalar.dma_start(out=bias_bf16[:], in_=b_c1.rearrange("(n t) -> n t", t=M_TILES))
        gamma_bf16 = keep.tile([P, 1], BF16)
        nc.scalar.dma_start(out=gamma_bf16[:], in_=bn_gamma.rearrange("(o one) -> o one", one=1))
        beta_bf16 = keep.tile([P, 1], BF16)
        nc.scalar.dma_start(out=beta_bf16[:], in_=bn_beta.rearrange("(o one) -> o one", one=1))
        slope_bf16 = keep.tile([P, 1], BF16)
        nc.scalar.dma_start(out=slope_bf16[:], in_=prelu_a.partition_broadcast(P))
        gamma = keep.tile([P, 1], F32)
        beta = keep.tile([P, 1], F32)
        slope = keep.tile([P, 1], F32)
        one_minus_slope = keep.tile([P, 1], F32)
        eps = keep.tile([P, 1], F32)
        minus_gamma = keep.tile([P, 1], F32)
        slope_gamma = keep.tile([P, 1], F32)
        slope_beta = keep.tile([P, 1], F32)

        def widen_constants():
            nc.vector.tensor_copy(out=bias[:], in_=bias_bf16[:])
            nc.vector.tensor_copy(out=gamma[:], in_=gamma_bf16[:])
            nc.vector.tensor_copy(out=beta[:], in_=beta_bf16[:])
            nc.vector.tensor_copy(out=slope[:], in_=slope_bf16[:])
            nc.vector.tensor_scalar(
                out=one_minus_slope[:], in0=slope[:], scalar1=-1.0, scalar2=1.0,
                op0=ALU.mult, op1=ALU.add,
            )
            nc.vector.tensor_scalar(
                out=eps[:], in0=slope[:], scalar1=0.0, scalar2=BN_EPS, op0=ALU.mult, op1=ALU.add
            )
            nc.vector.tensor_scalar(
                out=minus_gamma[:], in0=gamma[:], scalar1=-1.0, scalar2=0.0,
                op0=ALU.mult, op1=ALU.add,
            )
            nc.vector.tensor_mul(out=slope_gamma[:], in0=slope[:], in1=gamma[:])
            nc.vector.tensor_mul(out=slope_beta[:], in0=slope[:], in1=beta[:])

        with ExitStack() as stream:
            stream.enter_context(tc.manual_schedule(engines=set(PINNED)))
            x_pool = stream.enter_context(tc.tile_pool(name="x_pool", bufs=3))
            col_pool = stream.enter_context(tc.tile_pool(name="col_pool", bufs=3))
            work = stream.enter_context(tc.tile_pool(name="work", bufs=2))
            quotient_pool = stream.enter_context(tc.tile_pool(name="quotient_pool", bufs=2))
            single = stream.enter_context(tc.tile_pool(name="single", bufs=1))
            haar_pool = stream.enter_context(tc.tile_pool(name="haar_pool", bufs=2))
            mx_psum = stream.enter_context(tc.psum_pool(name="mx_psum", bufs=2))
            haar_psum = stream.enter_context(tc.psum_pool(name="haar_psum", bufs=2))
            pieces = [(g, s) for g in range(C_PASSES) for s in range(HALF // PIECE)]

            def load_piece(pool, half, g, s, part=0, n_parts=1):
                b, h = divmod(half, 2)
                n_rows = 2 * PIECE_ROWS // n_parts
                row = 2 * (h * HALF_ROWS + s * PIECE_ROWS) + part * n_rows
                x_piece = pool.tile([P, PACK, n_rows * W], BF16)
                nc.sync.dma_start(
                    out=x_piece[:],
                    in_=x[b, g * K_PASS : (g + 1) * K_PASS, row : row + n_rows, :].rearrange(
                        "(p j) r w -> p j (r w)", j=PACK
                    ),
                )
                return x_piece[:].rearrange("p j (r a w c) -> p j r a w c", a=2, w=W2, c=2)

            def add_columns(half, g, s, n_parts=1):
                col_sum = col_pool.tile([P, 2, PACK, PIECE], F32)
                n_rows = PIECE_ROWS // n_parts
                for part in range(n_parts):
                    pixels = load_piece(x_pool, half, g, s, part, n_parts)
                    for a in range(2):
                        nc.vector.tensor_tensor(
                            out=col_sum[:, a].rearrange("p j (r w) -> p j r w", w=W2)[
                                :, :, part * n_rows : (part + 1) * n_rows, :
                            ],
                            in0=pixels[:, :, :, a, :, 0],
                            in1=pixels[:, :, :, a, :, 1],
                            op=ALU.add,
                        )
                return col_sum

            def add_rows_on_vector(ll_grouped, g, s, col_sum):
                planes = col_sum[:].rearrange("p a j (n i) -> p a n j i", i=RUN)
                nc.vector.tensor_tensor(
                    out=ll_grouped[:, g, s * PIECE : (s + 1) * PIECE, :].rearrange(
                        "p (n i) j -> p n j i", i=RUN
                    ),
                    in0=planes[:, 0],
                    in1=planes[:, 1],
                    op=ALU.add,
                )

            def add_rows_on_tensor(ll_grouped, g, s, col_sum):
                turned, rounded = [], []

                def add():
                    for blk in range(PIECE // P):
                        total = haar_psum.tile([P, PACK, P], F32, tag="haar")
                        for a in range(2):
                            for j in range(PACK):
                                add_transposed(
                                    nc, total[:, j, :], col_sum[:, a, j, blk * P : (blk + 1) * P],
                                    ident_f32[:], a == 0 and j == 0, a == 1 and j == PACK - 1,
                                )
                        turned.append(total)

                def take_out():
                    for blk in range(PIECE // P):
                        pairs = haar_pool.tile([P, PAIRS, P, 2], BF16, tag="pairs")
                        nc.scalar.copy(
                            out=pairs[:],
                            in_=turned[blk][:].rearrange("x (u e) p -> x u p e", e=2),
                        )
                        rounded.append(pairs)

                def turn_back():
                    words = haar_psum.tile([P, PIECE // P, PAIRS, P], F32, tag="haar")
                    for blk in range(PIECE // P):
                        row_words = rounded[blk][:].rearrange("x u p e -> x (u p e)").bitcast(F32)
                        for u in range(PAIRS):
                            nc.tensor.transpose(
                                words[:, blk, u, :], row_words[:, u * P : (u + 1) * P], ident_f32[:]
                            )
                    turned.append(words)

                def put():
                    first = (g * HALF + s * PIECE) * PAIRS
                    nc.scalar.copy(
                        out=ll_grouped[:].rearrange("p g x j -> p (g x j)").bitcast(F32)[
                            :, first : first + PIECE * PAIRS
                        ].rearrange("p (b x u) -> p b x u", x=P, u=PAIRS),
                        in_=turned[-1][:].rearrange("p b u x -> p b x u"),
                    )

                return add, take_out, turn_back, put

            ll_tiles, col_sums, on_tensor = {}, {}, {}

            def open_half(half):
                ll_grouped = work.tile([P, C_PASSES, HALF, PACK], BF16, align_bytes=64)
                ll_tiles[half] = ll_grouped

            def columns(half, i, n_parts=1):
                g, s = pieces[i]
                col_sums[half, i] = add_columns(half, g, s, n_parts)
                on_tensor[half, i] = add_rows_on_tensor(ll_tiles[half], g, s, col_sums[half, i])

            def rows(half, i):
                g, s = pieces[i]
                add_rows_on_vector(ll_tiles[half], g, s, col_sums[half, i])

            def part(half, i, which):
                on_tensor[half, i][which]()

            def haar_by_matmul(ll_grouped, half, some_pieces, early):
                for g, s in some_pieces:
                    pixels = load_piece(early, half, g, s)
                    some_rows = PIECE_ROWS // 2
                    for top in range(0, PIECE_ROWS, some_rows):
                        total = mx_psum.tile([P, PACK, some_rows, W2], F32, tag="mx")
                        for tap, (a, c) in enumerate(TAPS):
                            nc.tensor.matmul(
                                out=total[:],
                                lhsT=ident_bf16[:],
                                rhs=pixels[:, :, top : top + some_rows, a, :, c],
                                start=(tap == 0),
                                stop=(tap == len(TAPS) - 1),
                            )
                        first = s * PIECE + top * W2
                        nc.scalar.copy(
                            out=ll_grouped[:, g, first : first + some_rows * W2, :],
                            in_=total[:].rearrange("p j r w -> p (r w) j"),
                        )

            def first_convolution(ll_grouped):
                ll_codes = single.tile([P, C_PASSES, HALF], U32, align_bytes=64)
                ll_scales = single.tile([P, C_PASSES, HALF], U8, align_bytes=64)
                nc.vector.quantize_mx(
                    out=ll_codes[:].rearrange("p g x -> p (g x)").bitcast(FP8X4),
                    scales=ll_scales[:].rearrange("p g x -> p (g x)"),
                    in_=ll_grouped[:].rearrange("p g x j -> p (g x j)"),
                )
                y_rows = single.tile([P, M_TILES, HALF], BF16)
                for t in range(M_TILES):
                    cols = slice(t * P, (t + 1) * P)
                    y_acc = mx_psum.tile([P, HALF], F32, tag="mx")
                    for g in range(C_PASSES):
                        nc.tensor.matmul_mx(
                            out=y_acc[:],
                            lhsT=w1_codes[:, g, cols].bitcast(FP8X4),
                            lhsT_scale=w1_scales[:, g, cols],
                            rhs=ll_codes[:, g, :].bitcast(FP8X4),
                            rhs_scale=ll_scales[:, g, :],
                            start=(g == 0),
                            stop=(g == C_PASSES - 1),
                        )
                    nc.scalar.activation(
                        out=y_rows[:, t, :], in_=y_acc[:], func=ACT.Identity,
                        bias=bias[:, t : t + 1], scale=0.5,
                    )
                return y_rows

            def interleave(copy, y_rows):
                y_grouped = single.tile([P, HALF, PACK], BF16, align_bytes=64)
                copy(out=y_grouped[:], in_=y_rows[:].rearrange("p t x -> p x t"))
                return y_grouped

            def projection(s, y_quantised):
                proj = mx_psum.tile([P, HALF_ROWS, W2], F32, tag="mx")
                nc.tensor.matmul_mx(
                    out=proj[:].rearrange("p r w -> p (r w)"),
                    lhsT=wqkv_codes[:, s, :].bitcast(FP8X4),
                    lhsT_scale=wqkv_scales[:, s, :],
                    rhs=y_quantised[0][:].bitcast(FP8X4),
                    rhs_scale=y_quantised[1][:],
                    start=True,
                    stop=True,
                )
                return proj

            def project(half, y_grouped):
                b, h = divmod(half, 2)
                rows = slice(1 + h * HALF_ROWS, 1 + (h + 1) * HALF_ROWS)
                y_codes = work.tile([P, HALF], U32, align_bytes=64)
                y_scales = work.tile([P, HALF], U8, align_bytes=64)
                nc.vector.quantize_mx(
                    out=y_codes[:].bitcast(FP8X4),
                    scales=y_scales[:],
                    in_=y_grouped[:].rearrange("p x t -> p (x t)"),
                )
                for s in (1, 2):
                    proj = projection(s, (y_codes, y_scales))
                    planes = (k_moved if s == 1 else v_moved)[:, b % SETS]
                    nc.scalar.copy(out=planes[:, 1, rows, 0:W2], in_=proj[:])
                    flat = planes.rearrange("p c r w -> p c (r w)")
                    first, end = rows.start * PITCH, rows.stop * PITCH - PAD
                    for plane, step in ((0, -1), (2, 1)):
                        nc.sync.dma_start(
                            out=flat[:, plane, first:end], in_=flat[:, 1, first + step : end + step]
                        )
                return y_codes, y_scales

            def turn_words(dst, dst_first, words, firsts):
                turned = mx_psum.tile([P, len(firsts), PAIRS, P], F32, tag="mx")
                for i, first in enumerate(firsts):
                    for u in range(PAIRS):
                        nc.tensor.transpose(
                            turned[:, i, u, :],
                            words[:, first + u : first + PAIRS * P : PAIRS],
                            ident_f32[:],
                        )
                n_words = len(firsts) * PAIRS * P
                nc.scalar.copy(
                    out=dst[:, dst_first : dst_first + n_words].rearrange(
                        "p (i n u) -> p i n u", n=P, u=PAIRS
                    ),
                    in_=turned[:].rearrange("p i u n -> p i n u"),
                )

            with tc.tile_pool(name="stage", bufs=1) as stage, tc.tile_pool(
                name="early", bufs=3
            ) as early:
                w1_rows = stage.tile([P, M_TILES, C], BF16)
                wqkv_rows = stage.tile([P, 3, M], BF16)
                for s, w_s in enumerate((w_q, w_k, w_v)):
                    nc.scalar.dma_start(out=wqkv_rows[:, s, :], in_=w_s)
                w1_grouped = stage.tile([P, C_PASSES, M_TILES, P, PACK], BF16, align_bytes=64)
                wqkv_grouped = stage.tile([P, 3, O, PACK], BF16, align_bytes=64)
                def turn_weights():
                    nc.sync.dma_start(
                        out=w1_rows[:], in_=w_c1.rearrange("(n t) c -> n t c", t=M_TILES)
                    )
                    w1_words = w1_rows[:].rearrange("n t c -> n (t c)").bitcast(F32)
                    w1_words_out = w1_grouped[:].rearrange("p g t n j -> p (g t n j)").bitcast(F32)
                    for t in range(0, M_TILES, 2):
                        for g in range(C_PASSES):
                            turn_words(
                                w1_words_out, (g * M_TILES + t) * PAIRS * P,
                                w1_words, [(t + i) * C // 2 + g * PAIRS * P for i in range(2)],
                            )
                    wqkv_words = wqkv_rows[:].rearrange("o s m -> o (s m)").bitcast(F32)
                    wqkv_words_out = wqkv_grouped[:].rearrange("p s o j -> p (s o j)").bitcast(F32)
                    for group in ((0, 1), (2,)):
                        turn_words(
                            wqkv_words_out, group[0] * PAIRS * O,
                            wqkv_words, [s * PAIRS * P for s in group],
                        )

                open_half(0)
                open_half(HALF_ON_TENSOR)
                columns(0, 0, n_parts=2)
                rows(0, 0)
                widen_constants()
                columns(0, 1)
                rows(0, 1)
                columns(0, 2)
                turn_weights()
                rows(0, 2)
                columns(0, 3)
                haar_by_matmul(ll_tiles[HALF_ON_TENSOR], HALF_ON_TENSOR, pieces[:2], early)
                rows(0, 3)
                for g in range(C_PASSES):
                    nc.vector.quantize_mx(
                        out=w1_codes[:, g, :].bitcast(FP8X4),
                        scales=w1_scales[:, g, :],
                        in_=w1_grouped[:, g].rearrange("p t n j -> p (t n j)"),
                    )
                y_grouped = interleave(nc.scalar.copy, first_convolution(ll_tiles[0]))
                columns(HALF_ON_TENSOR, 3)
                haar_by_matmul(ll_tiles[HALF_ON_TENSOR], HALF_ON_TENSOR, pieces[2:-1], early)
                rows(HALF_ON_TENSOR, 3)
                for s in range(3):
                    nc.vector.quantize_mx(
                        out=wqkv_codes[:, s, :].bitcast(FP8X4),
                        scales=wqkv_scales[:, s, :],
                        in_=wqkv_grouped[:, s].rearrange("p o j -> p (o j)"),
                    )

            z_pool = stream.enter_context(tc.tile_pool(name="z_pool", bufs=2, reuse_waits="tile"))
            prod_pool = stream.enter_context(
                tc.tile_pool(name="prod_pool", bufs=3, reuse_waits="tile")
            )
            sum_psum = stream.enter_context(tc.psum_pool(name="sum_psum", bufs=1))
            ev_psum = stream.enter_context(tc.psum_pool(name="ev_psum", bufs=2))
            max_psum = stream.enter_context(tc.psum_pool(name="max_psum", bufs=1))
            sides = (slice(0, HALF // 2), slice(HALF // 2, HALF))

            def add_over_window(total, terms, di):
                for dj in range(KS):
                    for blk in range(BLOCKS):
                        cols = slice(blk * P, (blk + 1) * P)
                        add_transposed(
                            nc, total[:, cols], terms[:, dj, cols], ident_f32[:],
                            di == 0 and dj == 0 and blk == 0,
                            di == KS - 1 and dj == KS - 1 and blk == BLOCKS - 1,
                        )

            def window_row(moved, half, di):
                b, h = divmod(half, 2)
                top = h * HALF_ROWS + di
                return moved[:, b % SETS, :, top : top + HALF_ROWS, 0:W2]

            def by_rows(t):
                return t.rearrange("p c (r w) -> p c r w", w=W2)

            def query(y_quantised):
                return projection(0, y_quantised)

            def scores(half, q_half):
                z = z_pool.tile([P, KS, KS, HALF], F32)
                for di in range(KS):
                    nc.vector.tensor_tensor(
                        out=by_rows(z[:, di]),
                        in0=q_half[:].unsqueeze(1).to_broadcast([P, KS, HALF_ROWS, W2]),
                        in1=window_row(k_moved, half, di),
                        op=ALU.mult,
                    )
                return z

            def round_scores(z, n_rows):
                z_rough = single.tile([P, KS, KS, HALF], BF16)
                for di in range(n_rows):
                    nc.scalar.copy(out=z_rough[:, di], in_=z[:, di])
                return [(z_rough if di < n_rows else z)[:, di] for di in range(KS)]

            def maximum(z_rows):
                tree = single.tile([P, KS, HALF], BF16)
                for side in sides:
                    nc.vector.tensor_tensor(
                        out=tree[:, :, side], in0=z_rows[0][:, :, side],
                        in1=z_rows[1][:, :, side], op=ALU.max,
                    )
                for side in sides:
                    nc.vector.tensor_tensor(
                        out=tree[:, :, side], in0=tree[:, :, side], in1=z_rows[2][:, :, side],
                        op=ALU.max,
                    )
                for dj in range(1, KS):
                    for side in sides:
                        nc.vector.tensor_tensor(
                            out=tree[:, 0, side], in0=tree[:, 0, side], in1=tree[:, dj, side],
                            op=ALU.max,
                        )
                z_max = max_psum.tile([P, HALF], F32)
                nc.tensor.matmul(
                    out=z_max[:], lhsT=ident_bf16[:], rhs=tree[:, 0, :], start=True, stop=True
                )
                return z_max, tree[:, 0, HALF - 1 : HALF]

            def subtract(z, z_max, di):
                nc.vector.tensor_tensor(
                    out=z[:, di],
                    in0=z[:, di],
                    in1=z_max[:].unsqueeze(1).to_broadcast([P, KS, HALF]),
                    op=ALU.subtract,
                )

            def exponential(z, e_sum, di):
                nc.scalar.activation(out=z[:, di], in_=z[:, di], func=ACT.Exp)
                add_over_window(e_sum, z[:, di], di)

            def weigh_columns(engine, half, e, di, prod, djs):
                engine.tensor_tensor(
                    out=by_rows(prod)[:, djs], in0=by_rows(e[:, di])[:, djs],
                    in1=window_row(v_moved, half, di)[:, djs], op=ALU.mult,
                )

            def weigh(engine, half, e, di, in_place=False, n=KS):
                if in_place:
                    prod = e[:, di]
                else:
                    prod_tile = prod_pool.tile([P, KS, HALF], F32)
                    prod = prod_tile[:]
                weigh_columns(engine, half, e, di, prod, slice(0, n))
                return prod

            def logarithm(e_sum):
                quotient = quotient_pool.tile([P, HALF], F32)
                nc.scalar.activation(out=quotient[:], in_=e_sum[:], func=ACT.Ln)
                return quotient

            def invert(quotient):
                nc.scalar.activation(out=quotient[:], in_=quotient[:], func=ACT.Exp, scale=-1.0)

            def divide(quotient, ev_sum):
                nc.vector.tensor_tensor(
                    out=quotient[:], in0=ev_sum[:], in1=quotient[:], op=ALU.mult
                )

            def attention(quotient, pool=mx_psum, tag="mx"):
                att_back = pool.tile([P, HALF], F32, tag=tag)
                for blk in range(BLOCKS):
                    cols = slice(blk * P, (blk + 1) * P)
                    nc.tensor.transpose(att_back[:, cols], quotient[:, cols], ident_f32[:])
                return att_back

            halves = range(N_HALVES)
            last = N_HALVES - 1
            y_mx, z_tiles, max_tiles, ev_sums, inverses = {}, {}, {}, {}, {}

            def after_vector(written):
                if written.dtype == BF16:
                    fence = single.tile([P, 1], BF16, name="fence_bf16")
                else:
                    fence = single.tile([P, 1], U32, name="fence_u32")
                nc.gpsimd.tensor_copy(out=fence[:], in_=written)

            last_written = {}

            def statistics(half, att_half):
                nc.vector.bn_stats(out=stats[:, half, :], in_=att_half)

            def weights(t, between):
                e_sum = sum_psum.tile([P, HALF], F32)
                for di in range(KS):
                    subtract(z_tiles[t], max_tiles[t], di)
                    exponential(z_tiles[t], e_sum, di)
                    if di in between:
                        between[di]()
                return e_sum

            def take_attention(h, pool=mx_psum, tag="mx"):
                att_back = attention(inverses[h], pool, tag)
                nc.scalar.copy(out=att[:, h, :], in_=att_back[:])

            def put_late_row(t):
                after_vector(last_written[t + LEAD])
                late_prod = weigh(nc.gpsimd, t, z_tiles[t], KS - 1)
                return lambda: add_over_window(ev_sums[t], late_prod, KS - 1)

            kept, q_halves = {}, {}

            def logarithms(t, e_sum):
                if t % 2 == 0 and t < last - 1:
                    waiting = single.tile([P, HALF], F32)
                    nc.scalar.copy(out=waiting[:], in_=e_sum[:])
                    kept[t] = waiting
                else:
                    if t - 1 in kept:
                        inverses[t - 1] = logarithm(kept[t - 1])
                    inverses[t] = logarithm(e_sum)

            def inversions(t):
                if t % 2 == 1 or t >= last - 1:
                    if t - 1 in kept:
                        invert(inverses[t - 1])
                    invert(inverses[t])

            def sum_of_products(t, prods):
                ev_sum = ev_psum.tile([P, HALF], F32)
                ev_sums[t] = ev_sum
                for di in range(len(prods)):
                    add_over_window(ev_sum, prods[di], di)

            pending = []

            def late_and_pending(t):
                late = put_late_row(t - 1) if t >= 1 else None

                def both():
                    if late:
                        late()
                    while_pending = list(pending)
                    pending.clear()
                    for one in while_pending:
                        one()
                return both

            def haar_step(step):
                t = step - LEAD
                ahead = step + 1
                q_half = q_halves[t + 1]
                e_sum = weights(t, {0: late_and_pending(t)})
                if t >= 2 and t % 2 == 0:
                    inversions(t - 1)
                prods = [
                    weigh(nc.gpsimd, t, z_tiles[t], di, n=KS - 1 if t < 2 and di == 1 else KS)
                    for di in range(KS - 1)
                ]
                z_tiles[t + 1] = scores(t + 1, q_half)
                z_rows = round_scores(z_tiles[t + 1], KS)
                if t >= 2 and t % 2 == 0:
                    for h in (t - 2, t - 1):
                        divide(inverses[h], ev_sums[h])
                    for h in (t - 2, t - 1):
                        take_attention(h)
                if t >= 3 and t % 2 == 1:
                    for h in (t - 3, t - 2):
                        statistics(h, att[:, h, :])
                if t < 2:
                    weigh_columns(nc.vector, t, z_tiles[t], 1, prods[1], slice(KS - 1, KS))
                y_grouped = interleave(nc.scalar.copy, first_convolution(ll_tiles[step]))
                n_tensor = 2 if t == 0 else (2 if t % 2 == 0 else 1)
                open_half(ahead)
                columns(ahead, 0)
                part(ahead, 0, ADD)
                if t % 2 == 1:
                    logarithms(t, e_sum)
                max_tiles[t + 1], last_written[step] = maximum(z_rows)
                part(ahead, 0, TAKE_OUT)
                columns(ahead, 1)
                if t % 2 == 0:
                    logarithms(t, e_sum)
                if n_tensor == 1:
                    sum_of_products(t, prods)
                if t % 2 == 0 and t > 0:
                    columns(ahead, 2)
                y_mx[step] = project(step, y_grouped)
                part(ahead, 0, TURN_BACK)
                part(ahead, 0, PUT)
                if n_tensor >= 2:
                    part(ahead, 1, ADD)
                    part(ahead, 1, TAKE_OUT)
                if t % 2 == 1 or t == 0:
                    columns(ahead, 2)
                if n_tensor >= 2:
                    part(ahead, 1, TURN_BACK)
                    pending.append(lambda: part(ahead, 1, PUT))
                if n_tensor >= 3:
                    part(ahead, 2, ADD)
                    part(ahead, 2, TAKE_OUT)
                    part(ahead, 2, TURN_BACK)
                    part(ahead, 2, PUT)
                q_halves[t + 2] = query(y_mx[t + 2])
                if n_tensor > 1:
                    sum_of_products(t, prods)
                if n_tensor < 2:
                    rows(ahead, 1)
                columns(ahead, 3)
                if n_tensor < 3:
                    rows(ahead, 2)
                rows(ahead, 3)
                last_written[step] = ll_tiles[ahead][:, C_PASSES - 1, HALF - 1, PACK - 1 : PACK]

            def last_fronts():
                for t in range(last - LEAD, last):
                    q_half = q_halves[t + 1]
                    e_sum = weights(t, {0: late_and_pending(t)})
                    if t % 2 == 0:
                        inversions(t - 1)
                    prods = [weigh(nc.gpsimd, t, z_tiles[t], di) for di in range(KS - 1)]
                    z_tiles[t + 1] = scores(t + 1, q_half)
                    z_rows = round_scores(z_tiles[t + 1], KS if t == last - LEAD + 1 else KS - 1)
                    if t % 2 == 0:
                        for h in (t - 2, t - 1):
                            divide(inverses[h], ev_sums[h])
                    if t == last - LEAD:
                        y_rows = first_convolution(ll_tiles[last])
                        for h in (t - 2, t - 1):
                            take_attention(h, haar_psum, "haar")
                        max_tiles[t + 1], last_written[t + LEAD] = maximum(z_rows)
                        y_mx[last] = project(last, interleave(nc.vector.tensor_copy, y_rows))
                        last_written[t + LEAD] = y_mx[last][0][:, HALF - 1 : HALF]
                        q_halves[t + 2] = query(y_mx[t + 2])
                        sum_of_products(t, prods)
                        logarithms(t, e_sum)
                    if t == last - LEAD + 1:
                        for h in (t - 3, t - 2):
                            statistics(h, att[:, h, :])
                        max_tiles[t + 1], last_written[t + LEAD] = maximum(z_rows)
                        q_halves[t + 2] = query(y_mx[t + 2])
                        sum_of_products(t, prods)
                        logarithms(t, e_sum)
                    if t == last - LEAD + 2:
                        take_attention(t - 2)
                        sum_of_products(t, prods)
                        max_tiles[t + 1], last_written[t + LEAD] = maximum(z_rows)
                        logarithms(t, e_sum)
                        inversions(t)
                        take_attention(t - 1)
                        row = weigh(nc.vector, t, z_tiles[t], KS - 1)
                        add_over_window(ev_sums[t], row, KS - 1)

            def last_step():
                e_sum = weights(last, {})
                e = z_tiles[last]
                divide(inverses[last - 1], ev_sums[last - 1])
                logarithms(last, e_sum)
                inversions(last)
                first_rows = [weigh(nc.vector, last, e, di) for di in range(2)]
                nc.vector.tensor_tensor(
                    out=first_rows[0], in0=first_rows[0], in1=first_rows[1], op=ALU.add
                )
                ev_sum = ev_psum.tile([P, HALF], F32)
                add_over_window(ev_sum, first_rows[0], 0)
                take_attention(last - 1)
                last_row = weigh(nc.vector, last, e, KS - 1, in_place=True)
                add_over_window(ev_sum, last_row, KS - 1)
                for h in (last - 3, last - 2):
                    statistics(h, att[:, h, :])
                nc.scalar.activation(out=warm[:], in_=warm[:], func=ACT.Abs_reciprocal_sqrt)
                divide(inverses[last], ev_sum)
                statistics(last - 1, att[:, last - 1, :])
                att_back = attention(inverses[last])
                statistics(last, att_back[:])
                nc.scalar.copy(out=att[:, last, :], in_=att_back[:])

            def head(y_grouped):
                open_half(2)
                columns(2, 0)
                part(2, 0, ADD)
                part(2, 0, TAKE_OUT)
                y_mx[0] = project(0, y_grouped)
                y_grouped = interleave(nc.scalar.copy, first_convolution(ll_tiles[1]))
                columns(2, 1)
                part(2, 0, TURN_BACK)
                part(2, 0, PUT)
                part(2, 1, ADD)
                columns(2, 2)
                rows(2, 2)
                columns(2, 3)
                part(2, 1, TAKE_OUT)
                y_mx[1] = project(1, y_grouped)
                q_half = query(y_mx[0])
                part(2, 1, TURN_BACK)
                part(2, 1, PUT)
                part(2, 3, ADD)
                open_half(3)
                columns(3, 2)
                rows(3, 2)
                part(2, 3, TAKE_OUT)
                part(2, 3, TURN_BACK)
                part(2, 3, PUT)
                columns(3, 3)
                rows(3, 3)
                z_tiles[0] = scores(0, q_half)
                z_rows = round_scores(z_tiles[0], KS)
                y_grouped = interleave(nc.scalar.copy, first_convolution(ll_tiles[2]))
                columns(3, 0)
                rows(3, 0)
                columns(3, 1)
                rows(3, 1)
                max_tiles[0], written = maximum(z_rows)
                y_mx[2] = project(2, y_grouped)
                q_halves[1] = query(y_mx[1])

            head(y_grouped)
            for step in range(LEAD, N_HALVES - 1):
                haar_step(step)
            last_fronts()
            last_step()

        final_pool = whole.enter_context(tc.tile_pool(name="final_pool", bufs=5, reuse_waits="tile"))
        mean_var = final_pool.tile([P, 2], F32)
        nc.vector.bn_aggr(out=mean_var[:], in_=stats[:].rearrange("p t s -> p (t s)"))
        inv_std = final_pool.tile([P, 1], F32)
        nc.scalar.activation(
            out=inv_std[:], in_=mean_var[:, 1:2], func=ACT.Abs_reciprocal_sqrt, bias=eps[:]
        )
        mean_gamma = final_pool.tile([P, 1], F32)
        nc.vector.tensor_mul(out=mean_gamma[:], in0=mean_var[:, 0:1], in1=minus_gamma[:])
        slope_mean_gamma = final_pool.tile([P, 1], F32)
        nc.vector.tensor_mul(out=slope_mean_gamma[:], in0=slope[:], in1=mean_gamma[:])
        shift = final_pool.tile([P, 1], F32)
        slope_shift = final_pool.tile([P, 1], F32)
        gain = final_pool.tile([P, 1], F32)
        slope_gain = final_pool.tile([P, 1], F32)
        nc.vector.tensor_mul(out=gain[:], in0=gamma[:], in1=inv_std[:])
        nc.vector.tensor_scalar(
            out=shift[:], in0=mean_gamma[:], scalar1=inv_std[:], scalar2=beta[:],
            op0=ALU.mult, op1=ALU.add,
        )
        nc.vector.tensor_mul(out=slope_gain[:], in0=slope_gamma[:], in1=inv_std[:])
        nc.vector.tensor_scalar(
            out=slope_shift[:], in0=slope_mean_gamma[:], scalar1=inv_std[:], scalar2=slope_beta[:],
            op0=ALU.mult, op1=ALU.add,
        )

        flat = att[:].rearrange("p t x -> p (t x)")
        rows_of_out = out.rearrange("b o i j -> o b (i j)")
        parts = [(b, 0, H2 * W2) for b in range(B - 1)] + [(B - 1, k * HALF, HALF) for k in range(2)]
        positives, finals = [], []

        def sides_of_slope(b, first, n):
            att_part = flat[:, b * H2 * W2 + first : b * H2 * W2 + first + n]
            positive = final_pool.tile([P, H2 * W2], F32)
            nc.scalar.activation(
                out=positive[:, :n], in_=att_part, func=ACT.Relu, bias=shift[:], scale=gain[:]
            )
            final = final_pool.tile([P, H2 * W2], F32)
            if b < B - 1:
                nc.vector.tensor_scalar(
                    out=final[:, :n], in0=att_part, scalar1=slope_gain[:], scalar2=slope_shift[:],
                    op0=ALU.mult, op1=ALU.add,
                )
            else:
                nc.scalar.activation(
                    out=final[:, :n], in_=att_part, func=ACT.Identity,
                    bias=slope_shift[:], scale=slope_gain[:],
                )
            positives.append(positive)
            finals.append(final)

        sides_of_slope(parts[0][0], parts[0][1], parts[0][2])
        for i, (b, first, n) in enumerate(parts):
            if i + 1 < len(parts):
                sides_of_slope(parts[i + 1][0], parts[i + 1][1], parts[i + 1][2])
            nc.vector.scalar_tensor_tensor(
                out=finals[i][:, :n], in0=positives[i][:, :n], scalar=one_minus_slope[:],
                in1=finals[i][:, :n], op0=ALU.mult, op1=ALU.add,
            )
            nc.sync.dma_start(
                out=rows_of_out[:, b, first : first + n], in_=finals[i][:, :n]
            )
